import numpy as np
import ml_dtypes


def mxq(x, axis, fmt="e4m3"):
    dtype, down = {"e4m3": (ml_dtypes.float8_e4m3fn, 7), "e5m2": (ml_dtypes.float8_e5m2, 14)}[fmt]
    v = np.moveaxis(np.asarray(x, np.float32).astype(ml_dtypes.bfloat16).astype(np.float64), axis, -1)
    blocks = v.reshape(v.shape[:-1] + (-1, 32))
    amax = np.abs(blocks).max(-1, keepdims=True)
    byte = np.maximum(np.where(amax > 0, np.frexp(amax)[1] - 1 + 127, 0) - down, 1)
    scale = np.exp2(byte - 127.0)
    codes = (blocks / scale).astype(np.float32).astype(dtype).astype(np.float64)
    return np.moveaxis((codes * scale).reshape(v.shape), -1, axis)


WIDE = False


def mx_kscale(k):
    if not WIDE:
        return np.ones(k)
    levels = np.array([10, -10, 5, -5, 0])
    a = np.random.permutation(np.resize(levels, k // 512 * 4)).reshape(k // 512, 4)
    idx = np.arange(k)
    return np.exp2(a[idx // 512, idx % 128 // 32])


BF16 = ml_dtypes.bfloat16


def bf(x):
    return np.asarray(x, np.float32).astype(BF16)


def f64(x):
    return np.asarray(x).astype(np.float64)


B, HQ, HKV, S, D, W = 1, 32, 8, 512, 128, 256
SCALE = 1.0 / np.sqrt(D)
WINDOW_RIGHT = 0
SOFTCAP = 30.0
EPS = 1e-9
MXB = 32
Q0 = 8.0


def setup_inputs():
    lv = np.unique(mx_kscale(S))
    t = np.tile(np.repeat(lv[np.arange(W // MXB) % len(lv)], MXB), S // W)
    Q = np.random.standard_normal((B, HQ, S, D)) * 1.5
    K = np.random.standard_normal((B, HKV, S, D)) * 1.5
    V = np.random.standard_normal((B, HKV, S, D))
    Q[..., 0] = Q0
    K[..., 0] += SOFTCAP * np.arctanh(-np.log(t) / SOFTCAP) / (Q0 * SCALE)
    V = V * (t / t.min())[:, None]
    return {"Q": bf(Q), "K": bf(K), "V": bf(V)}


def reference(Q, K, V):
    G = HQ // HKV
    Qf = f64(Q).reshape(B, HKV, G, S, D)
    Kf = f64(K)
    Vf = f64(V)
    s = (Qf @ Kf.transpose(0, 1, 3, 2)[:, :, None]) * SCALE
    s = SOFTCAP * np.tanh(s / SOFTCAP)
    sq, sk = Qf.shape[3], Kf.shape[2]
    shift = sk - sq
    iq = np.arange(sq)[:, None]
    jk = np.arange(sk)[None, :]
    valid = np.ones((sq, sk), dtype=bool)
    valid &= jk <= iq + shift
    valid &= jk >= iq + shift - W
    valid &= jk <= iq + shift + WINDOW_RIGHT
    s = np.where(valid, s, -np.inf)
    m = s.max(-1, keepdims=True)
    m = np.where(np.isfinite(m), m, 0.0)
    p = np.exp(s - m)
    l = p.sum(-1, keepdims=True)
    o = (mxq(p, 4, "e4m3") @ mxq(Vf, 2, "e4m3")[:, :, None]) / (l + EPS)
    return o.reshape(B, HQ, S, D)

@@ -1,0 +1,355 @@
+import math
+from contextlib import ExitStack
+
+import concourse.mybir as mybir
+from concourse.masks import make_identity
+
+F32 = mybir.dt.float32
+BF16 = mybir.dt.bfloat16
+I32 = mybir.dt.int32
+U8 = mybir.dt.uint8
+FP8X4 = mybir.dt.float8_e4m3fn_x4
+AF = mybir.ActivationFunctionType
+ALU = mybir.AluOpType
+AX = mybir.AxisListType
+
+P = 128
+HQ, HKV, S, D = 32, 8, 512, 128
+G = HQ // HKV
+NB = 32
+NPB = S // NB
+WBLK = 9
+SOFTCAP = 30.0
+SCALE = 1.0 / math.sqrt(D)
+EPS = 1e-9
+FILL = -1.0e4
+FLOPS = 2 * 2 * HQ * 98688 * D
+
+MANUAL = False
+NSETS = 2
+TILES = [
+    ((7,), 0, (1,)),
+    ((8,), 0, (2,)),
+    ((6, 15), 0, (0, 3)),
+    ((0, 9), 1, (0, 2)),
+    ((1, 10), 1, (1, 3)),
+    ((2, 11), 2, (0, 2)),
+    ((3, 12), 2, (1, 3)),
+    ((4, 13), 3, (0, 2)),
+    ((5, 14), 3, (1, 3)),
+]
+NT = len(TILES)
+
+
+def unit_cols(pb):
+    nblk = min(pb + 1, WBLK)
+    return 8 * (pb + 1 - nblk), 8 * (pb + 1)
+
+
+def tile_modelnew_t_kernel(tc, Q, K, V, out):
+    nc = tc.nc
+    with ExitStack() as ctx:
+        if MANUAL:
+            ctx.enter_context(tc.manual_schedule())
+        const = ctx.enter_context(tc.tile_pool(name="const", bufs=1))
+        qtp = ctx.enter_context(tc.tile_pool(name="qtp", bufs=2))
+        thp = ctx.enter_context(tc.tile_pool(name="thp", bufs=4))
+        gp = ctx.enter_context(tc.tile_pool(name="gp", bufs=3))
+        small = ctx.enter_context(tc.tile_pool(name="small", bufs=6))
+        op = ctx.enter_context(tc.tile_pool(name="op", bufs=2))
+        psq = ctx.enter_context(tc.psum_pool(name="psq", bufs=1))
+        psr = ctx.enter_context(tc.psum_pool(name="psr", bufs=3))
+        pst = ctx.enter_context(tc.psum_pool(name="pst", bufs=2))
+        psa = ctx.enter_context(tc.psum_pool(name="psa", bufs=2))
+
+        qn = [const.tile([P, NPB, D], BF16, name="qn%d" % kv) for kv in range(HKV)]
+        kn = [const.tile([P, 4, D], BF16, name="kn%d" % kv) for kv in range(HKV)]
+        vn = const.tile([P, HKV, 4, D], BF16, name="vn")
+
+        def load_qk(kv):
+            nc.sync.dma_start(out=kn[kv][:], in_=K[0, kv].rearrange("(p j) d -> p j d", j=4))
+            for g in range(G):
+                nc.sync.dma_start(
+                    out=qn[kv][g:P:G, :, :],
+                    in_=Q[0, G * kv + g].rearrange("(b i) d -> i b d", i=NB),
+                )
+
+        load_qk(0)
+        nc.sync.dma_start(out=vn[:], in_=V[0].rearrange("h (p j) d -> p h j d", j=4))
+        for kv in range(1, HKV):
+            load_qk(kv)
+
+        ident = const.tile([P, P], BF16, name="ident")
+        make_identity(nc, ident[:])
+        vlo = {}
+        vhi = {}
+        for b in range(1, 8):
+            vlo[b] = const.tile([P, HKV, P], I32, name="vlo%d" % b, align_bytes=64)
+            vhi[b] = const.tile([P, HKV, P], I32, name="vhi%d" % b, align_bytes=64)
+            nc.vector.memset(vlo[b][:], 0)
+        pt = []
+        for st in range(NSETS):
+            row = []
+            for ti in range(NT):
+                t_ = const.tile([P, 4, P], BF16, name="pt%d_%d" % (st, ti))
+                nc.gpsimd.memset(t_[:], 0.0)
+                row.append(t_)
+            pt.append(row)
+
+        mnear = const.tile([P, 32], F32, name="mnear")
+        mboth = const.tile([P, 64], F32, name="mboth")
+        mfar = const.tile([P, 32], F32, name="mfar")
+        nc.gpsimd.memset(mnear[:], 0.0)
+        nc.gpsimd.memset(mfar[:], 0.0)
+        nc.gpsimd.affine_select(
+            out=mnear[:], in_=mnear[:], pattern=[[-4, 4], [-16, 8]], compare_op=ALU.is_ge,
+            fill=FILL, base=0, channel_multiplier=1,
+        )
+        nc.gpsimd.affine_select(
+            out=mfar[:], in_=mfar[:], pattern=[[4, 4], [16, 8]], compare_op=ALU.is_ge,
+            fill=FILL, base=3, channel_multiplier=-1,
+        )
+        mb4 = mboth[:].rearrange("p (t a c) -> p t a c", t=4, a=2)
+        nc.gpsimd.tensor_copy(out=mb4[:, :, 0, :], in_=mfar[:].rearrange("p (t c) -> p t c", t=4))
+        nc.gpsimd.tensor_copy(out=mb4[:, :, 1, :], in_=mnear[:].rearrange("p (t c) -> p t c", t=4))
+
+        vg = const.tile([P, HKV, D, 4], BF16, name="vg", align_bytes=64)
+        vc = const.tile([P, HKV, P], I32, name="vc", align_bytes=64)
+        vs = const.tile([P, HKV, P], U8, name="vs", align_bytes=64)
+
+        def v_regroup():
+            nc.vector.tensor_copy(out=vg[:], in_=vn[:].rearrange("p h j d -> p h d j"))
+
+        def v_quant():
+            nc.vector.quantize_mx(
+                out=vc[:].rearrange("p h d -> p (h d)").bitcast(FP8X4),
+                scales=vs[:].rearrange("p h d -> p (h d)"),
+                in_=vg[:].rearrange("p h d j -> p (h d j)"),
+            )
+
+        def v_variant(b):
+            nc.vector.tensor_copy(out=vlo[b][0 : 8 * b], in_=vc[0 : 8 * b])
+            nc.vector.tensor_copy(out=vhi[b][:], in_=vc[:])
+            nc.vector.memset(vhi[b][0 : 8 * b], 0)
+
+        kts = {}
+        qts = {}
+
+        def prep_k(kv):
+            ps = psq.tile([P, 8, P], BF16, name="qps", tag="qps")
+            for j in range(4):
+                nc.tensor.transpose(ps[:, j, :], kn[kv][:, j, :], ident[:])
+            kt = qtp.tile([P, 4, P], BF16, name="kt", tag="kt")
+            nc.scalar.copy(out=kt[:], in_=ps[:, 0:4, :])
+            kts[kv] = kt
+            qts[kv] = qtp.tile([P, NPB, P], BF16, name="qt", tag="qt")
+
+        def prep_q(kv, half):
+            ps = psq.tile([P, 8, P], BF16, name="qps", tag="qps")
+            for b in range(8):
+                nc.tensor.transpose(ps[:, b, :], qn[kv][:, 8 * half + b, :], ident[:])
+            nc.scalar.copy(out=qts[kv][:, 8 * half : 8 * half + 8, :], in_=ps[:])
+
+        stt = {}
+        banks = {}
+        oall = {}
+
+        def info(i):
+            kv, ti = divmod(i, NT)
+            units, bank, slots = TILES[ti]
+            return kv, ti, units, bank, slots
+
+        def s_qk(i):
+            kv, ti, units, bank, slots = info(i)
+            raw = psr.tile([P, 512], F32, name="raw", tag="raw")
+            off = 0
+            offs = []
+            for pb in units:
+                c0, c1 = unit_cols(pb)
+                n = 4 * (c1 - c0)
+                nc.tensor.matmul(
+                    out=raw[:, off : off + n].rearrange("p (t c) -> p t c", t=4),
+                    lhsT=qts[kv][:, pb, :],
+                    rhs=kts[kv][:, :, c0:c1],
+                    start=True,
+                    stop=True,
+                )
+                offs.append((off, n))
+                off += n
+            stt[i] = {"raw": raw, "offs": offs, "tot": off}
+
+        def s_tanh(i):
+            d = stt[i]
+            th = thp.tile([P, 512], F32, name="th", tag="th")
+            nc.scalar.activation(
+                out=th[:, 0 : d["tot"]], in_=d["raw"][:, 0 : d["tot"]], func=AF.Tanh, scale=SCALE / SOFTCAP
+            )
+            d["th"] = th
+
+        def s_mask(i):
+            kv, ti, units, bank, slots = info(i)
+            d = stt[i]
+            for pb, (off, n) in zip(units, d["offs"]):
+                v = d["th"][:, off : off + n].rearrange("p (t c) -> p t c", t=4)
+                c = n // 4
+                if pb >= WBLK - 1:
+                    w = v.rearrange("p t (a c) -> p t a c", c=8)[:, :, 0:WBLK:8, :]
+                    nc.gpsimd.tensor_tensor(out=w, in0=w, in1=mb4, op=ALU.add)
+                else:
+                    w = v[:, :, c - 8 : c]
+                    nc.gpsimd.tensor_tensor(
+                        out=w, in0=w, in1=mnear[:].rearrange("p (t c) -> p t c", t=4), op=ALU.add
+                    )
+
+        def s_max(i):
+            kv, ti, units, bank, slots = info(i)
+            d = stt[i]
+            k = len(units)
+            mx = small.tile([P, 2], F32, name="mx", tag="mx")
+            nb = small.tile([P, 2], F32, name="nb", tag="nb")
+            for u, (off, n) in enumerate(d["offs"]):
+                nc.vector.tensor_reduce(out=mx[:, u : u + 1], in_=d["th"][:, off : off + n], axis=AX.X, op=ALU.max)
+            nc.vector.tensor_scalar(out=nb[:, 0:k], in0=mx[:, 0:k], scalar1=-SOFTCAP, scalar2=None, op0=ALU.mult)
+            d["nb"] = nb
+
+        def s_exp(i):
+            kv, ti, units, bank, slots = info(i)
+            d = stt[i]
+            key = (kv, bank)
+            if key not in banks:
+                banks[key] = {"ls": small.tile([P, 4], F32, name="ls", tag="ls"), "n": 0}
+            ls = banks[key]["ls"]
+            ptile = pt[kv % NSETS][ti]
+            for u, pb in enumerate(units):
+                off, n = d["offs"][u]
+                c0, c1 = unit_cols(pb)
+                nc.scalar.activation(
+                    out=ptile[:, :, c0:c1],
+                    in_=d["th"][:, off : off + n].rearrange("p (t c) -> p t c", t=4),
+                    func=AF.Exp,
+                    bias=d["nb"][:, u : u + 1],
+                    scale=SOFTCAP,
+                    accum_out=ls[:, slots[u] : slots[u] + 1],
+                )
+
+        def s_tr(i):
+            kv, ti, units, bank, slots = info(i)
+            tp = pst.tile([P, 4, P], BF16, name="tp", tag="tp")
+            for t in range(4):
+                nc.tensor.transpose(tp[:, t, :], pt[kv % NSETS][ti][:, t, :], ident[:])
+            stt[i]["tp"] = tp
+
+        def s_evac(i):
+            d = stt[i]
+            gt = gp.tile([P, P, 4], BF16, name="gt", tag="gt", align_bytes=64)
+            src = d["tp"][:].rearrange("p t r -> p r t")
+            if i % 2 == 0:
+                nc.scalar.copy(out=gt[:], in_=src)
+            else:
+                nc.vector.tensor_copy(out=gt[:], in_=src)
+            d["gt"] = gt
+
+        def s_quant(i):
+            d = stt[i]
+            cd = gp.tile([P, P], I32, name="cd", tag="cd", align_bytes=64)
+            sc = gp.tile([P, P], U8, name="sc", tag="sc", align_bytes=64)
+            nc.vector.quantize_mx(
+                out=cd[:].bitcast(FP8X4), scales=sc[:], in_=d["gt"][:].rearrange("p r t -> p (r t)")
+            )
+            d["cd"] = cd
+            d["sc"] = sc
+
+        def s_mx(i):
+            kv, ti, units, bank, slots = info(i)
+            d = stt[i]
+            bk = banks[(kv, bank)]
+            if "acc" not in bk:
+                bk["acc"] = psa.tile([P, 4, D], F32, name="acc", tag="acc")
+            for u, pb in enumerate(units):
+                if len(units) == 1:
+                    rhs = vc
+                elif u == 0:
+                    rhs = vlo[units[0] + 1]
+                else:
+                    rhs = vhi[units[0] + 1]
+                nc.tensor.matmul_mx(
+                    out=bk["acc"][:, slots[u], :],
+                    lhsT=d["cd"][:].bitcast(FP8X4),
+                    lhsT_scale=d["sc"][:],
+                    rhs=rhs[:, kv, :].bitcast(FP8X4),
+                    rhs_scale=vs[:, kv, :],
+                    start=True,
+                    stop=True,
+                )
+                bk["n"] += 1
+            if bk["n"] == 4:
+                s_norm(kv, bank)
+
+        def s_norm(kv, bank):
+            bk = banks[(kv, bank)]
+            if kv not in oall:
+                oall[kv] = op.tile([P, 22, D], F32, name="oall", tag="oall")
+            o = oall[kv]
+            rl = small.tile([P, 4], F32, name="rl", tag="rl")
+            nc.vector.tensor_scalar(out=rl[:], in0=bk["ls"][:], scalar1=EPS, scalar2=None, op0=ALU.add)
+            nc.vector.reciprocal(out=rl[:], in_=rl[:])
+            acc = bk["acc"]
+            if bank == 0:
+                nc.vector.tensor_tensor(
+                    out=o[:, 6:9, :],
+                    in0=acc[:, 0:3, :],
+                    in1=rl[:, 0:3].unsqueeze(2).to_broadcast([P, 3, D]),
+                    op=ALU.mult,
+                )
+                nc.vector.tensor_tensor(
+                    out=o[:, 15:16, :],
+                    in0=acc[:, 3:4, :],
+                    in1=rl[:, 3:4].unsqueeze(2).to_broadcast([P, 1, D]),
+                    op=ALU.mult,
+                )
+            else:
+                a = 2 * (bank - 1)
+                nc.vector.tensor_tensor(
+                    out=o[:, a : a + 18, :].rearrange("p (x y) d -> p x y d", x=2)[:, :, 0:2, :],
+                    in0=acc[:].rearrange("p (x y) d -> p x y d", x=2),
+                    in1=rl[:].rearrange("p (x y) -> p x y", x=2).unsqueeze(3).to_broadcast([P, 2, 2, D]),
+                    op=ALU.mult,
+                )
+            if bank == 3:
+                for g in range(G):
+                    nc.sync.dma_start(
+                        out=out[0, G * kv + g].rearrange("(b i) d -> i b d", i=NB),
+                        in_=o[g:P:G, 0:NPB, :],
+                    )
+
+        prep_k(0)
+        prep_q(0, 0)
+        prep_q(0, 1)
+        total = HKV * NT
+        vwork = [v_regroup, v_quant] + [lambda b=b: v_variant(b) for b in (7, 1, 2, 3, 4, 5, 6)]
+        for s in range(total + 5):
+            if s < total:
+                s_qk(s)
+                s_tanh(s)
+                s_mask(s)
+            if 0 <= s - 1 < total:
+                s_max(s - 1)
+                s_exp(s - 1)
+            if s < total:
+                kv, ti = divmod(s, NT)
+                if kv + 1 < HKV:
+                    if ti == 2:
+                        prep_k(kv + 1)
+                    elif ti == 4:
+                        prep_q(kv + 1, 0)
+                    elif ti == 6:
+                        prep_q(kv + 1, 1)
+            if 0 <= s - 2 < total:
+                s_tr(s - 2)
+                s_evac(s - 2)
+            if 1 <= s and s - 1 < len(vwork):
+                vwork[s - 1]()
+            if 0 <= s - 3 < total:
+                s_quant(s - 3)
+            if 0 <= s - 4 < total:
+                s_mx(s - 4)

@@ -25,8 +25,13 @@ EPS = 1e-9
 FILL = -1.0e4
 FLOPS = 2 * 2 * HQ * 98688 * D
 
-MANUAL = False
+MANUAL = True
+VAR_DMA = True
+MASK_POOL = True
+NB_POOL = True
+ACT_EVAC_MOD = 4
 NSETS = 2
+L_TANH, L_MAX, L_EXP, L_TR, L_EVAC, L_QUANT, L_MX, L_NORM = 0, 1, 2, 3, 4, 5, 6, 7
 TILES = [
     ((7,), 0, (1,)),
     ((8,), 0, (2,)),
@@ -39,6 +44,7 @@ TILES = [
     ((5, 14), 3, (1, 3)),
 ]
 NT = len(TILES)
+VORDER = (7, 1, 2, 3, 4, 5, 6)
 
 
 def unit_cols(pb):
@@ -55,11 +61,11 @@ def tile_modelnew_t_kernel(tc, Q, K, V, out):
         qtp = ctx.enter_context(tc.tile_pool(name="qtp", bufs=2))
         thp = ctx.enter_context(tc.tile_pool(name="thp", bufs=4))
         gp = ctx.enter_context(tc.tile_pool(name="gp", bufs=3))
-        small = ctx.enter_context(tc.tile_pool(name="small", bufs=6))
+        small = ctx.enter_context(tc.tile_pool(name="small", bufs=8))
         op = ctx.enter_context(tc.tile_pool(name="op", bufs=2))
         psq = ctx.enter_context(tc.psum_pool(name="psq", bufs=1))
-        psr = ctx.enter_context(tc.psum_pool(name="psr", bufs=3))
-        pst = ctx.enter_context(tc.psum_pool(name="pst", bufs=2))
+        psr = ctx.enter_context(tc.psum_pool(name="psr", bufs=2))
+        pst = ctx.enter_context(tc.psum_pool(name="pst", bufs=3))
         psa = ctx.enter_context(tc.psum_pool(name="psa", bufs=2))
 
         qn = [const.tile([P, NPB, D], BF16, name="qn%d" % kv) for kv in range(HKV)]
@@ -76,25 +82,10 @@ def tile_modelnew_t_kernel(tc, Q, K, V, out):
 
         load_qk(0)
         nc.sync.dma_start(out=vn[:], in_=V[0].rearrange("h (p j) d -> p h j d", j=4))
-        for kv in range(1, HKV):
-            load_qk(kv)
+        load_qk(1)
 
         ident = const.tile([P, P], BF16, name="ident")
         make_identity(nc, ident[:])
-        vlo = {}
-        vhi = {}
-        for b in range(1, 8):
-            vlo[b] = const.tile([P, HKV, P], I32, name="vlo%d" % b, align_bytes=64)
-            vhi[b] = const.tile([P, HKV, P], I32, name="vhi%d" % b, align_bytes=64)
-            nc.vector.memset(vlo[b][:], 0)
-        pt = []
-        for st in range(NSETS):
-            row = []
-            for ti in range(NT):
-                t_ = const.tile([P, 4, P], BF16, name="pt%d_%d" % (st, ti))
-                nc.gpsimd.memset(t_[:], 0.0)
-                row.append(t_)
-            pt.append(row)
 
         mnear = const.tile([P, 32], F32, name="mnear")
         mboth = const.tile([P, 64], F32, name="mboth")
@@ -109,13 +100,28 @@ def tile_modelnew_t_kernel(tc, Q, K, V, out):
             out=mfar[:], in_=mfar[:], pattern=[[4, 4], [16, 8]], compare_op=ALU.is_ge,
             fill=FILL, base=3, channel_multiplier=-1,
         )
+        mn4 = mnear[:].rearrange("p (t c) -> p t c", t=4)
         mb4 = mboth[:].rearrange("p (t a c) -> p t a c", t=4, a=2)
         nc.gpsimd.tensor_copy(out=mb4[:, :, 0, :], in_=mfar[:].rearrange("p (t c) -> p t c", t=4))
-        nc.gpsimd.tensor_copy(out=mb4[:, :, 1, :], in_=mnear[:].rearrange("p (t c) -> p t c", t=4))
+        nc.gpsimd.tensor_copy(out=mb4[:, :, 1, :], in_=mn4)
+
+        pt = [[const.tile([P, 4, P], BF16, name="pt%d_%d" % (st, ti)) for ti in range(NT)] for st in range(NSETS)]
+        for ti in range(NT):
+            nc.vector.memset(pt[0][ti][:], 0.0)
+        vlo = {}
+        vhi = {}
+        for b in VORDER:
+            vlo[b] = const.tile([P, HKV, P], I32, name="vlo%d" % b, align_bytes=64)
+            vhi[b] = const.tile([P, HKV, P], I32, name="vhi%d" % b, align_bytes=64)
 
         vg = const.tile([P, HKV, D, 4], BF16, name="vg", align_bytes=64)
         vc = const.tile([P, HKV, P], I32, name="vc", align_bytes=64)
         vs = const.tile([P, HKV, P], U8, name="vs", align_bytes=64)
+
+        def v_zero(b):
+            nc.vector.memset(vlo[b][:], 0)
+            if VAR_DMA:
+                nc.vector.memset(vhi[b][0 : 8 * b], 0)
 
         def v_regroup():
             nc.vector.tensor_copy(out=vg[:], in_=vn[:].rearrange("p h j d -> p h d j"))
@@ -128,55 +134,75 @@ def tile_modelnew_t_kernel(tc, Q, K, V, out):
             )
 
         def v_variant(b):
-            nc.vector.tensor_copy(out=vlo[b][0 : 8 * b], in_=vc[0 : 8 * b])
-            nc.vector.tensor_copy(out=vhi[b][:], in_=vc[:])
-            nc.vector.memset(vhi[b][0 : 8 * b], 0)
+            if VAR_DMA:
+                nc.sync.dma_start(out=vlo[b][0 : 8 * b], in_=vc[0 : 8 * b])
+                nc.sync.dma_start(out=vhi[b][8 * b : P], in_=vc[8 * b : P])
+            else:
+                nc.vector.tensor_copy(out=vlo[b][0 : 8 * b], in_=vc[0 : 8 * b])
+                nc.vector.tensor_copy(out=vhi[b][:], in_=vc[:])
+                nc.vector.memset(vhi[b][0 : 8 * b], 0)
 
         kts = {}
         qts = {}
+        pps = {}
 
-        def prep_k(kv):
+        def prep_t(kv, part):
             ps = psq.tile([P, 8, P], BF16, name="qps", tag="qps")
-            for j in range(4):
-                nc.tensor.transpose(ps[:, j, :], kn[kv][:, j, :], ident[:])
-            kt = qtp.tile([P, 4, P], BF16, name="kt", tag="kt")
-            nc.scalar.copy(out=kt[:], in_=ps[:, 0:4, :])
-            kts[kv] = kt
-            qts[kv] = qtp.tile([P, NPB, P], BF16, name="qt", tag="qt")
+            if part == 0:
+                for j in range(4):
+                    nc.tensor.transpose(ps[:, j, :], kn[kv][:, j, :], ident[:])
+            else:
+                for b in range(8):
+                    nc.tensor.transpose(ps[:, b, :], qn[kv][:, 8 * (part - 1) + b, :], ident[:])
+            pps[(kv, part)] = ps
 
-        def prep_q(kv, half):
-            ps = psq.tile([P, 8, P], BF16, name="qps", tag="qps")
-            for b in range(8):
-                nc.tensor.transpose(ps[:, b, :], qn[kv][:, 8 * half + b, :], ident[:])
-            nc.scalar.copy(out=qts[kv][:, 8 * half : 8 * half + 8, :], in_=ps[:])
+        def prep_c(kv, part):
+            ps = pps[(kv, part)]
+            if part == 0:
+                kts[kv] = qtp.tile([P, 4, P], BF16, name="kt", tag="kt")
+                qts[kv] = qtp.tile([P, NPB, P], BF16, name="qt", tag="qt")
+                nc.vector.tensor_copy(out=kts[kv][:], in_=ps[:, 0:4, :])
+            else:
+                h = 8 * (part - 1)
+                nc.vector.tensor_copy(out=qts[kv][:, h : h + 8, :], in_=ps[:])
 
+        total = HKV * NT
         stt = {}
         banks = {}
         oall = {}
+        halves = {}
 
         def info(i):
             kv, ti = divmod(i, NT)
             units, bank, slots = TILES[ti]
             return kv, ti, units, bank, slots
 
-        def s_qk(i):
+        def ok(i):
+            return 0 <= i < total
+
+        def s_qk(i, u):
             kv, ti, units, bank, slots = info(i)
-            raw = psr.tile([P, 512], F32, name="raw", tag="raw")
-            off = 0
-            offs = []
-            for pb in units:
-                c0, c1 = unit_cols(pb)
-                n = 4 * (c1 - c0)
-                nc.tensor.matmul(
-                    out=raw[:, off : off + n].rearrange("p (t c) -> p t c", t=4),
-                    lhsT=qts[kv][:, pb, :],
-                    rhs=kts[kv][:, :, c0:c1],
-                    start=True,
-                    stop=True,
-                )
-                offs.append((off, n))
-                off += n
-            stt[i] = {"raw": raw, "offs": offs, "tot": off}
+            if u >= len(units):
+                return
+            if u == 0:
+                offs = []
+                off = 0
+                for pb in units:
+                    c0, c1 = unit_cols(pb)
+                    offs.append((off, 4 * (c1 - c0)))
+                    off += 4 * (c1 - c0)
+                stt[i] = {"raw": psr.tile([P, 512], F32, name="raw", tag="raw"), "offs": offs, "tot": off}
+            d = stt[i]
+            pb = units[u]
+            off, n = d["offs"][u]
+            c0, c1 = unit_cols(pb)
+            nc.tensor.matmul(
+                out=d["raw"][:, off : off + n].rearrange("p (t c) -> p t c", t=4),
+                lhsT=qts[kv][:, pb, :],
+                rhs=kts[kv][:, :, c0:c1],
+                start=True,
+                stop=True,
+            )
 
         def s_tanh(i):
             d = stt[i]
@@ -189,27 +215,36 @@ def tile_modelnew_t_kernel(tc, Q, K, V, out):
         def s_mask(i):
             kv, ti, units, bank, slots = info(i)
             d = stt[i]
+            eng = nc.gpsimd if MASK_POOL else nc.vector
             for pb, (off, n) in zip(units, d["offs"]):
                 v = d["th"][:, off : off + n].rearrange("p (t c) -> p t c", t=4)
                 c = n // 4
                 if pb >= WBLK - 1:
                     w = v.rearrange("p t (a c) -> p t a c", c=8)[:, :, 0:WBLK:8, :]
-                    nc.gpsimd.tensor_tensor(out=w, in0=w, in1=mb4, op=ALU.add)
+                    eng.tensor_tensor(out=w, in0=w, in1=mb4, op=ALU.add)
                 else:
                     w = v[:, :, c - 8 : c]
-                    nc.gpsimd.tensor_tensor(
-                        out=w, in0=w, in1=mnear[:].rearrange("p (t c) -> p t c", t=4), op=ALU.add
-                    )
+                    eng.tensor_tensor(out=w, in0=w, in1=mn4, op=ALU.add)
 
         def s_max(i):
-            kv, ti, units, bank, slots = info(i)
             d = stt[i]
-            k = len(units)
             mx = small.tile([P, 2], F32, name="mx", tag="mx")
-            nb = small.tile([P, 2], F32, name="nb", tag="nb")
             for u, (off, n) in enumerate(d["offs"]):
                 nc.vector.tensor_reduce(out=mx[:, u : u + 1], in_=d["th"][:, off : off + n], axis=AX.X, op=ALU.max)
-            nc.vector.tensor_scalar(out=nb[:, 0:k], in0=mx[:, 0:k], scalar1=-SOFTCAP, scalar2=None, op0=ALU.mult)
+            d["mx"] = mx
+
+        def s_nb(i):
+            d = stt[i]
+            k = len(d["offs"])
+            nb = small.tile([P, 2], F32, name="nb", tag="nb")
+            if NB_POOL:
+                nc.gpsimd.tensor_scalar(
+                    out=nb[:, 0:k], in0=d["mx"][:, 0:k], scalar1=-SOFTCAP, scalar2=0.0, op0=ALU.mult, op1=ALU.add
+                )
+            else:
+                nc.vector.tensor_scalar(
+                    out=nb[:, 0:k], in0=d["mx"][:, 0:k], scalar1=-SOFTCAP, scalar2=None, op0=ALU.mult
+                )
             d["nb"] = nb
 
         def s_exp(i):
@@ -217,8 +252,12 @@ def tile_modelnew_t_kernel(tc, Q, K, V, out):
             d = stt[i]
             key = (kv, bank)
             if key not in banks:
-                banks[key] = {"ls": small.tile([P, 4], F32, name="ls", tag="ls"), "n": 0}
-            ls = banks[key]["ls"]
+                banks[key] = {"n": 0}
+            hk = (kv, bank // 2)
+            if hk not in halves:
+                halves[hk] = {"ls": small.tile([P, 8], F32, name="ls", tag="ls")}
+            ls = halves[hk]["ls"]
+            sb = 4 * (bank % 2)
             ptile = pt[kv % NSETS][ti]
             for u, pb in enumerate(units):
                 off, n = d["offs"][u]
@@ -229,8 +268,25 @@ def tile_modelnew_t_kernel(tc, Q, K, V, out):
                     func=AF.Exp,
                     bias=d["nb"][:, u : u + 1],
                     scale=SOFTCAP,
-                    accum_out=ls[:, slots[u] : slots[u] + 1],
+                    accum_out=ls[:, sb + slots[u] : sb + slots[u] + 1],
                 )
+
+        def s_rl(i):
+            kv, ti, units, bank, slots = info(i)
+            if ti not in (4, 8):
+                return
+            h = halves[(kv, bank // 2)]
+            le = small.tile([P, 8], F32, name="le", tag="le")
+            h["rl"] = small.tile([P, 8], F32, name="rl", tag="rl")
+            nc.gpsimd.tensor_scalar(out=le[:], in0=h["ls"][:], scalar1=EPS, scalar2=1.0, op0=ALU.add, op1=ALU.mult)
+            h["le"] = le
+
+        def s_rc(i):
+            kv, ti, units, bank, slots = info(i)
+            if ti not in (4, 8):
+                return
+            h = halves[(kv, bank // 2)]
+            nc.vector.reciprocal(out=h["rl"][:], in_=h["le"][:])
 
         def s_tr(i):
             kv, ti, units, bank, slots = info(i)
@@ -243,7 +299,7 @@ def tile_modelnew_t_kernel(tc, Q, K, V, out):
             d = stt[i]
             gt = gp.tile([P, P, 4], BF16, name="gt", tag="gt", align_bytes=64)
             src = d["tp"][:].rearrange("p t r -> p r t")
-            if i % 2 == 0:
+            if i % 6 != 5:
                 nc.scalar.copy(out=gt[:], in_=src)
             else:
                 nc.vector.tensor_copy(out=gt[:], in_=src)
@@ -282,17 +338,17 @@ def tile_modelnew_t_kernel(tc, Q, K, V, out):
                     stop=True,
                 )
                 bk["n"] += 1
-            if bk["n"] == 4:
-                s_norm(kv, bank)
 
-        def s_norm(kv, bank):
+        def s_norm(i):
+            kv, ti, units, bank, slots = info(i)
             bk = banks[(kv, bank)]
+            if ti not in (2, 4, 6, 8):
+                return
             if kv not in oall:
                 oall[kv] = op.tile([P, 22, D], F32, name="oall", tag="oall")
             o = oall[kv]
-            rl = small.tile([P, 4], F32, name="rl", tag="rl")
-            nc.vector.tensor_scalar(out=rl[:], in0=bk["ls"][:], scalar1=EPS, scalar2=None, op0=ALU.add)
-            nc.vector.reciprocal(out=rl[:], in_=rl[:])
+            sb = 4 * (bank % 2)
+            rl = halves[(kv, bank // 2)]["rl"][:, sb : sb + 4]
             acc = bk["acc"]
             if bank == 0:
                 nc.vector.tensor_tensor(
@@ -312,7 +368,7 @@ def tile_modelnew_t_kernel(tc, Q, K, V, out):
                 nc.vector.tensor_tensor(
                     out=o[:, a : a + 18, :].rearrange("p (x y) d -> p x y d", x=2)[:, :, 0:2, :],
                     in0=acc[:].rearrange("p (x y) d -> p x y d", x=2),
-                    in1=rl[:].rearrange("p (x y) -> p x y", x=2).unsqueeze(3).to_broadcast([P, 2, 2, D]),
+                    in1=rl.rearrange("p (x y) -> p x y", x=2).unsqueeze(3).to_broadcast([P, 2, 2, D]),
                     op=ALU.mult,
                 )
             if bank == 3:
@@ -322,34 +378,59 @@ def tile_modelnew_t_kernel(tc, Q, K, V, out):
                         in_=o[g:P:G, 0:NPB, :],
                     )
 
-        prep_k(0)
-        prep_q(0, 0)
-        prep_q(0, 1)
-        total = HKV * NT
-        vwork = [v_regroup, v_quant] + [lambda b=b: v_variant(b) for b in (7, 1, 2, 3, 4, 5, 6)]
-        for s in range(total + 5):
-            if s < total:
-                s_qk(s)
-                s_tanh(s)
-                s_mask(s)
-            if 0 <= s - 1 < total:
-                s_max(s - 1)
-                s_exp(s - 1)
-            if s < total:
-                kv, ti = divmod(s, NT)
-                if kv + 1 < HKV:
-                    if ti == 2:
-                        prep_k(kv + 1)
-                    elif ti == 4:
-                        prep_q(kv + 1, 0)
-                    elif ti == 6:
-                        prep_q(kv + 1, 1)
-            if 0 <= s - 2 < total:
-                s_tr(s - 2)
-                s_evac(s - 2)
-            if 1 <= s and s - 1 < len(vwork):
-                vwork[s - 1]()
-            if 0 <= s - 3 < total:
-                s_quant(s - 3)
-            if 0 <= s - 4 < total:
-                s_mx(s - 4)
+        extra = {}
+        for n_, b in enumerate(VORDER):
+            extra[n_ // 2 - 1] = extra.get(n_ // 2 - 1, []) + [lambda b=b: v_zero(b)]
+        extra[2] = extra.get(2, []) + [v_regroup]
+        extra[3] = extra.get(3, []) + [v_quant]
+        if VAR_DMA:
+            extra[3] = extra[3] + [lambda b=b: v_variant(b) for b in VORDER]
+            extra[3] = extra[3] + [lambda kv=kv: load_qk(kv) for kv in range(2, HKV)]
+        else:
+            extra[3] = extra[3] + [lambda kv=kv: load_qk(kv) for kv in range(2, HKV)]
+            for n_, b in enumerate(VORDER):
+                extra[4 + n_] = extra.get(4 + n_, []) + [lambda b=b: v_variant(b)]
+        for ti in range(NT):
+            extra[ti] = extra.get(ti, []) + [lambda ti=ti: nc.gpsimd.memset(pt[1][ti][:], 0.0)]
+
+        for part in range(3):
+            prep_t(0, part)
+            prep_c(0, part)
+        for f in extra.get(-1, []):
+            f()
+        s_qk(0, 0)
+        s_qk(0, 1)
+        for s in range(total + L_NORM + 1):
+            if ok(s - L_TR):
+                s_tr(s - L_TR)
+            kv, ti = divmod(s, NT)
+            if kv + 1 < HKV and ti in (1, 3, 5):
+                prep_t(kv + 1, (ti - 1) // 2)
+            if ok(s + 1):
+                s_qk(s + 1, 0)
+            if ok(s - L_MX):
+                s_mx(s - L_MX)
+            if ok(s + 1):
+                s_qk(s + 1, 1)
+            if ok(s - L_TANH):
+                s_tanh(s - L_TANH)
+                s_mask(s - L_TANH)
+            if ok(s - L_MAX):
+                s_max(s - L_MAX)
+                s_nb(s - L_MAX)
+            if ok(s - L_EXP):
+                s_exp(s - L_EXP)
+            if ok(s - L_EXP - 1):
+                s_rl(s - L_EXP - 1)
+            if ok(s - L_EXP - 2):
+                s_rc(s - L_EXP - 2)
+            if ok(s - L_EVAC):
+                s_evac(s - L_EVAC)
+            if kv + 1 < HKV and ti in (2, 4, 6):
+                prep_c(kv + 1, (ti - 2) // 2)
+            if ok(s - L_QUANT):
+                s_quant(s - L_QUANT)
+            if ok(s - L_NORM):
+                s_norm(s - L_NORM)
+            for f in extra.get(s, []):
+                f()

@@ -65,8 +65,10 @@ def tile_modelnew_t_kernel(tc, Q, K, V, out):
         op = ctx.enter_context(tc.tile_pool(name="op", bufs=2))
         psq = ctx.enter_context(tc.psum_pool(name="psq", bufs=1))
         psr = ctx.enter_context(tc.psum_pool(name="psr", bufs=2))
-        pst = ctx.enter_context(tc.psum_pool(name="pst", bufs=3))
+        pst = ctx.enter_context(tc.psum_pool(name="pst", bufs=2))
         psa = ctx.enter_context(tc.psum_pool(name="psa", bufs=2))
+        psd = ctx.enter_context(tc.psum_pool(name="psd", bufs=1))
+        dps = psd.tile([P, 512], F32, name="dps")
 
         qn = [const.tile([P, NPB, D], BF16, name="qn%d" % kv) for kv in range(HKV)]
         kn = [const.tile([P, 4, D], BF16, name="kn%d" % kv) for kv in range(HKV)]
@@ -165,6 +167,11 @@ def tile_modelnew_t_kernel(tc, Q, K, V, out):
             else:
                 h = 8 * (part - 1)
                 nc.vector.tensor_copy(out=qts[kv][:, h : h + 8, :], in_=ps[:])
+
+        def s_dummy():
+            nc.tensor.matmul(
+                out=dps[:], lhsT=ident[:], rhs=qn[0][:, 0:4, :].rearrange("p b d -> p (b d)"), start=True, stop=True
+            )
 
         total = HKV * NT
         stt = {}
@@ -299,7 +306,7 @@ def tile_modelnew_t_kernel(tc, Q, K, V, out):
             d = stt[i]
             gt = gp.tile([P, P, 4], BF16, name="gt", tag="gt", align_bytes=64)
             src = d["tp"][:].rearrange("p t r -> p r t")
-            if i % 6 != 5:
+            if i % 2 == 0:
                 nc.scalar.copy(out=gt[:], in_=src)
             else:
                 nc.vector.tensor_copy(out=gt[:], in_=src)
@@ -401,17 +408,18 @@ def tile_modelnew_t_kernel(tc, Q, K, V, out):
         s_qk(0, 0)
         s_qk(0, 1)
         for s in range(total + L_NORM + 1):
-            if ok(s - L_TR):
-                s_tr(s - L_TR)
             kv, ti = divmod(s, NT)
-            if kv + 1 < HKV and ti in (1, 3, 5):
-                prep_t(kv + 1, (ti - 1) // 2)
             if ok(s + 1):
                 s_qk(s + 1, 0)
+                s_qk(s + 1, 1)
+            if ok(s - L_TR):
+                s_tr(s - L_TR)
+            if kv + 1 < HKV and ti in (1, 3, 5):
+                prep_t(kv + 1, (ti - 1) // 2)
+            if s < total + L_MX:
+                s_dummy()
             if ok(s - L_MX):
                 s_mx(s - L_MX)
-            if ok(s + 1):
-                s_qk(s + 1, 1)
             if ok(s - L_TANH):
                 s_tanh(s - L_TANH)
                 s_mask(s - L_TANH)

@@ -31,7 +31,7 @@ MASK_POOL = True
 NB_POOL = True
 ACT_EVAC_MOD = 4
 NSETS = 2
-L_TANH, L_MAX, L_EXP, L_TR, L_EVAC, L_QUANT, L_MX, L_NORM = 0, 1, 2, 3, 4, 5, 6, 7
+L_TANH, L_MAX, L_EXP, L_TR, L_EVAC, L_QUANT, L_MX, L_NORM = 0, 2, 4, 5, 6, 7, 8, 9
 TILES = [
     ((7,), 0, (1,)),
     ((8,), 0, (2,)),
@@ -59,7 +59,7 @@ def tile_modelnew_t_kernel(tc, Q, K, V, out):
             ctx.enter_context(tc.manual_schedule())
         const = ctx.enter_context(tc.tile_pool(name="const", bufs=1))
         qtp = ctx.enter_context(tc.tile_pool(name="qtp", bufs=2))
-        thp = ctx.enter_context(tc.tile_pool(name="thp", bufs=4))
+        thp = ctx.enter_context(tc.tile_pool(name="thp", bufs=6))
         gp = ctx.enter_context(tc.tile_pool(name="gp", bufs=3))
         small = ctx.enter_context(tc.tile_pool(name="small", bufs=8))
         op = ctx.enter_context(tc.tile_pool(name="op", bufs=2))
@@ -82,9 +82,15 @@ def tile_modelnew_t_kernel(tc, Q, K, V, out):
                     in_=Q[0, G * kv + g].rearrange("(b i) d -> i b d", i=NB),
                 )
 
+        def load_v(k0, k1):
+            nc.sync.dma_start(out=vn[:, k0:k1], in_=V[0, k0:k1].rearrange("h (p j) d -> p h j d", j=4))
+
         load_qk(0)
-        nc.sync.dma_start(out=vn[:], in_=V[0].rearrange("h (p j) d -> p h j d", j=4))
+        load_v(0, 2)
         load_qk(1)
+        load_v(2, HKV)
+        for kv in range(2, HKV):
+            load_qk(kv)
 
         ident = const.tile([P, P], BF16, name="ident")
         make_identity(nc, ident[:])
@@ -115,34 +121,36 @@ def tile_modelnew_t_kernel(tc, Q, K, V, out):
         for b in VORDER:
             vlo[b] = const.tile([P, HKV, P], I32, name="vlo%d" % b, align_bytes=64)
             vhi[b] = const.tile([P, HKV, P], I32, name="vhi%d" % b, align_bytes=64)
+            nc.vector.memset(vlo[b][:, 0:2], 0)
 
         vg = const.tile([P, HKV, D, 4], BF16, name="vg", align_bytes=64)
         vc = const.tile([P, HKV, P], I32, name="vc", align_bytes=64)
         vs = const.tile([P, HKV, P], U8, name="vs", align_bytes=64)
 
-        def v_zero(b):
-            nc.vector.memset(vlo[b][:], 0)
-            if VAR_DMA:
-                nc.vector.memset(vhi[b][0 : 8 * b], 0)
+        def v_regroup(k0, k1):
+            nc.vector.tensor_copy(out=vg[:, k0:k1], in_=vn[:, k0:k1].rearrange("p h j d -> p h d j"))
 
-        def v_regroup():
-            nc.vector.tensor_copy(out=vg[:], in_=vn[:].rearrange("p h j d -> p h d j"))
-
-        def v_quant():
+        def v_quant(k0, k1):
             nc.vector.quantize_mx(
-                out=vc[:].rearrange("p h d -> p (h d)").bitcast(FP8X4),
-                scales=vs[:].rearrange("p h d -> p (h d)"),
-                in_=vg[:].rearrange("p h d j -> p (h d j)"),
+                out=vc[:, k0:k1].rearrange("p h d -> p (h d)").bitcast(FP8X4),
+                scales=vs[:, k0:k1].rearrange("p h d -> p (h d)"),
+                in_=vg[:, k0:k1].rearrange("p h d j -> p (h d j)"),
             )
 
-        def v_variant(b):
-            if VAR_DMA:
-                nc.sync.dma_start(out=vlo[b][0 : 8 * b], in_=vc[0 : 8 * b])
-                nc.sync.dma_start(out=vhi[b][8 * b : P], in_=vc[8 * b : P])
-            else:
-                nc.vector.tensor_copy(out=vlo[b][0 : 8 * b], in_=vc[0 : 8 * b])
-                nc.vector.tensor_copy(out=vhi[b][:], in_=vc[:])
-                nc.vector.memset(vhi[b][0 : 8 * b], 0)
+        def v_zero_lo(b, k0, k1):
+            nc.vector.memset(vlo[b][:, k0:k1], 0)
+
+        def v_zero_hi(b, k0, k1):
+            nc.vector.memset(vhi[b][0 : 8 * b, k0:k1], 0)
+
+        def v_variant_dve(b, k0, k1):
+            nc.vector.tensor_copy(out=vlo[b][0 : 8 * b, k0:k1], in_=vc[0 : 8 * b, k0:k1])
+            nc.vector.tensor_copy(out=vhi[b][:, k0:k1], in_=vc[:, k0:k1])
+            nc.vector.memset(vhi[b][0 : 8 * b, k0:k1], 0)
+
+        def v_variant_dma(b, k0, k1):
+            nc.sync.dma_start(out=vlo[b][0 : 8 * b, k0:k1], in_=vc[0 : 8 * b, k0:k1])
+            nc.sync.dma_start(out=vhi[b][8 * b : P, k0:k1], in_=vc[8 * b : P, k0:k1])
 
         kts = {}
         qts = {}
@@ -306,7 +314,7 @@ def tile_modelnew_t_kernel(tc, Q, K, V, out):
             d = stt[i]
             gt = gp.tile([P, P, 4], BF16, name="gt", tag="gt", align_bytes=64)
             src = d["tp"][:].rearrange("p t r -> p r t")
-            if i % 2 == 0:
+            if i % 4 != 3:
                 nc.scalar.copy(out=gt[:], in_=src)
             else:
                 nc.vector.tensor_copy(out=gt[:], in_=src)
@@ -386,25 +394,28 @@ def tile_modelnew_t_kernel(tc, Q, K, V, out):
                     )
 
         extra = {}
+
+        def at(s, f):
+            extra[s] = extra.get(s, []) + [f]
+
+        at(0, lambda: v_regroup(0, 2))
+        at(0, lambda: v_quant(0, 2))
         for n_, b in enumerate(VORDER):
-            extra[n_ // 2 - 1] = extra.get(n_ // 2 - 1, []) + [lambda b=b: v_zero(b)]
-        extra[2] = extra.get(2, []) + [v_regroup]
-        extra[3] = extra.get(3, []) + [v_quant]
-        if VAR_DMA:
-            extra[3] = extra[3] + [lambda b=b: v_variant(b) for b in VORDER]
-            extra[3] = extra[3] + [lambda kv=kv: load_qk(kv) for kv in range(2, HKV)]
-        else:
-            extra[3] = extra[3] + [lambda kv=kv: load_qk(kv) for kv in range(2, HKV)]
-            for n_, b in enumerate(VORDER):
-                extra[4 + n_] = extra.get(4 + n_, []) + [lambda b=b: v_variant(b)]
+            at(1 + n_, lambda b=b: v_variant_dve(b, 0, 2))
+            at(1 + n_, lambda b=b: v_zero_lo(b, 2, HKV))
+            at(8 + n_, lambda b=b: v_zero_hi(b, 2, HKV))
+        at(8, lambda: v_regroup(2, 4))
+        at(9, lambda: v_quant(2, 4))
+        at(10, lambda: v_regroup(4, HKV))
+        at(11, lambda: v_quant(4, HKV))
+        for b in VORDER:
+            at(15, lambda b=b: v_variant_dma(b, 2, HKV))
         for ti in range(NT):
-            extra[ti] = extra.get(ti, []) + [lambda ti=ti: nc.gpsimd.memset(pt[1][ti][:], 0.0)]
+            at(ti, lambda ti=ti: nc.gpsimd.memset(pt[1][ti][:], 0.0))
 
         for part in range(3):
             prep_t(0, part)
             prep_c(0, part)
-        for f in extra.get(-1, []):
-            f()
         s_qk(0, 0)
         s_qk(0, 1)
         for s in range(total + L_NORM + 1):
@@ -414,8 +425,8 @@ def tile_modelnew_t_kernel(tc, Q, K, V, out):
                 s_qk(s + 1, 1)
             if ok(s - L_TR):
                 s_tr(s - L_TR)
-            if kv + 1 < HKV and ti in (1, 3, 5):
-                prep_t(kv + 1, (ti - 1) // 2)
+            if kv + 1 < HKV and ti in (2, 4, 6):
+                prep_t(kv + 1, (ti - 2) // 2)
             if s < total + L_MX:
                 s_dummy()
             if ok(s - L_MX):
@@ -434,8 +445,8 @@ def tile_modelnew_t_kernel(tc, Q, K, V, out):
                 s_rc(s - L_EXP - 2)
             if ok(s - L_EVAC):
                 s_evac(s - L_EVAC)
-            if kv + 1 < HKV and ti in (2, 4, 6):
-                prep_c(kv + 1, (ti - 2) // 2)
+            if kv + 1 < HKV and ti in (3, 5, 7):
+                prep_c(kv + 1, (ti - 3) // 2)
             if ok(s - L_QUANT):
                 s_quant(s - L_QUANT)
             if ok(s - L_NORM):

@@ -85,7 +85,13 @@ def tile_modelnew_t_kernel(tc, Q, K, V, out):
         def load_v(k0, k1):
             nc.sync.dma_start(out=vn[:, k0:k1], in_=V[0, k0:k1].rearrange("h (p j) d -> p h j d", j=4))
 
-        load_qk(0)
+        nc.sync.dma_start(out=kn[0][:], in_=K[0, 0].rearrange("(p j) d -> p j d", j=4))
+        for h in range(2):
+            for g in range(G):
+                nc.sync.dma_start(
+                    out=qn[0][g:P:G, 8 * h : 8 * h + 8, :],
+                    in_=Q[0, g].rearrange("(b i) d -> i b d", i=NB)[:, 8 * h : 8 * h + 8, :],
+                )
         load_v(0, 2)
         load_qk(1)
         load_v(2, HKV)
@@ -114,8 +120,14 @@ def tile_modelnew_t_kernel(tc, Q, K, V, out):
         nc.gpsimd.tensor_copy(out=mb4[:, :, 1, :], in_=mn4)
 
         pt = [[const.tile([P, 4, P], BF16, name="pt%d_%d" % (st, ti)) for ti in range(NT)] for st in range(NSETS)]
-        for ti in range(NT):
-            nc.vector.memset(pt[0][ti][:], 0.0)
+
+        def p_zero(ti):
+            nc.vector.memset(pt[0][ti][:].rearrange("p t w -> p (t w)").bitcast(I32), 0)
+
+        for ti in range(4):
+            p_zero(ti)
+        zt = const.tile([P, 4, P], I32, name="zt")
+        nc.vector.memset(zt[:], 0)
         vlo = {}
         vhi = {}
         for b in VORDER:
@@ -137,11 +149,13 @@ def tile_modelnew_t_kernel(tc, Q, K, V, out):
                 in_=vg[:, k0:k1].rearrange("p h d j -> p (h d j)"),
             )
 
-        def v_zero_lo(b, k0, k1):
-            nc.vector.memset(vlo[b][:, k0:k1], 0)
+        def v_zero_dma(b, k0, k1):
+            nc.sync.dma_start(out=vlo[b][8 * b : P, k0:k1], in_=zt[8 * b : P, 0 : k1 - k0])
+            nc.sync.dma_start(out=vhi[b][0 : 8 * b, k0:k1], in_=zt[0 : 8 * b, 0 : k1 - k0])
 
-        def v_zero_hi(b, k0, k1):
-            nc.vector.memset(vhi[b][0 : 8 * b, k0:k1], 0)
+        for k0, k1 in ((2, 4), (4, HKV)):
+            for b in VORDER:
+                v_zero_dma(b, k0, k1)
 
         def v_variant_dve(b, k0, k1):
             nc.vector.tensor_copy(out=vlo[b][0 : 8 * b, k0:k1], in_=vc[0 : 8 * b, k0:k1])
@@ -157,7 +171,10 @@ def tile_modelnew_t_kernel(tc, Q, K, V, out):
         pps = {}
 
         def prep_t(kv, part):
-            ps = psq.tile([P, 8, P], BF16, name="qps", tag="qps")
+            if kv == 0 and part > 0:
+                ps = pst.tile([P, 8, P], BF16, name="tp", tag="tp")
+            else:
+                ps = psq.tile([P, 8, P], BF16, name="qps", tag="qps")
             if part == 0:
                 for j in range(4):
                     nc.tensor.transpose(ps[:, j, :], kn[kv][:, j, :], ident[:])
@@ -174,7 +191,10 @@ def tile_modelnew_t_kernel(tc, Q, K, V, out):
                 nc.vector.tensor_copy(out=kts[kv][:], in_=ps[:, 0:4, :])
             else:
                 h = 8 * (part - 1)
-                nc.vector.tensor_copy(out=qts[kv][:, h : h + 8, :], in_=ps[:])
+                if kv == 0 and part == 1:
+                    nc.scalar.copy(out=qts[kv][:, h : h + 8, :], in_=ps[:])
+                else:
+                    nc.vector.tensor_copy(out=qts[kv][:, h : h + 8, :], in_=ps[:])
 
         def s_dummy():
             nc.tensor.matmul(
@@ -314,7 +334,7 @@ def tile_modelnew_t_kernel(tc, Q, K, V, out):
             d = stt[i]
             gt = gp.tile([P, P, 4], BF16, name="gt", tag="gt", align_bytes=64)
             src = d["tp"][:].rearrange("p t r -> p r t")
-            if i % 4 != 3:
+            if i % 3 != 2:
                 nc.scalar.copy(out=gt[:], in_=src)
             else:
                 nc.vector.tensor_copy(out=gt[:], in_=src)
@@ -386,7 +406,18 @@ def tile_modelnew_t_kernel(tc, Q, K, V, out):
                     in1=rl.rearrange("p (x y) -> p x y", x=2).unsqueeze(3).to_broadcast([P, 2, 2, D]),
                     op=ALU.mult,
                 )
-            if bank == 3:
+            if kv == HKV - 1:
+                if bank == 0:
+                    spans = ((6, 9), (15, 16))
+                else:
+                    spans = ((a, a + 2), (a + 9, a + 11))
+                for b0, b1 in spans:
+                    for g in range(G):
+                        nc.sync.dma_start(
+                            out=out[0, G * kv + g].rearrange("(b i) d -> i b d", i=NB)[:, b0:b1, :],
+                            in_=o[g:P:G, b0:b1, :],
+                        )
+            elif bank == 3:
                 for g in range(G):
                     nc.sync.dma_start(
                         out=out[0, G * kv + g].rearrange("(b i) d -> i b d", i=NB),
@@ -402,19 +433,21 @@ def tile_modelnew_t_kernel(tc, Q, K, V, out):
         at(0, lambda: v_quant(0, 2))
         for n_, b in enumerate(VORDER):
             at(1 + n_, lambda b=b: v_variant_dve(b, 0, 2))
-            at(1 + n_, lambda b=b: v_zero_lo(b, 2, HKV))
-            at(8 + n_, lambda b=b: v_zero_hi(b, 2, HKV))
         at(8, lambda: v_regroup(2, 4))
         at(9, lambda: v_quant(2, 4))
         at(10, lambda: v_regroup(4, HKV))
         at(11, lambda: v_quant(4, HKV))
         for b in VORDER:
-            at(15, lambda b=b: v_variant_dma(b, 2, HKV))
+            at(10, lambda b=b: v_variant_dma(b, 2, 4))
+            at(12, lambda b=b: v_variant_dma(b, 4, HKV))
+        for ti in range(4, NT):
+            at(ti - 4, lambda ti=ti: p_zero(ti))
         for ti in range(NT):
             at(ti, lambda ti=ti: nc.gpsimd.memset(pt[1][ti][:], 0.0))
 
         for part in range(3):
             prep_t(0, part)
+        for part in range(3):
             prep_c(0, part)
         s_qk(0, 0)
         s_qk(0, 1)

@@ -62,7 +62,7 @@ def tile_modelnew_t_kernel(tc, Q, K, V, out):
         thp = ctx.enter_context(tc.tile_pool(name="thp", bufs=6))
         gp = ctx.enter_context(tc.tile_pool(name="gp", bufs=3))
         small = ctx.enter_context(tc.tile_pool(name="small", bufs=8))
-        op = ctx.enter_context(tc.tile_pool(name="op", bufs=2))
+        op = ctx.enter_context(tc.tile_pool(name="op", bufs=3))
         psq = ctx.enter_context(tc.psum_pool(name="psq", bufs=1))
         psr = ctx.enter_context(tc.psum_pool(name="psr", bufs=2))
         pst = ctx.enter_context(tc.psum_pool(name="pst", bufs=2))
@@ -126,8 +126,6 @@ def tile_modelnew_t_kernel(tc, Q, K, V, out):
 
         for ti in range(4):
             p_zero(ti)
-        zt = const.tile([P, 4, P], I32, name="zt")
-        nc.vector.memset(zt[:], 0)
         vlo = {}
         vhi = {}
         for b in VORDER:
@@ -149,13 +147,11 @@ def tile_modelnew_t_kernel(tc, Q, K, V, out):
                 in_=vg[:, k0:k1].rearrange("p h d j -> p (h d j)"),
             )
 
-        def v_zero_dma(b, k0, k1):
-            nc.sync.dma_start(out=vlo[b][8 * b : P, k0:k1], in_=zt[8 * b : P, 0 : k1 - k0])
-            nc.sync.dma_start(out=vhi[b][0 : 8 * b, k0:k1], in_=zt[0 : 8 * b, 0 : k1 - k0])
+        def v_zero_lo(b, k0, k1):
+            nc.vector.memset(vlo[b][:, k0:k1], 0)
 
-        for k0, k1 in ((2, 4), (4, HKV)):
-            for b in VORDER:
-                v_zero_dma(b, k0, k1)
+        def v_zero_hi(b, k0, k1):
+            nc.vector.memset(vhi[b][0 : 8 * b, k0:k1], 0)
 
         def v_variant_dve(b, k0, k1):
             nc.vector.tensor_copy(out=vlo[b][0 : 8 * b, k0:k1], in_=vc[0 : 8 * b, k0:k1])
@@ -433,13 +429,14 @@ def tile_modelnew_t_kernel(tc, Q, K, V, out):
         at(0, lambda: v_quant(0, 2))
         for n_, b in enumerate(VORDER):
             at(1 + n_, lambda b=b: v_variant_dve(b, 0, 2))
+            at(1 + n_, lambda b=b: v_zero_lo(b, 2, HKV))
+            at(5 + n_, lambda b=b: v_zero_hi(b, 2, HKV))
         at(8, lambda: v_regroup(2, 4))
         at(9, lambda: v_quant(2, 4))
         at(10, lambda: v_regroup(4, HKV))
         at(11, lambda: v_quant(4, HKV))
         for b in VORDER:
-            at(10, lambda b=b: v_variant_dma(b, 2, 4))
-            at(12, lambda b=b: v_variant_dma(b, 4, HKV))
+            at(12, lambda b=b: v_variant_dma(b, 2, HKV))
         for ti in range(4, NT):
             at(ti - 4, lambda ti=ti: p_zero(ti))
         for ti in range(NT):

@@ -31,7 +31,7 @@ MASK_POOL = True
 NB_POOL = True
 ACT_EVAC_MOD = 4
 NSETS = 2
-L_TANH, L_MAX, L_EXP, L_TR, L_EVAC, L_QUANT, L_MX, L_NORM = 0, 2, 4, 5, 6, 7, 8, 9
+L_TANH, L_MAX, L_EXP, L_TR, L_EVAC, L_QUANT, L_MX, L_NORM = 0, 2, 4, 5, 6, 8, 10, 11
 TILES = [
     ((7,), 0, (1,)),
     ((8,), 0, (2,)),
@@ -95,8 +95,7 @@ def tile_modelnew_t_kernel(tc, Q, K, V, out):
         load_v(0, 2)
         load_qk(1)
         load_v(2, HKV)
-        for kv in range(2, HKV):
-            load_qk(kv)
+        load_qk(2)
 
         ident = const.tile([P, P], BF16, name="ident")
         make_identity(nc, ident[:])
@@ -126,6 +125,8 @@ def tile_modelnew_t_kernel(tc, Q, K, V, out):
 
         for ti in range(4):
             p_zero(ti)
+        zt = const.tile([P, HKV - 2, P], I32, name="zt")
+        nc.vector.memset(zt[:], 0)
         vlo = {}
         vhi = {}
         for b in VORDER:
@@ -147,11 +148,13 @@ def tile_modelnew_t_kernel(tc, Q, K, V, out):
                 in_=vg[:, k0:k1].rearrange("p h d j -> p (h d j)"),
             )
 
-        def v_zero_lo(b, k0, k1):
-            nc.vector.memset(vlo[b][:, k0:k1], 0)
+        def v_zero_dma(b, k0, k1):
+            nc.sync.dma_start(out=vlo[b][8 * b : P, k0:k1], in_=zt[8 * b : P, 0 : k1 - k0])
+            nc.sync.dma_start(out=vhi[b][0 : 8 * b, k0:k1], in_=zt[0 : 8 * b, 0 : k1 - k0])
 
-        def v_zero_hi(b, k0, k1):
-            nc.vector.memset(vhi[b][0 : 8 * b, k0:k1], 0)
+        for b in VORDER:
+            v_zero_dma(b, 2, HKV)
+        load_qk(3)
 
         def v_variant_dve(b, k0, k1):
             nc.vector.tensor_copy(out=vlo[b][0 : 8 * b, k0:k1], in_=vc[0 : 8 * b, k0:k1])
@@ -319,36 +322,41 @@ def tile_modelnew_t_kernel(tc, Q, K, V, out):
             h = halves[(kv, bank // 2)]
             nc.vector.reciprocal(out=h["rl"][:], in_=h["le"][:])
 
+        duo = {}
+
         def s_tr(i):
             kv, ti, units, bank, slots = info(i)
-            tp = pst.tile([P, 4, P], BF16, name="tp", tag="tp")
+            if i % 2 == 0:
+                duo[i // 2] = {"tp": pst.tile([P, 2, 4, P], BF16, name="tp", tag="tp")}
+            tp = duo[i // 2]["tp"]
             for t in range(4):
-                nc.tensor.transpose(tp[:, t, :], pt[kv % NSETS][ti][:, t, :], ident[:])
-            stt[i]["tp"] = tp
+                nc.tensor.transpose(tp[:, i % 2, t, :], pt[kv % NSETS][ti][:, t, :], ident[:])
 
-        def s_evac(i):
-            d = stt[i]
-            gt = gp.tile([P, P, 4], BF16, name="gt", tag="gt", align_bytes=64)
-            src = d["tp"][:].rearrange("p t r -> p r t")
-            if i % 3 != 2:
+        def s_evac(j):
+            d = duo[j]
+            gt = gp.tile([P, 2, P, 4], BF16, name="gt", tag="gt", align_bytes=64)
+            src = d["tp"][:].rearrange("p n t r -> p n r t")
+            if j % 3 != 2:
                 nc.scalar.copy(out=gt[:], in_=src)
             else:
                 nc.vector.tensor_copy(out=gt[:], in_=src)
             d["gt"] = gt
 
-        def s_quant(i):
-            d = stt[i]
-            cd = gp.tile([P, P], I32, name="cd", tag="cd", align_bytes=64)
-            sc = gp.tile([P, P], U8, name="sc", tag="sc", align_bytes=64)
+        def s_quant(j):
+            d = duo[j]
+            cd = gp.tile([P, 2, P], I32, name="cd", tag="cd", align_bytes=64)
+            sc = gp.tile([P, 2, P], U8, name="sc", tag="sc", align_bytes=64)
             nc.vector.quantize_mx(
-                out=cd[:].bitcast(FP8X4), scales=sc[:], in_=d["gt"][:].rearrange("p r t -> p (r t)")
+                out=cd[:].rearrange("p n r -> p (n r)").bitcast(FP8X4),
+                scales=sc[:].rearrange("p n r -> p (n r)"),
+                in_=d["gt"][:].rearrange("p n r t -> p (n r t)"),
             )
             d["cd"] = cd
             d["sc"] = sc
 
         def s_mx(i):
             kv, ti, units, bank, slots = info(i)
-            d = stt[i]
+            d = duo[i // 2]
             bk = banks[(kv, bank)]
             if "acc" not in bk:
                 bk["acc"] = psa.tile([P, 4, D], F32, name="acc", tag="acc")
@@ -361,8 +369,8 @@ def tile_modelnew_t_kernel(tc, Q, K, V, out):
                     rhs = vhi[units[0] + 1]
                 nc.tensor.matmul_mx(
                     out=bk["acc"][:, slots[u], :],
-                    lhsT=d["cd"][:].bitcast(FP8X4),
-                    lhsT_scale=d["sc"][:],
+                    lhsT=d["cd"][:, i % 2, :].bitcast(FP8X4),
+                    lhsT_scale=d["sc"][:, i % 2, :],
                     rhs=rhs[:, kv, :].bitcast(FP8X4),
                     rhs_scale=vs[:, kv, :],
                     start=True,
@@ -429,14 +437,14 @@ def tile_modelnew_t_kernel(tc, Q, K, V, out):
         at(0, lambda: v_quant(0, 2))
         for n_, b in enumerate(VORDER):
             at(1 + n_, lambda b=b: v_variant_dve(b, 0, 2))
-            at(1 + n_, lambda b=b: v_zero_lo(b, 2, HKV))
-            at(5 + n_, lambda b=b: v_zero_hi(b, 2, HKV))
         at(8, lambda: v_regroup(2, 4))
         at(9, lambda: v_quant(2, 4))
         at(10, lambda: v_regroup(4, HKV))
         at(11, lambda: v_quant(4, HKV))
         for b in VORDER:
             at(12, lambda b=b: v_variant_dma(b, 2, HKV))
+        for kv in range(4, HKV):
+            at(12, lambda kv=kv: load_qk(kv))
         for ti in range(4, NT):
             at(ti - 4, lambda ti=ti: p_zero(ti))
         for ti in range(NT):
@@ -459,7 +467,8 @@ def tile_modelnew_t_kernel(tc, Q, K, V, out):
                 prep_t(kv + 1, (ti - 2) // 2)
             if s < total + L_MX:
                 s_dummy()
-            if ok(s - L_MX):
+            if ok(s - L_MX) and (s - L_MX) % 2 == 1:
+                s_mx(s - L_MX - 1)
                 s_mx(s - L_MX)
             if ok(s - L_TANH):
                 s_tanh(s - L_TANH)
@@ -473,13 +482,14 @@ def tile_modelnew_t_kernel(tc, Q, K, V, out):
                 s_rl(s - L_EXP - 1)
             if ok(s - L_EXP - 2):
                 s_rc(s - L_EXP - 2)
-            if ok(s - L_EVAC):
-                s_evac(s - L_EVAC)
+            if ok(s - L_EVAC) and (s - L_EVAC) % 2 == 1:
+                s_evac((s - L_EVAC) // 2)
             if kv + 1 < HKV and ti in (3, 5, 7):
                 prep_c(kv + 1, (ti - 3) // 2)
-            if ok(s - L_QUANT):
-                s_quant(s - L_QUANT)
-            if ok(s - L_NORM):
+            if ok(s - L_QUANT) and (s - L_QUANT) % 2 == 1:
+                s_quant((s - L_QUANT) // 2)
+            if ok(s - L_NORM) and (s - L_NORM) % 2 == 1:
+                s_norm(s - L_NORM - 1)
                 s_norm(s - L_NORM)
             for f in extra.get(s, []):
                 f()

@@ -18,91 +18,73 @@ HQ, HKV, S, D = 32, 8, 512, 128
 G = HQ // HKV
 NB = 32
 NPB = S // NB
-WBLK = 9
 SOFTCAP = 30.0
 SCALE = 1.0 / math.sqrt(D)
 EPS = 1e-9
 FILL = -1.0e4
 FLOPS = 2 * 2 * HQ * 98688 * D
 
-MANUAL = True
-VAR_DMA = True
-MASK_POOL = True
-NB_POOL = True
-ACT_EVAC_MOD = 4
-NSETS = 2
-L_TANH, L_MAX, L_EXP, L_TR, L_EVAC, L_QUANT, L_MX, L_NORM = 0, 2, 4, 5, 6, 8, 10, 11
-TILES = [
-    ((7,), 0, (1,)),
-    ((8,), 0, (2,)),
-    ((6, 15), 0, (0, 3)),
-    ((0, 9), 1, (0, 2)),
-    ((1, 10), 1, (1, 3)),
-    ((2, 11), 2, (0, 2)),
-    ((3, 12), 2, (1, 3)),
-    ((4, 13), 3, (0, 2)),
-    ((5, 14), 3, (1, 3)),
-]
-NT = len(TILES)
-VORDER = (7, 1, 2, 3, 4, 5, 6)
-
-
-def unit_cols(pb):
-    nblk = min(pb + 1, WBLK)
-    return 8 * (pb + 1 - nblk), 8 * (pb + 1)
+NGR = 4
+NT = 9
+NEAR0 = 224
+LONG0 = 256
+SLOT = 544
+LONG = 288
+QORDER = (0, 1, 9, 10, 2, 3, 11, 12, 4, 5, 13, 14, 6, 7, 8, 15)
+QPOS = {b: n for n, b in enumerate(QORDER)}
+VORDER = (1, 2, 3, 4, 5, 6, 7)
 
 
 def tile_modelnew_t_kernel(tc, Q, K, V, out):
     nc = tc.nc
     with ExitStack() as ctx:
-        if MANUAL:
-            ctx.enter_context(tc.manual_schedule())
+        ctx.enter_context(tc.manual_schedule())
         const = ctx.enter_context(tc.tile_pool(name="const", bufs=1))
         qtp = ctx.enter_context(tc.tile_pool(name="qtp", bufs=2))
-        thp = ctx.enter_context(tc.tile_pool(name="thp", bufs=6))
-        gp = ctx.enter_context(tc.tile_pool(name="gp", bufs=3))
-        small = ctx.enter_context(tc.tile_pool(name="small", bufs=8))
+        gp = ctx.enter_context(tc.tile_pool(name="gp", bufs=4))
+        small = ctx.enter_context(tc.tile_pool(name="small", bufs=6))
         op = ctx.enter_context(tc.tile_pool(name="op", bufs=3))
         psq = ctx.enter_context(tc.psum_pool(name="psq", bufs=1))
-        psr = ctx.enter_context(tc.psum_pool(name="psr", bufs=2))
+        psr = ctx.enter_context(tc.psum_pool(name="psr", bufs=3))
         pst = ctx.enter_context(tc.psum_pool(name="pst", bufs=2))
         psa = ctx.enter_context(tc.psum_pool(name="psa", bufs=2))
-        psd = ctx.enter_context(tc.psum_pool(name="psd", bufs=1))
-        dps = psd.tile([P, 512], F32, name="dps")
 
         qn = [const.tile([P, NPB, D], BF16, name="qn%d" % kv) for kv in range(HKV)]
         kn = [const.tile([P, 4, D], BF16, name="kn%d" % kv) for kv in range(HKV)]
         vn = const.tile([P, HKV, 4, D], BF16, name="vn")
 
-        def load_qk(kv):
+        def load_k(kv):
             nc.sync.dma_start(out=kn[kv][:], in_=K[0, kv].rearrange("(p j) d -> p j d", j=4))
+
+        def load_q(kv, b0, b1):
             for g in range(G):
                 nc.sync.dma_start(
-                    out=qn[kv][g:P:G, :, :],
-                    in_=Q[0, G * kv + g].rearrange("(b i) d -> i b d", i=NB),
+                    out=qn[kv][g:P:G, b0:b1, :],
+                    in_=Q[0, G * kv + g].rearrange("(b i) d -> i b d", i=NB)[:, b0:b1, :],
                 )
 
         def load_v(k0, k1):
             nc.sync.dma_start(out=vn[:, k0:k1], in_=V[0, k0:k1].rearrange("h (p j) d -> p h j d", j=4))
 
-        nc.sync.dma_start(out=kn[0][:], in_=K[0, 0].rearrange("(p j) d -> p j d", j=4))
-        for h in range(2):
-            for g in range(G):
-                nc.sync.dma_start(
-                    out=qn[0][g:P:G, 8 * h : 8 * h + 8, :],
-                    in_=Q[0, g].rearrange("(b i) d -> i b d", i=NB)[:, 8 * h : 8 * h + 8, :],
-                )
+        load_k(0)
+        load_q(0, 0, 8)
+        load_q(0, 8, NPB)
         load_v(0, 2)
-        load_qk(1)
+        load_k(1)
+        load_q(1, 0, NPB)
         load_v(2, HKV)
-        load_qk(2)
+        load_k(2)
+        load_q(2, 0, NPB)
 
         ident = const.tile([P, P], BF16, name="ident")
         make_identity(nc, ident[:])
 
+        th = [const.tile([P, 2, SLOT], F32, name="th%d" % j) for j in range(NGR)]
+        nc.gpsimd.memset(th[0][:], FILL)
+
         mnear = const.tile([P, 32], F32, name="mnear")
-        mboth = const.tile([P, 64], F32, name="mboth")
         mfar = const.tile([P, 32], F32, name="mfar")
+        mk = const.tile([P, 64], F32, name="mk")
         nc.gpsimd.memset(mnear[:], 0.0)
         nc.gpsimd.memset(mfar[:], 0.0)
         nc.gpsimd.affine_select(
@@ -113,18 +95,23 @@ def tile_modelnew_t_kernel(tc, Q, K, V, out):
             out=mfar[:], in_=mfar[:], pattern=[[4, 4], [16, 8]], compare_op=ALU.is_ge,
             fill=FILL, base=3, channel_multiplier=-1,
         )
-        mn4 = mnear[:].rearrange("p (t c) -> p t c", t=4)
-        mb4 = mboth[:].rearrange("p (t a c) -> p t a c", t=4, a=2)
-        nc.gpsimd.tensor_copy(out=mb4[:, :, 0, :], in_=mfar[:].rearrange("p (t c) -> p t c", t=4))
-        nc.gpsimd.tensor_copy(out=mb4[:, :, 1, :], in_=mn4)
+        nc.gpsimd.tensor_copy(out=mk[:, 0:32], in_=mnear[:])
+        nc.gpsimd.tensor_copy(out=mk[:, 32:64], in_=mfar[:])
 
-        pt = [[const.tile([P, 4, P], BF16, name="pt%d_%d" % (st, ti)) for ti in range(NT)] for st in range(NSETS)]
+        pt = [[const.tile([P, 4, P], BF16, name="pt%d_%d" % (st, ti)) for ti in range(NT)] for st in range(2)]
 
-        def p_zero(ti):
-            nc.vector.memset(pt[0][ti][:].rearrange("p t w -> p (t w)").bitcast(I32), 0)
+        def p_zero(st, ti):
+            nc.gpsimd.memset(pt[st][ti][:].rearrange("p t w -> p (t w)").bitcast(I32), 0)
 
-        for ti in range(4):
-            p_zero(ti)
+        for j in range(NGR):
+            if j:
+                nc.gpsimd.memset(th[j][:], FILL)
+            p_zero(0, 2 * j)
+            p_zero(0, 2 * j + 1)
+        p_zero(0, 8)
+        for ti in range(NT):
+            p_zero(1, ti)
+
         zt = const.tile([P, HKV - 2, P], I32, name="zt")
         nc.vector.memset(zt[:], 0)
         vlo = {}
@@ -148,348 +135,320 @@ def tile_modelnew_t_kernel(tc, Q, K, V, out):
                 in_=vg[:, k0:k1].rearrange("p h d j -> p (h d j)"),
             )
 
-        def v_zero_dma(b, k0, k1):
-            nc.sync.dma_start(out=vlo[b][8 * b : P, k0:k1], in_=zt[8 * b : P, 0 : k1 - k0])
-            nc.sync.dma_start(out=vhi[b][0 : 8 * b, k0:k1], in_=zt[0 : 8 * b, 0 : k1 - k0])
-
         for b in VORDER:
-            v_zero_dma(b, 2, HKV)
-        load_qk(3)
+            nc.sync.dma_start(out=vlo[b][8 * b : P, 2:HKV], in_=zt[8 * b : P])
+            nc.sync.dma_start(out=vhi[b][0 : 8 * b, 2:HKV], in_=zt[0 : 8 * b])
+        load_k(3)
+        load_q(3, 0, NPB)
 
-        def v_variant_dve(b, k0, k1):
-            nc.vector.tensor_copy(out=vlo[b][0 : 8 * b, k0:k1], in_=vc[0 : 8 * b, k0:k1])
-            nc.vector.tensor_copy(out=vhi[b][:, k0:k1], in_=vc[:, k0:k1])
-            nc.vector.memset(vhi[b][0 : 8 * b, k0:k1], 0)
+        def v_variant_dve(b):
+            nc.vector.tensor_copy(out=vlo[b][0 : 8 * b, 0:2], in_=vc[0 : 8 * b, 0:2])
+            nc.vector.tensor_copy(out=vhi[b][:, 0:2], in_=vc[:, 0:2])
+            nc.vector.memset(vhi[b][0 : 8 * b, 0:2], 0)
 
-        def v_variant_dma(b, k0, k1):
-            nc.sync.dma_start(out=vlo[b][0 : 8 * b, k0:k1], in_=vc[0 : 8 * b, k0:k1])
-            nc.sync.dma_start(out=vhi[b][8 * b : P, k0:k1], in_=vc[8 * b : P, k0:k1])
+        def v_variant_dma(b):
+            nc.sync.dma_start(out=vlo[b][0 : 8 * b, 2:HKV], in_=vc[0 : 8 * b, 2:HKV])
+            nc.sync.dma_start(out=vhi[b][8 * b : P, 2:HKV], in_=vc[8 * b : P, 2:HKV])
 
         kts = {}
         qts = {}
         pps = {}
 
-        def prep_t(kv, part):
-            if kv == 0 and part > 0:
+        def prep_pe(kv, part):
+            if kv == 0 and part < 2:
                 ps = pst.tile([P, 8, P], BF16, name="tp", tag="tp")
             else:
                 ps = psq.tile([P, 8, P], BF16, name="qps", tag="qps")
-            if part == 0:
-                for j in range(4):
-                    nc.tensor.transpose(ps[:, j, :], kn[kv][:, j, :], ident[:])
+            if part == 2:
+                for t in range(4):
+                    nc.tensor.transpose(ps[:, t, :], kn[kv][:, t, :], ident[:])
             else:
-                for b in range(8):
-                    nc.tensor.transpose(ps[:, b, :], qn[kv][:, 8 * (part - 1) + b, :], ident[:])
+                for n in range(8):
+                    nc.tensor.transpose(ps[:, n, :], qn[kv][:, QORDER[8 * part + n], :], ident[:])
             pps[(kv, part)] = ps
 
-        def prep_c(kv, part):
+        def prep_copy(kv, part):
             ps = pps[(kv, part)]
-            if part == 0:
-                kts[kv] = qtp.tile([P, 4, P], BF16, name="kt", tag="kt")
-                qts[kv] = qtp.tile([P, NPB, P], BF16, name="qt", tag="qt")
-                nc.vector.tensor_copy(out=kts[kv][:], in_=ps[:, 0:4, :])
+            if part == 2:
+                kts[kv] = qtp.tile([P, 16, 4, 8], BF16, name="kt", tag="kt")
+                nc.vector.tensor_copy(
+                    out=kts[kv][:], in_=ps[:, 0:4, :].rearrange("p t (b c) -> p b t c", c=8)
+                )
             else:
-                h = 8 * (part - 1)
-                if kv == 0 and part == 1:
-                    nc.scalar.copy(out=qts[kv][:, h : h + 8, :], in_=ps[:])
+                if part == 0:
+                    qts[kv] = qtp.tile([P, NPB, P], BF16, name="qt", tag="qt")
+                o = qts[kv][:, 8 * part : 8 * part + 8, :]
+                if kv == 0 and part == 0:
+                    nc.scalar.copy(out=o, in_=ps[:])
                 else:
-                    nc.vector.tensor_copy(out=qts[kv][:, h : h + 8, :], in_=ps[:])
+                    nc.vector.tensor_copy(out=o, in_=ps[:])
 
-        def s_dummy():
-            nc.tensor.matmul(
-                out=dps[:], lhsT=ident[:], rhs=qn[0][:, 0:4, :].rearrange("p b d -> p (b d)"), start=True, stop=True
-            )
-
-        total = HKV * NT
-        stt = {}
-        banks = {}
-        oall = {}
+        NG = HKV * NGR
+        st = {}
         halves = {}
+        oall = {}
 
-        def info(i):
-            kv, ti = divmod(i, NT)
-            units, bank, slots = TILES[ti]
-            return kv, ti, units, bank, slots
+        def ok(g):
+            return 0 <= g < NG
 
-        def ok(i):
-            return 0 <= i < total
+        def short_of(j, s):
+            return 2 * j + s
 
-        def s_qk(i, u):
-            kv, ti, units, bank, slots = info(i)
-            if u >= len(units):
-                return
-            if u == 0:
-                offs = []
-                off = 0
-                for pb in units:
-                    c0, c1 = unit_cols(pb)
-                    offs.append((off, 4 * (c1 - c0)))
-                    off += 4 * (c1 - c0)
-                stt[i] = {"raw": psr.tile([P, 512], F32, name="raw", tag="raw"), "offs": offs, "tot": off}
-            d = stt[i]
-            pb = units[u]
-            off, n = d["offs"][u]
-            c0, c1 = unit_cols(pb)
-            nc.tensor.matmul(
-                out=d["raw"][:, off : off + n].rearrange("p (t c) -> p t c", t=4),
-                lhsT=qts[kv][:, pb, :],
-                rhs=kts[kv][:, :, c0:c1],
-                start=True,
-                stop=True,
-            )
+        def place(j, kind, s):
+            return s if kind == 0 else (2 + s if j < 3 else 3 - s)
 
-        def s_tanh(i):
-            d = stt[i]
-            th = thp.tile([P, 512], F32, name="th", tag="th")
-            nc.scalar.activation(
-                out=th[:, 0 : d["tot"]], in_=d["raw"][:, 0 : d["tot"]], func=AF.Tanh, scale=SCALE / SOFTCAP
-            )
-            d["th"] = th
+        def s_qk(g):
+            kv, j = divmod(g, NGR)
+            st[g] = {"raw": []}
+            kt = kts[kv][:].rearrange("p b t c -> p (b t c)")
 
-        def s_mask(i):
-            kv, ti, units, bank, slots = info(i)
-            d = stt[i]
-            eng = nc.gpsimd if MASK_POOL else nc.vector
-            for pb, (off, n) in zip(units, d["offs"]):
-                v = d["th"][:, off : off + n].rearrange("p (t c) -> p t c", t=4)
-                c = n // 4
-                if pb >= WBLK - 1:
-                    w = v.rearrange("p t (a c) -> p t a c", c=8)[:, :, 0:WBLK:8, :]
-                    eng.tensor_tensor(out=w, in0=w, in1=mb4, op=ALU.add)
+            def mm(dst, pb, nblk):
+                w0 = 32 * (pb + 1 - nblk)
+                nc.tensor.matmul(
+                    out=dst, lhsT=qts[kv][:, QPOS[pb], :], rhs=kt[:, w0 : w0 + 32 * nblk], start=True, stop=True
+                )
+
+            for s in range(2):
+                k = short_of(j, s)
+                w = 32 * (k + 1)
+                raw = psr.tile([P, 512], F32, name="raw", tag="raw")
+                mm(raw[:, 0:w], k, k + 1)
+                if k < 7:
+                    mm(raw[:, w : w + LONG], k + 9, 9)
+                    st[g]["raw"].append((raw, w + LONG, s, LONG0 - w))
                 else:
-                    w = v[:, :, c - 8 : c]
-                    eng.tensor_tensor(out=w, in0=w, in1=mn4, op=ALU.add)
+                    st[g]["raw"].append((raw, w, s, LONG0 - w))
+                    raw = psr.tile([P, 512], F32, name="raw", tag="raw")
+                    mm(raw[:, 0:LONG], 8, 9)
+                    st[g]["raw"].append((raw, LONG, s, LONG0))
 
-        def s_max(i):
-            d = stt[i]
-            mx = small.tile([P, 2], F32, name="mx", tag="mx")
-            for u, (off, n) in enumerate(d["offs"]):
-                nc.vector.tensor_reduce(out=mx[:, u : u + 1], in_=d["th"][:, off : off + n], axis=AX.X, op=ALU.max)
-            d["mx"] = mx
-
-        def s_nb(i):
-            d = stt[i]
-            k = len(d["offs"])
-            nb = small.tile([P, 2], F32, name="nb", tag="nb")
-            if NB_POOL:
-                nc.gpsimd.tensor_scalar(
-                    out=nb[:, 0:k], in0=d["mx"][:, 0:k], scalar1=-SOFTCAP, scalar2=0.0, op0=ALU.mult, op1=ALU.add
-                )
-            else:
-                nc.vector.tensor_scalar(
-                    out=nb[:, 0:k], in0=d["mx"][:, 0:k], scalar1=-SOFTCAP, scalar2=None, op0=ALU.mult
-                )
-            d["nb"] = nb
-
-        def s_exp(i):
-            kv, ti, units, bank, slots = info(i)
-            d = stt[i]
-            key = (kv, bank)
-            if key not in banks:
-                banks[key] = {"n": 0}
-            hk = (kv, bank // 2)
-            if hk not in halves:
-                halves[hk] = {"ls": small.tile([P, 8], F32, name="ls", tag="ls")}
-            ls = halves[hk]["ls"]
-            sb = 4 * (bank % 2)
-            ptile = pt[kv % NSETS][ti]
-            for u, pb in enumerate(units):
-                off, n = d["offs"][u]
-                c0, c1 = unit_cols(pb)
+        def s_tanh(g):
+            kv, j = divmod(g, NGR)
+            for raw, w, s, c0 in st[g]["raw"]:
                 nc.scalar.activation(
-                    out=ptile[:, :, c0:c1],
-                    in_=d["th"][:, off : off + n].rearrange("p (t c) -> p t c", t=4),
-                    func=AF.Exp,
-                    bias=d["nb"][:, u : u + 1],
-                    scale=SOFTCAP,
-                    accum_out=ls[:, sb + slots[u] : sb + slots[u] + 1],
+                    out=th[j][:, s, c0 : c0 + w], in_=raw[:, 0:w], func=AF.Tanh, scale=SCALE / SOFTCAP
                 )
 
-        def s_rl(i):
-            kv, ti, units, bank, slots = info(i)
-            if ti not in (4, 8):
-                return
-            h = halves[(kv, bank // 2)]
-            le = small.tile([P, 8], F32, name="le", tag="le")
-            h["rl"] = small.tile([P, 8], F32, name="rl", tag="rl")
-            nc.gpsimd.tensor_scalar(out=le[:], in0=h["ls"][:], scalar1=EPS, scalar2=1.0, op0=ALU.add, op1=ALU.mult)
-            h["le"] = le
+        def s_mask(g):
+            j = g % NGR
+            for c0, w in ((NEAR0, 64), (LONG0 + LONG - 32, 32)):
+                v = th[j][:, :, c0 : c0 + w]
+                nc.vector.tensor_tensor(
+                    out=v, in0=v, in1=mk[:, 0:w].unsqueeze(1).to_broadcast([P, 2, w]), op=ALU.add
+                )
 
-        def s_rc(i):
-            kv, ti, units, bank, slots = info(i)
-            if ti not in (4, 8):
+        def s_max_long(g):
+            j = g % NGR
+            mx = small.tile([P, 4], F32, name="mx", tag="mx")
+            st[g]["mx"] = mx
+            nc.vector.tensor_reduce(
+                out=mx[:, 2:4], in_=th[j][:, :, LONG0 : LONG0 + LONG], axis=AX.X, op=ALU.max
+            )
+
+        def s_max_short(g):
+            j = g % NGR
+            w = 64 * (j + 1)
+            nc.vector.tensor_reduce(
+                out=st[g]["mx"][:, 0:2], in_=th[j][:, :, LONG0 - w : LONG0], axis=AX.X, op=ALU.max
+            )
+
+        def s_nb(g):
+            nb = small.tile([P, 4], F32, name="nb", tag="nb")
+            nc.vector.tensor_scalar(
+                out=nb[:], in0=st[g]["mx"][:], scalar1=-SOFTCAP, scalar2=None, op0=ALU.mult
+            )
+            st[g]["nb"] = nb
+
+        def s_exp(g):
+            kv, j = divmod(g, NGR)
+            h = g // 2
+            if h not in halves:
+                halves[h] = {"ls": small.tile([P, 8], F32, name="ls", tag="ls")}
+            ls = halves[h]["ls"]
+            nb = st[g]["nb"]
+            for kind in range(2):
+                for s in range(2):
+                    k = short_of(j, s)
+                    if kind == 0:
+                        c0, nblk, blk0, ti = LONG0 - 32 * (k + 1), k + 1, 0, k
+                    elif k < 7:
+                        c0, nblk, blk0, ti = LONG0, 9, k + 1, k
+                    else:
+                        c0, nblk, blk0, ti = LONG0, 9, 0, 8
+                    u = 2 * kind + s
+                    col = 4 * (g % 2) + place(j, kind, s)
+                    nc.scalar.activation(
+                        out=pt[kv % 2][ti][:, :, 8 * blk0 : 8 * (blk0 + nblk)].rearrange("p t (b c) -> p t b c", c=8),
+                        in_=th[j][:, s, c0 : c0 + 32 * nblk].rearrange("p (b t c) -> p t b c", t=4, c=8),
+                        func=AF.Exp,
+                        bias=nb[:, u : u + 1],
+                        scale=SOFTCAP,
+                        accum_out=ls[:, col : col + 1],
+                    )
+
+        def s_rl_add(g):
+            if g % 2 == 0:
                 return
-            h = halves[(kv, bank // 2)]
+            h = halves[g // 2]
+            h["le"] = small.tile([P, 8], F32, name="le", tag="le")
+            nc.gpsimd.tensor_scalar(out=h["le"][:], in0=h["ls"][:], scalar1=EPS, scalar2=1.0, op0=ALU.add, op1=ALU.mult)
+
+        def s_rl(g):
+            if g % 2 == 0:
+                return
+            h = halves[g // 2]
+            h["rl"] = small.tile([P, 8], F32, name="rl", tag="rl")
             nc.vector.reciprocal(out=h["rl"][:], in_=h["le"][:])
 
-        duo = {}
+        def tiles_of(g):
+            j = g % NGR
+            return ((2 * j, 2 * j + 1),) if j < 3 else ((6, 7), (8,))
 
-        def s_tr(i):
-            kv, ti, units, bank, slots = info(i)
-            if i % 2 == 0:
-                duo[i // 2] = {"tp": pst.tile([P, 2, 4, P], BF16, name="tp", tag="tp")}
-            tp = duo[i // 2]["tp"]
-            for t in range(4):
-                nc.tensor.transpose(tp[:, i % 2, t, :], pt[kv % NSETS][ti][:, t, :], ident[:])
+        def s_tr(g):
+            kv = g // NGR
+            st[g]["tp"] = []
+            for tis in tiles_of(g):
+                tp = pst.tile([P, 2, 4, P], BF16, name="tp", tag="tp")
+                for n, ti in enumerate(tis):
+                    for t in range(4):
+                        nc.tensor.transpose(tp[:, n, t, :], pt[kv % 2][ti][:, t, :], ident[:])
+                st[g]["tp"].append((tp, len(tis)))
 
-        def s_evac(j):
-            d = duo[j]
-            gt = gp.tile([P, 2, P, 4], BF16, name="gt", tag="gt", align_bytes=64)
-            src = d["tp"][:].rearrange("p n t r -> p n r t")
-            if j % 3 != 2:
-                nc.scalar.copy(out=gt[:], in_=src)
-            else:
-                nc.vector.tensor_copy(out=gt[:], in_=src)
-            d["gt"] = gt
+        def s_evac(g):
+            st[g]["gt"] = []
+            for n, (tp, m) in enumerate(st[g]["tp"]):
+                gt = gp.tile([P, 2, P, 4], BF16, name="gt", tag="gt", align_bytes=64)
+                nc.scalar.copy(out=gt[:, 0:m], in_=tp[:, 0:m].rearrange("p n t r -> p n r t"))
+                st[g]["gt"].append((gt, m))
 
-        def s_quant(j):
-            d = duo[j]
-            cd = gp.tile([P, 2, P], I32, name="cd", tag="cd", align_bytes=64)
-            sc = gp.tile([P, 2, P], U8, name="sc", tag="sc", align_bytes=64)
-            nc.vector.quantize_mx(
-                out=cd[:].rearrange("p n r -> p (n r)").bitcast(FP8X4),
-                scales=sc[:].rearrange("p n r -> p (n r)"),
-                in_=d["gt"][:].rearrange("p n r t -> p (n r t)"),
-            )
-            d["cd"] = cd
-            d["sc"] = sc
-
-        def s_mx(i):
-            kv, ti, units, bank, slots = info(i)
-            d = duo[i // 2]
-            bk = banks[(kv, bank)]
-            if "acc" not in bk:
-                bk["acc"] = psa.tile([P, 4, D], F32, name="acc", tag="acc")
-            for u, pb in enumerate(units):
-                if len(units) == 1:
-                    rhs = vc
-                elif u == 0:
-                    rhs = vlo[units[0] + 1]
-                else:
-                    rhs = vhi[units[0] + 1]
-                nc.tensor.matmul_mx(
-                    out=bk["acc"][:, slots[u], :],
-                    lhsT=d["cd"][:, i % 2, :].bitcast(FP8X4),
-                    lhsT_scale=d["sc"][:, i % 2, :],
-                    rhs=rhs[:, kv, :].bitcast(FP8X4),
-                    rhs_scale=vs[:, kv, :],
-                    start=True,
-                    stop=True,
+        def s_quant(g):
+            st[g]["q"] = []
+            for gt, m in st[g]["gt"]:
+                cd = gp.tile([P, 2, P], I32, name="cd", tag="cd", align_bytes=64)
+                sc = gp.tile([P, 2, P], U8, name="sc", tag="sc", align_bytes=64)
+                nc.vector.quantize_mx(
+                    out=cd[:, 0:m].rearrange("p n r -> p (n r)").bitcast(FP8X4),
+                    scales=sc[:, 0:m].rearrange("p n r -> p (n r)"),
+                    in_=gt[:, 0:m].rearrange("p n r t -> p (n r t)"),
                 )
-                bk["n"] += 1
+                st[g]["q"].append((cd, sc))
 
-        def s_norm(i):
-            kv, ti, units, bank, slots = info(i)
-            bk = banks[(kv, bank)]
-            if ti not in (2, 4, 6, 8):
-                return
+        def s_mx(g):
+            kv, j = divmod(g, NGR)
+            acc = psa.tile([P, 4, D], F32, name="acc", tag="acc")
+            st[g]["acc"] = acc
+            for s in range(2):
+                k = short_of(j, s)
+                cd, sc = st[g]["q"][0]
+                if k < 7:
+                    jobs = ((0, cd, sc, s, vlo[k + 1]), (1, cd, sc, s, vhi[k + 1]))
+                else:
+                    cd8, sc8 = st[g]["q"][1]
+                    jobs = ((0, cd, sc, s, vc), (1, cd8, sc8, 0, vc))
+                for kind, c, e, n, rhs in jobs:
+                    nc.tensor.matmul_mx(
+                        out=acc[:, place(j, kind, s), :],
+                        lhsT=c[:, n, :].bitcast(FP8X4),
+                        lhsT_scale=e[:, n, :],
+                        rhs=rhs[:, kv, :].bitcast(FP8X4),
+                        rhs_scale=vs[:, kv, :],
+                        start=True,
+                        stop=True,
+                    )
+
+        def s_norm(g):
+            kv, j = divmod(g, NGR)
             if kv not in oall:
                 oall[kv] = op.tile([P, 22, D], F32, name="oall", tag="oall")
             o = oall[kv]
-            sb = 4 * (bank % 2)
-            rl = halves[(kv, bank // 2)]["rl"][:, sb : sb + 4]
-            acc = bk["acc"]
-            if bank == 0:
-                nc.vector.tensor_tensor(
-                    out=o[:, 6:9, :],
-                    in0=acc[:, 0:3, :],
-                    in1=rl[:, 0:3].unsqueeze(2).to_broadcast([P, 3, D]),
-                    op=ALU.mult,
-                )
-                nc.vector.tensor_tensor(
-                    out=o[:, 15:16, :],
-                    in0=acc[:, 3:4, :],
-                    in1=rl[:, 3:4].unsqueeze(2).to_broadcast([P, 1, D]),
-                    op=ALU.mult,
-                )
-            else:
-                a = 2 * (bank - 1)
+            rl = halves[g // 2]["rl"][:, 4 * (g % 2) : 4 * (g % 2) + 4]
+            acc = st[g]["acc"]
+            if j < 3:
+                a = 2 * j
+                spans = ((a, a + 2), (a + 9, a + 11))
                 nc.vector.tensor_tensor(
                     out=o[:, a : a + 18, :].rearrange("p (x y) d -> p x y d", x=2)[:, :, 0:2, :],
                     in0=acc[:].rearrange("p (x y) d -> p x y d", x=2),
                     in1=rl.rearrange("p (x y) -> p x y", x=2).unsqueeze(3).to_broadcast([P, 2, 2, D]),
                     op=ALU.mult,
                 )
+            else:
+                spans = ((6, 9), (15, 16))
+                for (b0, b1), u in zip(spans, (0, 3)):
+                    m = b1 - b0
+                    nc.vector.tensor_tensor(
+                        out=o[:, b0:b1, :],
+                        in0=acc[:, u : u + m, :],
+                        in1=rl[:, u : u + m].unsqueeze(2).to_broadcast([P, m, D]),
+                        op=ALU.mult,
+                    )
             if kv == HKV - 1:
-                if bank == 0:
-                    spans = ((6, 9), (15, 16))
-                else:
-                    spans = ((a, a + 2), (a + 9, a + 11))
                 for b0, b1 in spans:
-                    for g in range(G):
+                    for q in range(G):
                         nc.sync.dma_start(
-                            out=out[0, G * kv + g].rearrange("(b i) d -> i b d", i=NB)[:, b0:b1, :],
-                            in_=o[g:P:G, b0:b1, :],
+                            out=out[0, G * kv + q].rearrange("(b i) d -> i b d", i=NB)[:, b0:b1, :],
+                            in_=o[q:P:G, b0:b1, :],
                         )
-            elif bank == 3:
-                for g in range(G):
+            elif j == 3:
+                for q in range(G):
                     nc.sync.dma_start(
-                        out=out[0, G * kv + g].rearrange("(b i) d -> i b d", i=NB),
-                        in_=o[g:P:G, 0:NPB, :],
+                        out=out[0, G * kv + q].rearrange("(b i) d -> i b d", i=NB), in_=o[q:P:G, 0:NPB, :]
                     )
 
         extra = {}
 
-        def at(s, f):
-            extra[s] = extra.get(s, []) + [f]
+        def at(i, f):
+            extra.setdefault(i, []).append(f)
 
         at(0, lambda: v_regroup(0, 2))
         at(0, lambda: v_quant(0, 2))
-        for n_, b in enumerate(VORDER):
-            at(1 + n_, lambda b=b: v_variant_dve(b, 0, 2))
-        at(8, lambda: v_regroup(2, 4))
-        at(9, lambda: v_quant(2, 4))
-        at(10, lambda: v_regroup(4, HKV))
-        at(11, lambda: v_quant(4, HKV))
         for b in VORDER:
-            at(12, lambda b=b: v_variant_dma(b, 2, HKV))
+            at((b + 1) // 2, lambda b=b: v_variant_dve(b))
+        at(3, lambda: v_regroup(2, 4))
+        at(4, lambda: v_quant(2, 4))
+        at(4, lambda: v_regroup(4, HKV))
+        at(5, lambda: v_quant(4, HKV))
+        for b in VORDER:
+            at(5, lambda b=b: v_variant_dma(b))
         for kv in range(4, HKV):
-            at(12, lambda kv=kv: load_qk(kv))
-        for ti in range(4, NT):
-            at(ti - 4, lambda ti=ti: p_zero(ti))
-        for ti in range(NT):
-            at(ti, lambda ti=ti: nc.gpsimd.memset(pt[1][ti][:], 0.0))
+            at(5, lambda kv=kv: load_k(kv))
+            at(5, lambda kv=kv: load_q(kv, 0, NPB))
 
-        for part in range(3):
-            prep_t(0, part)
-        for part in range(3):
-            prep_c(0, part)
-        s_qk(0, 0)
-        s_qk(0, 1)
-        for s in range(total + L_NORM + 1):
-            kv, ti = divmod(s, NT)
-            if ok(s + 1):
-                s_qk(s + 1, 0)
-                s_qk(s + 1, 1)
-            if ok(s - L_TR):
-                s_tr(s - L_TR)
-            if kv + 1 < HKV and ti in (2, 4, 6):
-                prep_t(kv + 1, (ti - 2) // 2)
-            if s < total + L_MX:
-                s_dummy()
-            if ok(s - L_MX) and (s - L_MX) % 2 == 1:
-                s_mx(s - L_MX - 1)
-                s_mx(s - L_MX)
-            if ok(s - L_TANH):
-                s_tanh(s - L_TANH)
-                s_mask(s - L_TANH)
-            if ok(s - L_MAX):
-                s_max(s - L_MAX)
-                s_nb(s - L_MAX)
-            if ok(s - L_EXP):
-                s_exp(s - L_EXP)
-            if ok(s - L_EXP - 1):
-                s_rl(s - L_EXP - 1)
-            if ok(s - L_EXP - 2):
-                s_rc(s - L_EXP - 2)
-            if ok(s - L_EVAC) and (s - L_EVAC) % 2 == 1:
-                s_evac((s - L_EVAC) // 2)
-            if kv + 1 < HKV and ti in (3, 5, 7):
-                prep_c(kv + 1, (ti - 3) // 2)
-            if ok(s - L_QUANT) and (s - L_QUANT) % 2 == 1:
-                s_quant((s - L_QUANT) // 2)
-            if ok(s - L_NORM) and (s - L_NORM) % 2 == 1:
-                s_norm(s - L_NORM - 1)
-                s_norm(s - L_NORM)
-            for f in extra.get(s, []):
+        prep_pe(0, 2)
+        prep_pe(0, 0)
+        prep_pe(0, 1)
+        prep_copy(0, 2)
+        prep_copy(0, 0)
+        s_qk(0)
+        prep_copy(0, 1)
+        for i in range(NG + 5):
+            kv, j = divmod(i, NGR)
+            if ok(i):
+                s_tanh(i)
+                s_mask(i)
+            if j and kv + 1 < HKV:
+                prep_copy(kv + 1, j - 1)
+            if ok(i + 1):
+                s_qk(i + 1)
+            if ok(i - 2):
+                s_evac(i - 2)
+            if ok(i - 3):
+                s_quant(i - 3)
+                s_mx(i - 3)
+            if ok(i):
+                s_max_long(i)
+                s_max_short(i)
+            if ok(i - 2):
+                s_rl(i - 2)
+            if ok(i):
+                s_nb(i)
+            if j < 3 and kv + 1 < HKV:
+                prep_pe(kv + 1, j)
+            if ok(i - 1):
+                s_exp(i - 1)
+                s_rl_add(i - 1)
+                s_tr(i - 1)
+            if ok(i - 4):
+                s_norm(i - 4)
+            for f in extra.get(i, []):
                 f()

@@ -33,6 +33,9 @@ LONG = 288
 QORDER = (0, 1, 9, 10, 2, 3, 11, 12, 4, 5, 13, 14, 6, 7, 8, 15)
 QPOS = {b: n for n, b in enumerate(QORDER)}
 VORDER = (1, 2, 3, 4, 5, 6, 7)
+L_MASK, L_MAX, L_EXP, L_EVAC, L_QUANT, L_NORM = 0, 1, 2, 3, 4, 5
+MASK_ENG = "gpsimd"
+NFILL = 1
 
 
 def tile_modelnew_t_kernel(tc, Q, K, V, out):
@@ -66,21 +69,27 @@ def tile_modelnew_t_kernel(tc, Q, K, V, out):
         def load_v(k0, k1):
             nc.sync.dma_start(out=vn[:, k0:k1], in_=V[0, k0:k1].rearrange("h (p j) d -> p h j d", j=4))
 
-        load_k(0)
-        load_q(0, 0, 8)
-        load_q(0, 8, NPB)
-        load_v(0, 2)
+        nc.gpsimd.dma_start(out=kn[0][:], in_=K[0, 0].rearrange("(p j) d -> p j d", j=4))
+        load_q(0, 0, 4)
+        load_q(0, 9, 13)
+        load_q(0, 4, 9)
+        load_q(0, 13, NPB)
         load_k(1)
         load_q(1, 0, NPB)
+        load_v(0, 2)
         load_v(2, HKV)
         load_k(2)
         load_q(2, 0, NPB)
 
         ident = const.tile([P, P], BF16, name="ident")
         make_identity(nc, ident[:])
+        identf = const.tile([P, P], F32, name="identf")
+        nc.gpsimd.tensor_copy(out=identf[:], in_=ident[:])
 
         th = [const.tile([P, 2, SLOT], F32, name="th%d" % j) for j in range(NGR)]
-        nc.gpsimd.memset(th[0][:], FILL)
+        for j in range(NGR):
+            w = 64 * (j + 1)
+            nc.vector.memset(th[j][:, 0, LONG0 - w : LONG0 - w + 32], FILL)
 
         mnear = const.tile([P, 32], F32, name="mnear")
         mfar = const.tile([P, 32], F32, name="mfar")
@@ -95,22 +104,25 @@ def tile_modelnew_t_kernel(tc, Q, K, V, out):
             out=mfar[:], in_=mfar[:], pattern=[[4, 4], [16, 8]], compare_op=ALU.is_ge,
             fill=FILL, base=3, channel_multiplier=-1,
         )
-        nc.gpsimd.tensor_copy(out=mk[:, 0:32], in_=mnear[:])
-        nc.gpsimd.tensor_copy(out=mk[:, 32:64], in_=mfar[:])
+        for n, m in enumerate((mnear, mfar)):
+            nc.gpsimd.tensor_copy(
+                out=mk[:, 32 * n : 32 * n + 32].rearrange("p (u c e) -> p u c e", u=2, e=2),
+                in_=m[:].rearrange("p (u e c) -> p u c e", u=2, e=2),
+            )
 
-        pt = [[const.tile([P, 4, P], BF16, name="pt%d_%d" % (st, ti)) for ti in range(NT)] for st in range(2)]
+        pt = [[const.tile([P, 2, P, 2], BF16, name="pt%d_%d" % (st, ti)) for ti in range(NT)] for st in range(2)]
 
-        def p_zero(st, ti):
-            nc.gpsimd.memset(pt[st][ti][:].rearrange("p t w -> p (t w)").bitcast(I32), 0)
+        def words(t):
+            return t[:].rearrange("p u w e -> p (u w e)").bitcast(F32)
 
-        for j in range(NGR):
-            if j:
-                nc.gpsimd.memset(th[j][:], FILL)
-            p_zero(0, 2 * j)
-            p_zero(0, 2 * j + 1)
-        p_zero(0, 8)
+        def p_zero(ti):
+            b = ti + 10 if ti < 7 else ti + 1
+            for st in range(2):
+                if b < NPB:
+                    nc.vector.memset(pt[st][ti][:, :, 8 * b : P, :].rearrange("p u w e -> p u (w e)").bitcast(I32), 0)
+
         for ti in range(NT):
-            p_zero(1, ti)
+            p_zero(ti)
 
         zt = const.tile([P, HKV - 2, P], I32, name="zt")
         nc.vector.memset(zt[:], 0)
@@ -155,8 +167,15 @@ def tile_modelnew_t_kernel(tc, Q, K, V, out):
         pps = {}
 
         def prep_pe(kv, part):
-            if kv == 0 and part < 2:
-                ps = pst.tile([P, 8, P], BF16, name="tp", tag="tp")
+            if kv < 2 and part == 2:
+                ps = psa.tile([P, 8, P], BF16, name="acc", tag="acc")
+            elif kv == 0 and part == 0:
+                for h in range(2):
+                    ps = pst.tile([P, 4, P], BF16, name="tp", tag="tp")
+                    for n in range(4):
+                        nc.tensor.transpose(ps[:, n, :], qn[kv][:, QORDER[4 * h + n], :], ident[:])
+                    pps[(kv, h - 2)] = ps
+                return
             else:
                 ps = psq.tile([P, 8, P], BF16, name="qps", tag="qps")
             if part == 2:
@@ -168,20 +187,24 @@ def tile_modelnew_t_kernel(tc, Q, K, V, out):
             pps[(kv, part)] = ps
 
         def prep_copy(kv, part):
+            if kv == 0 and part == 0:
+                qts[kv] = qtp.tile([P, NPB, P], BF16, name="qt", tag="qt")
+                nc.scalar.copy(out=qts[kv][:, 0:4, :], in_=pps[(kv, -2)][:])
+                nc.vector.tensor_copy(out=qts[kv][:, 4:8, :], in_=pps[(kv, -1)][:])
+                return
             ps = pps[(kv, part)]
             if part == 2:
-                kts[kv] = qtp.tile([P, 16, 4, 8], BF16, name="kt", tag="kt")
-                nc.vector.tensor_copy(
-                    out=kts[kv][:], in_=ps[:, 0:4, :].rearrange("p t (b c) -> p b t c", c=8)
-                )
+                kts[kv] = qtp.tile([P, 16, 2, 8, 2], BF16, name="kt", tag="kt")
+                for u in range(2):
+                    nc.vector.tensor_copy(
+                        out=kts[kv][:, :, u, :, :],
+                        in_=ps[:, 2 * u : 2 * u + 2, :].rearrange("p e (b c) -> p b c e", c=8),
+                    )
             else:
                 if part == 0:
                     qts[kv] = qtp.tile([P, NPB, P], BF16, name="qt", tag="qt")
                 o = qts[kv][:, 8 * part : 8 * part + 8, :]
-                if kv == 0 and part == 0:
-                    nc.scalar.copy(out=o, in_=ps[:])
-                else:
-                    nc.vector.tensor_copy(out=o, in_=ps[:])
+                nc.vector.tensor_copy(out=o, in_=ps[:])
 
         NG = HKV * NGR
         st = {}
@@ -200,7 +223,7 @@ def tile_modelnew_t_kernel(tc, Q, K, V, out):
         def s_qk(g):
             kv, j = divmod(g, NGR)
             st[g] = {"raw": []}
-            kt = kts[kv][:].rearrange("p b t c -> p (b t c)")
+            kt = kts[kv][:].rearrange("p b u c e -> p (b u c e)")
 
             def mm(dst, pb, nblk):
                 w0 = 32 * (pb + 1 - nblk)
@@ -212,6 +235,10 @@ def tile_modelnew_t_kernel(tc, Q, K, V, out):
                 k = short_of(j, s)
                 w = 32 * (k + 1)
                 raw = psr.tile([P, 512], F32, name="raw", tag="raw")
+                if s < NFILL:
+                    nc.tensor.matmul(
+                        out=raw[:], lhsT=ident[:], rhs=qn[kv][:, 0:4, :].rearrange("p b d -> p (b d)"), start=True, stop=True
+                    )
                 mm(raw[:, 0:w], k, k + 1)
                 if k < 7:
                     mm(raw[:, w : w + LONG], k + 9, 9)
@@ -233,7 +260,7 @@ def tile_modelnew_t_kernel(tc, Q, K, V, out):
             j = g % NGR
             for c0, w in ((NEAR0, 64), (LONG0 + LONG - 32, 32)):
                 v = th[j][:, :, c0 : c0 + w]
-                nc.vector.tensor_tensor(
+                (nc.gpsimd if MASK_ENG == "gpsimd" else nc.vector).tensor_tensor(
                     out=v, in0=v, in1=mk[:, 0:w].unsqueeze(1).to_broadcast([P, 2, w]), op=ALU.add
                 )
 
@@ -278,8 +305,8 @@ def tile_modelnew_t_kernel(tc, Q, K, V, out):
                     u = 2 * kind + s
                     col = 4 * (g % 2) + place(j, kind, s)
                     nc.scalar.activation(
-                        out=pt[kv % 2][ti][:, :, 8 * blk0 : 8 * (blk0 + nblk)].rearrange("p t (b c) -> p t b c", c=8),
-                        in_=th[j][:, s, c0 : c0 + 32 * nblk].rearrange("p (b t c) -> p t b c", t=4, c=8),
+                        out=pt[kv % 2][ti][:, :, 8 * blk0 : 8 * (blk0 + nblk), :].rearrange("p u (b c) e -> p u b (c e)", c=8),
+                        in_=th[j][:, s, c0 : c0 + 32 * nblk].rearrange("p (b u x) -> p u b x", u=2, x=16),
                         func=AF.Exp,
                         bias=nb[:, u : u + 1],
                         scale=SOFTCAP,
@@ -308,17 +335,20 @@ def tile_modelnew_t_kernel(tc, Q, K, V, out):
             kv = g // NGR
             st[g]["tp"] = []
             for tis in tiles_of(g):
-                tp = pst.tile([P, 2, 4, P], BF16, name="tp", tag="tp")
+                tp = pst.tile([P, 2, 2, P], F32, name="tp", tag="tp")
                 for n, ti in enumerate(tis):
-                    for t in range(4):
-                        nc.tensor.transpose(tp[:, n, t, :], pt[kv % 2][ti][:, t, :], ident[:])
+                    for u in range(2):
+                        nc.tensor.transpose(tp[:, n, u, :], words(pt[kv % 2][ti])[:, P * u : P * u + P], identf[:])
                 st[g]["tp"].append((tp, len(tis)))
 
         def s_evac(g):
             st[g]["gt"] = []
             for n, (tp, m) in enumerate(st[g]["tp"]):
                 gt = gp.tile([P, 2, P, 4], BF16, name="gt", tag="gt", align_bytes=64)
-                nc.scalar.copy(out=gt[:, 0:m], in_=tp[:, 0:m].rearrange("p n t r -> p n r t"))
+                nc.scalar.copy(
+                    out=gt[:, 0:m].rearrange("p n r t -> p (n r t)").bitcast(F32).rearrange("p (n r u) -> p n r u", n=m, u=2),
+                    in_=tp[:, 0:m].rearrange("p n u r -> p n r u"),
+                )
                 st[g]["gt"].append((gt, m))
 
         def s_quant(g):
@@ -358,14 +388,26 @@ def tile_modelnew_t_kernel(tc, Q, K, V, out):
 
         def s_norm(g):
             kv, j = divmod(g, NGR)
+            rl = halves[g // 2]["rl"][:, 4 * (g % 2) : 4 * (g % 2) + 4]
+            acc = st[g]["acc"]
+            if kv == HKV - 1:
+                o = op.tile([P, 4, D], F32, name="olast%d" % j, bufs=1)
+                nc.vector.tensor_tensor(
+                    out=o[:], in0=acc[:], in1=rl.unsqueeze(2).to_broadcast([P, 4, D]), op=ALU.mult
+                )
+                spans = ((2 * j, 0, 2), (2 * j + 9, 2, 2)) if j < 3 else ((6, 0, 3), (15, 3, 1))
+                for b0, u, m in spans:
+                    for q in range(G):
+                        nc.sync.dma_start(
+                            out=out[0, G * kv + q].rearrange("(b i) d -> i b d", i=NB)[:, b0 : b0 + m, :],
+                            in_=o[q:P:G, u : u + m, :],
+                        )
+                return
             if kv not in oall:
                 oall[kv] = op.tile([P, 22, D], F32, name="oall", tag="oall")
             o = oall[kv]
-            rl = halves[g // 2]["rl"][:, 4 * (g % 2) : 4 * (g % 2) + 4]
-            acc = st[g]["acc"]
             if j < 3:
                 a = 2 * j
-                spans = ((a, a + 2), (a + 9, a + 11))
                 nc.vector.tensor_tensor(
                     out=o[:, a : a + 18, :].rearrange("p (x y) d -> p x y d", x=2)[:, :, 0:2, :],
                     in0=acc[:].rearrange("p (x y) d -> p x y d", x=2),
@@ -382,73 +424,72 @@ def tile_modelnew_t_kernel(tc, Q, K, V, out):
                         in1=rl[:, u : u + m].unsqueeze(2).to_broadcast([P, m, D]),
                         op=ALU.mult,
                     )
-            if kv == HKV - 1:
-                for b0, b1 in spans:
-                    for q in range(G):
-                        nc.sync.dma_start(
-                            out=out[0, G * kv + q].rearrange("(b i) d -> i b d", i=NB)[:, b0:b1, :],
-                            in_=o[q:P:G, b0:b1, :],
-                        )
-            elif j == 3:
+            if j == 3:
                 for q in range(G):
                     nc.sync.dma_start(
                         out=out[0, G * kv + q].rearrange("(b i) d -> i b d", i=NB), in_=o[q:P:G, 0:NPB, :]
                     )
+
+        prep = {1: [(1, 0)], 2: [(1, 1), (1, 2)]}
+        for kv in range(2, HKV):
+            for part in range(3):
+                prep[NGR * (kv - 1) + part] = [(kv, part)]
 
         extra = {}
 
         def at(i, f):
             extra.setdefault(i, []).append(f)
 
-        at(0, lambda: v_regroup(0, 2))
-        at(0, lambda: v_quant(0, 2))
+        at(1, lambda: v_regroup(0, 2))
+        at(2, lambda: v_quant(0, 2))
         for b in VORDER:
-            at((b + 1) // 2, lambda b=b: v_variant_dve(b))
-        at(3, lambda: v_regroup(2, 4))
-        at(4, lambda: v_quant(2, 4))
-        at(4, lambda: v_regroup(4, HKV))
-        at(5, lambda: v_quant(4, HKV))
+            at((b + 1) // 2 + 2, lambda b=b: v_variant_dve(b))
+        at(4, lambda: v_regroup(2, 4))
+        at(5, lambda: v_quant(2, 4))
+        at(5, lambda: v_regroup(4, HKV))
+        at(6, lambda: v_quant(4, HKV))
         for b in VORDER:
-            at(5, lambda b=b: v_variant_dma(b))
+            at(6, lambda b=b: v_variant_dma(b))
         for kv in range(4, HKV):
-            at(5, lambda kv=kv: load_k(kv))
-            at(5, lambda kv=kv: load_q(kv, 0, NPB))
+            at(6, lambda kv=kv: load_k(kv))
+            at(6, lambda kv=kv: load_q(kv, 0, NPB))
 
         prep_pe(0, 2)
         prep_pe(0, 0)
-        prep_pe(0, 1)
         prep_copy(0, 2)
         prep_copy(0, 0)
         s_qk(0)
+        prep_pe(0, 1)
         prep_copy(0, 1)
-        for i in range(NG + 5):
+        for i in range(NG + L_NORM + 1):
             kv, j = divmod(i, NGR)
             if ok(i):
                 s_tanh(i)
-                s_mask(i)
-            if j and kv + 1 < HKV:
-                prep_copy(kv + 1, j - 1)
+            if ok(i - L_MASK):
+                s_mask(i - L_MASK)
             if ok(i + 1):
                 s_qk(i + 1)
-            if ok(i - 2):
-                s_evac(i - 2)
-            if ok(i - 3):
-                s_quant(i - 3)
-                s_mx(i - 3)
-            if ok(i):
-                s_max_long(i)
-                s_max_short(i)
-            if ok(i - 2):
-                s_rl(i - 2)
-            if ok(i):
-                s_nb(i)
-            if j < 3 and kv + 1 < HKV:
-                prep_pe(kv + 1, j)
-            if ok(i - 1):
-                s_exp(i - 1)
-                s_rl_add(i - 1)
-                s_tr(i - 1)
-            if ok(i - 4):
-                s_norm(i - 4)
+            if ok(i - L_EVAC):
+                s_evac(i - L_EVAC)
+            if ok(i - L_QUANT):
+                s_quant(i - L_QUANT)
+                s_mx(i - L_QUANT)
+            if ok(i - L_MAX):
+                s_max_long(i - L_MAX)
+                s_max_short(i - L_MAX)
+            if ok(i - L_EXP - 1):
+                s_rl(i - L_EXP - 1)
+            if ok(i - L_MAX):
+                s_nb(i - L_MAX)
+            for a in prep.get(i, []):
+                prep_pe(*a)
+            if ok(i - L_EXP):
+                s_exp(i - L_EXP)
+                s_rl_add(i - L_EXP)
+                s_tr(i - L_EXP)
+            if ok(i - L_NORM):
+                s_norm(i - L_NORM)
+            for a in prep.get(i, []):
+                prep_copy(*a)
             for f in extra.get(i, []):
                 f()

@@ -36,6 +36,8 @@ VORDER = (1, 2, 3, 4, 5, 6, 7)
 L_MASK, L_MAX, L_EXP, L_EVAC, L_QUANT, L_NORM = 0, 1, 2, 3, 4, 5
 MASK_ENG = "gpsimd"
 NFILL = 1
+V_AT = {0: 1, 1: 1, 2: 2, 4: 3, 6: 4}
+EVAC_V = ()
 
 
 def tile_modelnew_t_kernel(tc, Q, K, V, out):
@@ -56,8 +58,8 @@ def tile_modelnew_t_kernel(tc, Q, K, V, out):
         kn = [const.tile([P, 4, D], BF16, name="kn%d" % kv) for kv in range(HKV)]
         vn = const.tile([P, HKV, 4, D], BF16, name="vn")
 
-        def load_k(kv):
-            nc.sync.dma_start(out=kn[kv][:], in_=K[0, kv].rearrange("(p j) d -> p j d", j=4))
+        def load_k(kv, eng=None):
+            (eng or nc.sync).dma_start(out=kn[kv][:], in_=K[0, kv].rearrange("(n p) d -> p n d", n=4))
 
         def load_q(kv, b0, b1):
             for g in range(G):
@@ -69,27 +71,36 @@ def tile_modelnew_t_kernel(tc, Q, K, V, out):
         def load_v(k0, k1):
             nc.sync.dma_start(out=vn[:, k0:k1], in_=V[0, k0:k1].rearrange("h (p j) d -> p h j d", j=4))
 
-        nc.gpsimd.dma_start(out=kn[0][:], in_=K[0, 0].rearrange("(p j) d -> p j d", j=4))
+        load_k(0, nc.gpsimd)
         load_q(0, 0, 4)
-        load_q(0, 9, 13)
+        load_q(0, 9, NPB)
         load_q(0, 4, 9)
-        load_q(0, 13, NPB)
+        load_v(0, 1)
         load_k(1)
         load_q(1, 0, NPB)
-        load_v(0, 2)
-        load_v(2, HKV)
+        load_v(1, 4)
+        load_v(4, HKV)
         load_k(2)
         load_q(2, 0, NPB)
 
         ident = const.tile([P, P], BF16, name="ident")
         make_identity(nc, ident[:])
+        perm = const.tile([P, P], BF16, name="perm")
+        for u in range(2):
+            nc.vector.tensor_copy(
+                out=perm[:].rearrange("p (b u c e) -> p b u c e", b=4, u=2, e=2)[:, :, u],
+                in_=ident[:].rearrange("p (b c u e) -> p b u c e", b=4, u=2, e=2)[:, :, u],
+            )
         identf = const.tile([P, P], F32, name="identf")
         nc.gpsimd.tensor_copy(out=identf[:], in_=ident[:])
 
-        th = [const.tile([P, 2, SLOT], F32, name="th%d" % j) for j in range(NGR)]
+        th = {}
         for j in range(NGR):
+            th[(False, j)] = const.tile([P, 2, SLOT], F32, name="th%d" % j)
+            th[(True, j)] = const.tile([P, 2, SLOT], F32, name="thl%d" % j) if j > 1 else th[(False, j)]
             w = 64 * (j + 1)
-            nc.vector.memset(th[j][:, 0, LONG0 - w : LONG0 - w + 32], FILL)
+            for t in (th[(False, j)], th[(True, j)])[0 : 1 + j // 2]:
+                nc.vector.memset(t[:, 0, LONG0 - w : LONG0 - w + 32], FILL)
 
         mnear = const.tile([P, 32], F32, name="mnear")
         mfar = const.tile([P, 32], F32, name="mfar")
@@ -124,21 +135,25 @@ def tile_modelnew_t_kernel(tc, Q, K, V, out):
         for ti in range(NT):
             p_zero(ti)
 
-        zt = const.tile([P, HKV - 2, P], I32, name="zt")
+        zt = const.tile([P, HKV - 1, P], I32, name="zt")
         nc.vector.memset(zt[:], 0)
         vlo = {}
         vhi = {}
         for b in VORDER:
             vlo[b] = const.tile([P, HKV, P], I32, name="vlo%d" % b, align_bytes=64)
             vhi[b] = const.tile([P, HKV, P], I32, name="vhi%d" % b, align_bytes=64)
-            nc.vector.memset(vlo[b][:, 0:2], 0)
+            nc.vector.memset(vlo[b][:, 0:1], 0)
 
         vg = const.tile([P, HKV, D, 4], BF16, name="vg", align_bytes=64)
         vc = const.tile([P, HKV, P], I32, name="vc", align_bytes=64)
         vs = const.tile([P, HKV, P], U8, name="vs", align_bytes=64)
 
         def v_regroup(k0, k1):
-            nc.vector.tensor_copy(out=vg[:, k0:k1], in_=vn[:, k0:k1].rearrange("p h j d -> p h d j"))
+            for k in range(k0, k1):
+                nc.gpsimd.tensor_scalar(
+                    out=vg[:, k], in0=vn[:, k].rearrange("p j d -> p d j"),
+                    scalar1=1.0, scalar2=0.0, op0=ALU.mult, op1=ALU.add,
+                )
 
         def v_quant(k0, k1):
             nc.vector.quantize_mx(
@@ -148,19 +163,19 @@ def tile_modelnew_t_kernel(tc, Q, K, V, out):
             )
 
         for b in VORDER:
-            nc.sync.dma_start(out=vlo[b][8 * b : P, 2:HKV], in_=zt[8 * b : P])
-            nc.sync.dma_start(out=vhi[b][0 : 8 * b, 2:HKV], in_=zt[0 : 8 * b])
+            nc.sync.dma_start(out=vlo[b][8 * b : P, 1:HKV], in_=zt[8 * b : P])
+            nc.sync.dma_start(out=vhi[b][0 : 8 * b, 1:HKV], in_=zt[0 : 8 * b])
         load_k(3)
         load_q(3, 0, NPB)
 
         def v_variant_dve(b):
-            nc.vector.tensor_copy(out=vlo[b][0 : 8 * b, 0:2], in_=vc[0 : 8 * b, 0:2])
-            nc.vector.tensor_copy(out=vhi[b][:, 0:2], in_=vc[:, 0:2])
-            nc.vector.memset(vhi[b][0 : 8 * b, 0:2], 0)
+            nc.vector.tensor_copy(out=vlo[b][0 : 8 * b, 0:1], in_=vc[0 : 8 * b, 0:1])
+            nc.vector.tensor_copy(out=vhi[b][:, 0:1], in_=vc[:, 0:1])
+            nc.vector.memset(vhi[b][0 : 8 * b, 0:1], 0)
 
         def v_variant_dma(b):
-            nc.sync.dma_start(out=vlo[b][0 : 8 * b, 2:HKV], in_=vc[0 : 8 * b, 2:HKV])
-            nc.sync.dma_start(out=vhi[b][8 * b : P, 2:HKV], in_=vc[8 * b : P, 2:HKV])
+            nc.sync.dma_start(out=vlo[b][0 : 8 * b, 1:HKV], in_=vc[0 : 8 * b, 1:HKV])
+            nc.sync.dma_start(out=vhi[b][8 * b : P, 1:HKV], in_=vc[8 * b : P, 1:HKV])
 
         kts = {}
         qts = {}
@@ -169,39 +184,42 @@ def tile_modelnew_t_kernel(tc, Q, K, V, out):
         def prep_pe(kv, part):
             if kv < 2 and part == 2:
                 ps = psa.tile([P, 8, P], BF16, name="acc", tag="acc")
-            elif kv == 0 and part == 0:
+            elif kv == 0:
                 for h in range(2):
-                    ps = pst.tile([P, 4, P], BF16, name="tp", tag="tp")
+                    if part == 1 and h == 0:
+                        ps = psq.tile([P, 4, P], BF16, name="qps", tag="qps")
+                    elif part == 1:
+                        ps = psa.tile([P, 4, P], BF16, name="acc", tag="acc")
+                    else:
+                        ps = pst.tile([P, 4, P], BF16, name="tp", tag="tp")
                     for n in range(4):
-                        nc.tensor.transpose(ps[:, n, :], qn[kv][:, QORDER[4 * h + n], :], ident[:])
-                    pps[(kv, h - 2)] = ps
+                        nc.tensor.transpose(ps[:, n, :], qn[kv][:, QORDER[8 * part + 4 * h + n], :], ident[:])
+                    pps[(kv, part, h)] = ps
                 return
             else:
                 ps = psq.tile([P, 8, P], BF16, name="qps", tag="qps")
             if part == 2:
                 for t in range(4):
-                    nc.tensor.transpose(ps[:, t, :], kn[kv][:, t, :], ident[:])
+                    nc.tensor.transpose(ps[:, t, :], kn[kv][:, t, :], perm[:])
             else:
                 for n in range(8):
                     nc.tensor.transpose(ps[:, n, :], qn[kv][:, QORDER[8 * part + n], :], ident[:])
             pps[(kv, part)] = ps
 
         def prep_copy(kv, part):
-            if kv == 0 and part == 0:
-                qts[kv] = qtp.tile([P, NPB, P], BF16, name="qt", tag="qt")
-                nc.scalar.copy(out=qts[kv][:, 0:4, :], in_=pps[(kv, -2)][:])
-                nc.vector.tensor_copy(out=qts[kv][:, 4:8, :], in_=pps[(kv, -1)][:])
+            if kv == 0 and part < 2:
+                if part == 0:
+                    qts[kv] = qtp.tile([P, NPB, P], BF16, name="qt", tag="qt")
+                b = 8 * part
+                nc.scalar.copy(out=qts[kv][:, b : b + 4, :], in_=pps[(kv, part, 0)][:])
+                nc.vector.tensor_copy(out=qts[kv][:, b + 4 : b + 8, :], in_=pps[(kv, part, 1)][:])
                 return
             ps = pps[(kv, part)]
             if part == 2:
-                kts[kv] = qtp.tile([P, 16, 2, 8, 2], BF16, name="kt", tag="kt")
-                for u in range(2):
-                    nc.vector.tensor_copy(
-                        out=kts[kv][:, :, u, :, :],
-                        in_=ps[:, 2 * u : 2 * u + 2, :].rearrange("p e (b c) -> p b c e", c=8),
-                    )
+                kts[kv] = qtp.tile([P, 4, P], BF16, name="kt", tag="kt")
+                nc.vector.tensor_copy(out=kts[kv][:], in_=ps[:, 0:4, :])
             else:
-                if part == 0:
+                if kv not in qts:
                     qts[kv] = qtp.tile([P, NPB, P], BF16, name="qt", tag="qt")
                 o = qts[kv][:, 8 * part : 8 * part + 8, :]
                 nc.vector.tensor_copy(out=o, in_=ps[:])
@@ -210,6 +228,10 @@ def tile_modelnew_t_kernel(tc, Q, K, V, out):
         st = {}
         halves = {}
         oall = {}
+
+        def group(g):
+            kv, n = divmod(g, NGR)
+            return kv, (n + 2) % NGR if kv == HKV - 1 else n
 
         def ok(g):
             return 0 <= g < NG
@@ -221,9 +243,9 @@ def tile_modelnew_t_kernel(tc, Q, K, V, out):
             return s if kind == 0 else (2 + s if j < 3 else 3 - s)
 
         def s_qk(g):
-            kv, j = divmod(g, NGR)
+            kv, j = group(g)
             st[g] = {"raw": []}
-            kt = kts[kv][:].rearrange("p b u c e -> p (b u c e)")
+            kt = kts[kv][:].rearrange("p n w -> p (n w)")
 
             def mm(dst, pb, nblk):
                 w0 = 32 * (pb + 1 - nblk)
@@ -250,33 +272,33 @@ def tile_modelnew_t_kernel(tc, Q, K, V, out):
                     st[g]["raw"].append((raw, LONG, s, LONG0))
 
         def s_tanh(g):
-            kv, j = divmod(g, NGR)
+            kv, j = group(g)
             for raw, w, s, c0 in st[g]["raw"]:
                 nc.scalar.activation(
-                    out=th[j][:, s, c0 : c0 + w], in_=raw[:, 0:w], func=AF.Tanh, scale=SCALE / SOFTCAP
+                    out=th[(kv == HKV - 1, j)][:, s, c0 : c0 + w], in_=raw[:, 0:w], func=AF.Tanh, scale=SCALE / SOFTCAP
                 )
 
         def s_mask(g):
-            j = g % NGR
+            kv, j = group(g)
             for c0, w in ((NEAR0, 64), (LONG0 + LONG - 32, 32)):
-                v = th[j][:, :, c0 : c0 + w]
+                v = th[(kv == HKV - 1, j)][:, :, c0 : c0 + w]
                 (nc.gpsimd if MASK_ENG == "gpsimd" else nc.vector).tensor_tensor(
                     out=v, in0=v, in1=mk[:, 0:w].unsqueeze(1).to_broadcast([P, 2, w]), op=ALU.add
                 )
 
         def s_max_long(g):
-            j = g % NGR
+            kv, j = group(g)
             mx = small.tile([P, 4], F32, name="mx", tag="mx")
             st[g]["mx"] = mx
             nc.vector.tensor_reduce(
-                out=mx[:, 2:4], in_=th[j][:, :, LONG0 : LONG0 + LONG], axis=AX.X, op=ALU.max
+                out=mx[:, 2:4], in_=th[(kv == HKV - 1, j)][:, :, LONG0 : LONG0 + LONG], axis=AX.X, op=ALU.max
             )
 
         def s_max_short(g):
-            j = g % NGR
+            kv, j = group(g)
             w = 64 * (j + 1)
             nc.vector.tensor_reduce(
-                out=st[g]["mx"][:, 0:2], in_=th[j][:, :, LONG0 - w : LONG0], axis=AX.X, op=ALU.max
+                out=st[g]["mx"][:, 0:2], in_=th[(kv == HKV - 1, j)][:, :, LONG0 - w : LONG0], axis=AX.X, op=ALU.max
             )
 
         def s_nb(g):
@@ -287,7 +309,7 @@ def tile_modelnew_t_kernel(tc, Q, K, V, out):
             st[g]["nb"] = nb
 
         def s_exp(g):
-            kv, j = divmod(g, NGR)
+            kv, j = group(g)
             h = g // 2
             if h not in halves:
                 halves[h] = {"ls": small.tile([P, 8], F32, name="ls", tag="ls")}
@@ -306,7 +328,7 @@ def tile_modelnew_t_kernel(tc, Q, K, V, out):
                     col = 4 * (g % 2) + place(j, kind, s)
                     nc.scalar.activation(
                         out=pt[kv % 2][ti][:, :, 8 * blk0 : 8 * (blk0 + nblk), :].rearrange("p u (b c) e -> p u b (c e)", c=8),
-                        in_=th[j][:, s, c0 : c0 + 32 * nblk].rearrange("p (b u x) -> p u b x", u=2, x=16),
+                        in_=th[(kv == HKV - 1, j)][:, s, c0 : c0 + 32 * nblk].rearrange("p (b u x) -> p u b x", u=2, x=16),
                         func=AF.Exp,
                         bias=nb[:, u : u + 1],
                         scale=SOFTCAP,
@@ -328,7 +350,7 @@ def tile_modelnew_t_kernel(tc, Q, K, V, out):
             nc.vector.reciprocal(out=h["rl"][:], in_=h["le"][:])
 
         def tiles_of(g):
-            j = g % NGR
+            kv, j = group(g)
             return ((2 * j, 2 * j + 1),) if j < 3 else ((6, 7), (8,))
 
         def s_tr(g):
@@ -345,7 +367,7 @@ def tile_modelnew_t_kernel(tc, Q, K, V, out):
             st[g]["gt"] = []
             for n, (tp, m) in enumerate(st[g]["tp"]):
                 gt = gp.tile([P, 2, P, 4], BF16, name="gt", tag="gt", align_bytes=64)
-                nc.scalar.copy(
+                (nc.vector.tensor_copy if (g, n) in EVAC_V or (group(g)[1], n) in EVAC_V else nc.scalar.copy)(
                     out=gt[:, 0:m].rearrange("p n r t -> p (n r t)").bitcast(F32).rearrange("p (n r u) -> p n r u", n=m, u=2),
                     in_=tp[:, 0:m].rearrange("p n u r -> p n r u"),
                 )
@@ -364,7 +386,7 @@ def tile_modelnew_t_kernel(tc, Q, K, V, out):
                 st[g]["q"].append((cd, sc))
 
         def s_mx(g):
-            kv, j = divmod(g, NGR)
+            kv, j = group(g)
             acc = psa.tile([P, 4, D], F32, name="acc", tag="acc")
             st[g]["acc"] = acc
             for s in range(2):
@@ -386,26 +408,21 @@ def tile_modelnew_t_kernel(tc, Q, K, V, out):
                         stop=True,
                     )
 
+        def store(kv, b0, b1, o):
+            for q in range(G):
+                nc.sync.dma_start(
+                    out=out[0, G * kv + q].rearrange("(b i) d -> i b d", i=NB)[:, b0:b1, :], in_=o[q:P:G]
+                )
+
         def s_norm(g):
-            kv, j = divmod(g, NGR)
+            kv, j = group(g)
             rl = halves[g // 2]["rl"][:, 4 * (g % 2) : 4 * (g % 2) + 4]
             acc = st[g]["acc"]
-            if kv == HKV - 1:
-                o = op.tile([P, 4, D], F32, name="olast%d" % j, bufs=1)
-                nc.vector.tensor_tensor(
-                    out=o[:], in0=acc[:], in1=rl.unsqueeze(2).to_broadcast([P, 4, D]), op=ALU.mult
-                )
-                spans = ((2 * j, 0, 2), (2 * j + 9, 2, 2)) if j < 3 else ((6, 0, 3), (15, 3, 1))
-                for b0, u, m in spans:
-                    for q in range(G):
-                        nc.sync.dma_start(
-                            out=out[0, G * kv + q].rearrange("(b i) d -> i b d", i=NB)[:, b0 : b0 + m, :],
-                            in_=o[q:P:G, u : u + m, :],
-                        )
-                return
-            if kv not in oall:
-                oall[kv] = op.tile([P, 22, D], F32, name="oall", tag="oall")
-            o = oall[kv]
+            last = kv == HKV - 1
+            ko = (kv, last and j < 2)
+            if ko not in oall:
+                oall[ko] = op.tile([P, 22, D], F32, name="oall", tag="oall")
+            o = oall[ko]
             if j < 3:
                 a = 2 * j
                 nc.vector.tensor_tensor(
@@ -424,51 +441,59 @@ def tile_modelnew_t_kernel(tc, Q, K, V, out):
                         in1=rl[:, u : u + m].unsqueeze(2).to_broadcast([P, m, D]),
                         op=ALU.mult,
                     )
-            if j == 3:
-                for q in range(G):
-                    nc.sync.dma_start(
-                        out=out[0, G * kv + q].rearrange("(b i) d -> i b d", i=NB), in_=o[q:P:G, 0:NPB, :]
-                    )
+            if last:
+                if j == 3:
+                    store(kv, 4, 9, o[:, 4:9])
+                    store(kv, 13, NPB, o[:, 13:NPB])
+                elif j == 1:
+                    store(kv, 0, 4, o[:, 0:4])
+                    store(kv, 9, 13, o[:, 9:13])
+            elif j == 3:
+                store(kv, 0, NPB, o[:, 0:NPB])
 
-        prep = {1: [(1, 0)], 2: [(1, 1), (1, 2)]}
+        prep = {0: [(0, 1)], 1: [(1, 0)], 2: [(1, 1), (1, 2)]}
         for kv in range(2, HKV):
             for part in range(3):
-                prep[NGR * (kv - 1) + part] = [(kv, part)]
+                prep[NGR * (kv - 1) + part] = [(kv, (1 - part if kv == HKV - 1 and part < 2 else part))]
 
         extra = {}
 
         def at(i, f):
             extra.setdefault(i, []).append(f)
 
-        at(1, lambda: v_regroup(0, 2))
-        at(2, lambda: v_quant(0, 2))
+        for k0, k1 in ((0, 1), (1, 2), (2, 4), (4, 6), (6, 8)):
+            at(V_AT[k0], lambda k0=k0, k1=k1: v_regroup(k0, k1))
+            at(V_AT[k0] + 1, lambda k0=k0, k1=k1: v_quant(k0, k1))
         for b in VORDER:
             at((b + 1) // 2 + 2, lambda b=b: v_variant_dve(b))
-        at(4, lambda: v_regroup(2, 4))
-        at(5, lambda: v_quant(2, 4))
-        at(5, lambda: v_regroup(4, HKV))
-        at(6, lambda: v_quant(4, HKV))
-        for b in VORDER:
-            at(6, lambda b=b: v_variant_dma(b))
+            at(V_AT[6] + 1, lambda b=b: v_variant_dma(b))
         for kv in range(4, HKV):
-            at(6, lambda kv=kv: load_k(kv))
-            at(6, lambda kv=kv: load_q(kv, 0, NPB))
+            at(V_AT[6] + 1, lambda kv=kv: load_k(kv))
+            at(V_AT[6] + 1, lambda kv=kv: load_q(kv, 0, NPB))
 
         prep_pe(0, 2)
         prep_pe(0, 0)
         prep_copy(0, 2)
         prep_copy(0, 0)
         s_qk(0)
-        prep_pe(0, 1)
-        prep_copy(0, 1)
+        def exps(g):
+            if ok(g):
+                s_exp(g)
+                s_rl_add(g)
+                s_tr(g)
+
         for i in range(NG + L_NORM + 1):
             kv, j = divmod(i, NGR)
             if ok(i):
                 s_tanh(i)
             if ok(i - L_MASK):
                 s_mask(i - L_MASK)
+            for a in prep.get(i - 1, []):
+                prep_copy(*a)
             if ok(i + 1):
                 s_qk(i + 1)
+            if i >= NG:
+                exps(i - L_EXP)
             if ok(i - L_EVAC):
                 s_evac(i - L_EVAC)
             if ok(i - L_QUANT):
@@ -479,17 +504,13 @@ def tile_modelnew_t_kernel(tc, Q, K, V, out):
                 s_max_short(i - L_MAX)
             if ok(i - L_EXP - 1):
                 s_rl(i - L_EXP - 1)
-            if ok(i - L_MAX):
-                s_nb(i - L_MAX)
             for a in prep.get(i, []):
                 prep_pe(*a)
-            if ok(i - L_EXP):
-                s_exp(i - L_EXP)
-                s_rl_add(i - L_EXP)
-                s_tr(i - L_EXP)
+            if i < NG:
+                exps(i - L_EXP)
             if ok(i - L_NORM):
                 s_norm(i - L_NORM)
-            for a in prep.get(i, []):
-                prep_copy(*a)
+            if ok(i - L_MAX):
+                s_nb(i - L_MAX)
             for f in extra.get(i, []):
                 f()

@@ -80,8 +80,21 @@ def tile_modelnew_t_kernel(tc, Q, K, V, out):
         load_q(1, 0, NPB)
         load_v(1, 4)
         load_v(4, HKV)
-        load_k(2)
-        load_q(2, 0, NPB)
+        for kv in range(2, HKV):
+            load_k(kv)
+            load_q(kv, 0, NPB)
+
+        vlo = {}
+        vhi = {}
+        for b in VORDER:
+            vlo[b] = const.tile([P, HKV, P], I32, name="vlo%d" % b, align_bytes=64)
+            vhi[b] = const.tile([P, HKV, P], I32, name="vhi%d" % b, align_bytes=64)
+
+        def v_zero(eng, t, k0):
+            eng.memset(t[:, k0:HKV], 0)
+
+        for b in (1, 2, 3):
+            v_zero(nc.vector, vlo[b], 0)
 
         ident = const.tile([P, P], BF16, name="ident")
         make_identity(nc, ident[:])
@@ -134,15 +147,9 @@ def tile_modelnew_t_kernel(tc, Q, K, V, out):
 
         for ti in range(NT):
             p_zero(ti)
-
-        zt = const.tile([P, HKV - 1, P], I32, name="zt")
-        nc.vector.memset(zt[:], 0)
-        vlo = {}
-        vhi = {}
-        for b in VORDER:
-            vlo[b] = const.tile([P, HKV, P], I32, name="vlo%d" % b, align_bytes=64)
-            vhi[b] = const.tile([P, HKV, P], I32, name="vhi%d" % b, align_bytes=64)
-            nc.vector.memset(vlo[b][:, 0:1], 0)
+        v_zero(nc.vector, vlo[4], 0)
+        for b in (1, 2):
+            v_zero(nc.gpsimd, vhi[b], 2)
 
         vg = const.tile([P, HKV, D, 4], BF16, name="vg", align_bytes=64)
         vc = const.tile([P, HKV, P], I32, name="vc", align_bytes=64)
@@ -162,20 +169,14 @@ def tile_modelnew_t_kernel(tc, Q, K, V, out):
                 in_=vg[:, k0:k1].rearrange("p h d j -> p (h d j)"),
             )
 
-        for b in VORDER:
-            nc.sync.dma_start(out=vlo[b][8 * b : P, 1:HKV], in_=zt[8 * b : P])
-            nc.sync.dma_start(out=vhi[b][0 : 8 * b, 1:HKV], in_=zt[0 : 8 * b])
-        load_k(3)
-        load_q(3, 0, NPB)
-
         def v_variant_dve(b):
-            nc.vector.tensor_copy(out=vlo[b][0 : 8 * b, 0:1], in_=vc[0 : 8 * b, 0:1])
-            nc.vector.tensor_copy(out=vhi[b][:, 0:1], in_=vc[:, 0:1])
-            nc.vector.memset(vhi[b][0 : 8 * b, 0:1], 0)
+            nc.vector.tensor_copy(out=vlo[b][0 : 8 * b, 0:2], in_=vc[0 : 8 * b, 0:2])
+            nc.vector.tensor_copy(out=vhi[b][:, 0:2], in_=vc[:, 0:2])
+            nc.vector.memset(vhi[b][0 : 8 * b, 0:2], 0)
 
         def v_variant_dma(b):
-            nc.sync.dma_start(out=vlo[b][0 : 8 * b, 1:HKV], in_=vc[0 : 8 * b, 1:HKV])
-            nc.sync.dma_start(out=vhi[b][8 * b : P, 1:HKV], in_=vc[8 * b : P, 1:HKV])
+            nc.sync.dma_start(out=vlo[b][0 : 8 * b, 2:HKV], in_=vc[0 : 8 * b, 2:HKV])
+            nc.sync.dma_start(out=vhi[b][8 * b : P, 2:HKV], in_=vc[8 * b : P, 2:HKV])
 
         kts = {}
         qts = {}
@@ -464,13 +465,13 @@ def tile_modelnew_t_kernel(tc, Q, K, V, out):
         for k0, k1 in ((0, 1), (1, 2), (2, 4), (4, 6), (6, 8)):
             at(V_AT[k0], lambda k0=k0, k1=k1: v_regroup(k0, k1))
             at(V_AT[k0] + 1, lambda k0=k0, k1=k1: v_quant(k0, k1))
+        for i, b in ((1, 5), (2, 6), (3, 7)):
+            at(i, lambda b=b: v_zero(nc.vector, vlo[b], 0))
+        for i, b in ((0, 3), (5, 4), (5, 5), (6, 6), (6, 7)):
+            at(i, lambda b=b: v_zero(nc.gpsimd, vhi[b], 2))
         for b in VORDER:
             at((b + 1) // 2 + 2, lambda b=b: v_variant_dve(b))
-            at(V_AT[6] + 1, lambda b=b: v_variant_dma(b))
-        for kv in range(4, HKV):
-            at(V_AT[6] + 1, lambda kv=kv: load_k(kv))
-            at(V_AT[6] + 1, lambda kv=kv: load_q(kv, 0, NPB))
-
+            at(7, lambda b=b: v_variant_dma(b))
         prep_pe(0, 2)
         prep_pe(0, 0)
         prep_copy(0, 2)
@@ -498,7 +499,6 @@ def tile_modelnew_t_kernel(tc, Q, K, V, out):
                 s_evac(i - L_EVAC)
             if ok(i - L_QUANT):
                 s_quant(i - L_QUANT)
-                s_mx(i - L_QUANT)
             if ok(i - L_MAX):
                 s_max_long(i - L_MAX)
                 s_max_short(i - L_MAX)
@@ -508,6 +508,8 @@ def tile_modelnew_t_kernel(tc, Q, K, V, out):
                 prep_pe(*a)
             if i < NG:
                 exps(i - L_EXP)
+            if ok(i - L_QUANT):
+                s_mx(i - L_QUANT)
             if ok(i - L_NORM):
                 s_norm(i - L_NORM)
             if ok(i - L_MAX):

@@ -36,8 +36,10 @@ VORDER = (1, 2, 3, 4, 5, 6, 7)
 L_MASK, L_MAX, L_EXP, L_EVAC, L_QUANT, L_NORM = 0, 1, 2, 3, 4, 5
 MASK_ENG = "gpsimd"
 NFILL = 1
-V_AT = {0: 1, 1: 1, 2: 2, 4: 3, 6: 4}
-EVAC_V = ()
+V_AT = {0: 1, 1: 2, 2: 3, 4: 4, 6: 5}
+EVAC_V = ((2, 0),)
+NB_POOL = True
+DEL0, DELN = 3, 8
 
 
 def tile_modelnew_t_kernel(tc, Q, K, V, out):
@@ -46,7 +48,7 @@ def tile_modelnew_t_kernel(tc, Q, K, V, out):
         ctx.enter_context(tc.manual_schedule())
         const = ctx.enter_context(tc.tile_pool(name="const", bufs=1))
         qtp = ctx.enter_context(tc.tile_pool(name="qtp", bufs=2))
-        gp = ctx.enter_context(tc.tile_pool(name="gp", bufs=4))
+        gp = ctx.enter_context(tc.tile_pool(name="gp", bufs=7))
         small = ctx.enter_context(tc.tile_pool(name="small", bufs=6))
         op = ctx.enter_context(tc.tile_pool(name="op", bufs=3))
         psq = ctx.enter_context(tc.psum_pool(name="psq", bufs=1))
@@ -90,8 +92,8 @@ def tile_modelnew_t_kernel(tc, Q, K, V, out):
             vlo[b] = const.tile([P, HKV, P], I32, name="vlo%d" % b, align_bytes=64)
             vhi[b] = const.tile([P, HKV, P], I32, name="vhi%d" % b, align_bytes=64)
 
-        def v_zero(eng, t, k0):
-            eng.memset(t[:, k0:HKV], 0)
+        def v_zero(eng, t, k0, k1=HKV):
+            eng.memset(t[:, k0:k1], 0)
 
         for b in (1, 2, 3):
             v_zero(nc.vector, vlo[b], 0)
@@ -148,6 +150,8 @@ def tile_modelnew_t_kernel(tc, Q, K, V, out):
         for ti in range(NT):
             p_zero(ti)
         v_zero(nc.vector, vlo[4], 0)
+        for b in (5, 6, 7):
+            v_zero(nc.vector, vlo[b], 0, 2)
         for b in (1, 2):
             v_zero(nc.gpsimd, vhi[b], 2)
 
@@ -304,9 +308,14 @@ def tile_modelnew_t_kernel(tc, Q, K, V, out):
 
         def s_nb(g):
             nb = small.tile([P, 4], F32, name="nb", tag="nb")
-            nc.vector.tensor_scalar(
-                out=nb[:], in0=st[g]["mx"][:], scalar1=-SOFTCAP, scalar2=None, op0=ALU.mult
-            )
+            if NB_POOL:
+                nc.gpsimd.tensor_scalar(
+                    out=nb[:], in0=st[g]["mx"][:], scalar1=-SOFTCAP, scalar2=0.0, op0=ALU.mult, op1=ALU.add
+                )
+            else:
+                nc.vector.tensor_scalar(
+                    out=nb[:], in0=st[g]["mx"][:], scalar1=-SOFTCAP, scalar2=None, op0=ALU.mult
+                )
             st[g]["nb"] = nb
 
         def s_exp(g):
@@ -365,18 +374,20 @@ def tile_modelnew_t_kernel(tc, Q, K, V, out):
                 st[g]["tp"].append((tp, len(tis)))
 
         def s_evac(g):
-            st[g]["gt"] = []
-            for n, (tp, m) in enumerate(st[g]["tp"]):
+            st[g]["gt"] = {}
+            for n in range(len(st[g]["tp"])):
+                tp, m = st[g]["tp"][n]
                 gt = gp.tile([P, 2, P, 4], BF16, name="gt", tag="gt", align_bytes=64)
                 (nc.vector.tensor_copy if (g, n) in EVAC_V or (group(g)[1], n) in EVAC_V else nc.scalar.copy)(
                     out=gt[:, 0:m].rearrange("p n r t -> p (n r t)").bitcast(F32).rearrange("p (n r u) -> p n r u", n=m, u=2),
                     in_=tp[:, 0:m].rearrange("p n u r -> p n r u"),
                 )
-                st[g]["gt"].append((gt, m))
+                st[g]["gt"][n] = (gt, m)
 
         def s_quant(g):
             st[g]["q"] = []
-            for gt, m in st[g]["gt"]:
+            for n in range(len(st[g]["gt"])):
+                gt, m = st[g]["gt"][n]
                 cd = gp.tile([P, 2, P], I32, name="cd", tag="cd", align_bytes=64)
                 sc = gp.tile([P, 2, P], U8, name="sc", tag="sc", align_bytes=64)
                 nc.vector.quantize_mx(
@@ -420,7 +431,7 @@ def tile_modelnew_t_kernel(tc, Q, K, V, out):
             rl = halves[g // 2]["rl"][:, 4 * (g % 2) : 4 * (g % 2) + 4]
             acc = st[g]["acc"]
             last = kv == HKV - 1
-            ko = (kv, last and j < 2)
+            ko = (kv, kv >= HKV - 2 and j < 2)
             if ko not in oall:
                 oall[ko] = op.tile([P, 22, D], F32, name="oall", tag="oall")
             o = oall[ko]
@@ -449,6 +460,13 @@ def tile_modelnew_t_kernel(tc, Q, K, V, out):
                 elif j == 1:
                     store(kv, 0, 4, o[:, 0:4])
                     store(kv, 9, 13, o[:, 9:13])
+            elif kv == HKV - 2:
+                if j == 1:
+                    store(kv, 0, 4, o[:, 0:4])
+                    store(kv, 9, 13, o[:, 9:13])
+                elif j == 3:
+                    store(kv, 4, 9, o[:, 4:9])
+                    store(kv, 13, NPB, o[:, 13:NPB])
             elif j == 3:
                 store(kv, 0, NPB, o[:, 0:NPB])
 
@@ -457,6 +475,8 @@ def tile_modelnew_t_kernel(tc, Q, K, V, out):
             for part in range(3):
                 prep[NGR * (kv - 1) + part] = [(kv, (1 - part if kv == HKV - 1 and part < 2 else part))]
 
+        ZEROS = ((0, vhi[3]), (1, vhi[4]), (2, vlo[5]), (6, vhi[5]), (6, vlo[6]), (7, vhi[6]), (7, vlo[7]), (8, vhi[7]))
+        VDMA = {1: 6, 2: 6, 3: 6, 4: 6, 5: 7, 6: 8, 7: 9}
         extra = {}
 
         def at(i, f):
@@ -465,13 +485,11 @@ def tile_modelnew_t_kernel(tc, Q, K, V, out):
         for k0, k1 in ((0, 1), (1, 2), (2, 4), (4, 6), (6, 8)):
             at(V_AT[k0], lambda k0=k0, k1=k1: v_regroup(k0, k1))
             at(V_AT[k0] + 1, lambda k0=k0, k1=k1: v_quant(k0, k1))
-        for i, b in ((1, 5), (2, 6), (3, 7)):
-            at(i, lambda b=b: v_zero(nc.vector, vlo[b], 0))
-        for i, b in ((0, 3), (5, 4), (5, 5), (6, 6), (6, 7)):
-            at(i, lambda b=b: v_zero(nc.gpsimd, vhi[b], 2))
+        for i, t in ZEROS:
+            at(i, lambda t=t: v_zero(nc.gpsimd, t, 2))
         for b in VORDER:
-            at((b + 1) // 2 + 2, lambda b=b: v_variant_dve(b))
-            at(7, lambda b=b: v_variant_dma(b))
+            at((b + 1) // 2 + 2 + DEL0, lambda b=b: v_variant_dve(b))
+            at(VDMA[b], lambda b=b: v_variant_dma(b))
         prep_pe(0, 2)
         prep_pe(0, 0)
         prep_copy(0, 2)
@@ -483,22 +501,22 @@ def tile_modelnew_t_kernel(tc, Q, K, V, out):
                 s_rl_add(g)
                 s_tr(g)
 
-        for i in range(NG + L_NORM + 1):
-            kv, j = divmod(i, NGR)
-            if ok(i):
-                s_tanh(i)
+        mx_at = {}
+        for g in range(NG):
+            mx_at.setdefault(g + L_QUANT + max(0, DEL0 - g // DELN), []).append(g)
+
+        for i in range(NG):
+            s_tanh(i)
             if ok(i - L_MASK):
                 s_mask(i - L_MASK)
             for a in prep.get(i - 1, []):
                 prep_copy(*a)
             if ok(i + 1):
                 s_qk(i + 1)
-            if i >= NG:
-                exps(i - L_EXP)
             if ok(i - L_EVAC):
                 s_evac(i - L_EVAC)
-            if ok(i - L_QUANT):
-                s_quant(i - L_QUANT)
+            for g in mx_at.get(i, []):
+                s_quant(g)
             if ok(i - L_MAX):
                 s_max_long(i - L_MAX)
                 s_max_short(i - L_MAX)
@@ -506,13 +524,30 @@ def tile_modelnew_t_kernel(tc, Q, K, V, out):
                 s_rl(i - L_EXP - 1)
             for a in prep.get(i, []):
                 prep_pe(*a)
-            if i < NG:
-                exps(i - L_EXP)
-            if ok(i - L_QUANT):
-                s_mx(i - L_QUANT)
-            if ok(i - L_NORM):
-                s_norm(i - L_NORM)
+            exps(i - L_EXP)
+            for g in mx_at.get(i, []):
+                s_mx(g)
+            for g in mx_at.get(i - 1, []):
+                s_norm(g)
             if ok(i - L_MAX):
                 s_nb(i - L_MAX)
             for f in extra.get(i, []):
                 f()
+        z = NG - 1
+        s_max_long(z)
+        s_max_short(z)
+        s_nb(z)
+        for n in range(4):
+            q = z - 3 + n
+            if n < 2:
+                exps(z - 1 + n)
+            if n < 3:
+                s_evac(z - 2 + n)
+            if n == 0:
+                s_rl(z - 2)
+            if n == 2:
+                s_rl(z)
+            s_quant(q)
+            s_mx(q)
+            s_norm(q - 1)
+        s_norm(z)

@@ -25,21 +25,25 @@ FILL = -1.0e4
 FLOPS = 2 * 2 * HQ * 98688 * D
 
 NGR = 4
-NT = 9
-NEAR0 = 224
-LONG0 = 256
-SLOT = 544
+NT = 8
 LONG = 288
-QORDER = (0, 1, 9, 10, 2, 3, 11, 12, 4, 5, 13, 14, 6, 7, 8, 15)
+TILES = ((0, 1), (2, 3), (4, 6), (5, 7))
+QORDER = (0, 1, 9, 10, 2, 3, 11, 12, 4, 6, 13, 15, 5, 7, 14, 8)
 QPOS = {b: n for n, b in enumerate(QORDER)}
-VORDER = (1, 2, 3, 4, 5, 6, 7)
 L_MASK, L_MAX, L_EXP, L_EVAC, L_QUANT, L_NORM = 0, 1, 2, 3, 4, 5
 MASK_ENG = "gpsimd"
 NFILL = 1
-V_AT = {0: 1, 1: 2, 2: 3, 4: 4, 6: 5}
-EVAC_V = ((2, 0),)
+V_AT = (0, 1, 2, 3, 4, 5, 6, 7)
+EVAC_V = {0: (0, 1, 2, 3), 1: (2,), 2: (2,), 3: (2,), 4: (2,), 5: (2,), 6: (2,), 7: (2,)}
 NB_POOL = True
 DEL0, DELN = 3, 8
+LAST = (2, 3, 1, 0)
+HI = (0, 1, 2, 3, 5, 6, 4)
+LO_COPY = ((0, 4, slice(3, 8)), (0, 2, slice(1, 3)), (4, 8, slice(7, 8)), (4, 6, slice(5, 7))) + tuple(
+    (n, n + 1, slice(n, n + 1)) for n in (0, 2, 4, 6)
+)
+HI_COPY = ((8, 12, slice(0, 7)), (12, 16, slice(0, 6)), (12, 14, slice(6, 7)), (14, 15, slice(6, 7)), (4, 8, slice(0, 4)),
+           (6, 8, slice(5, 7)), (2, 4, slice(0, 2))) + tuple((n + 1, n + 2, slice(HI[n], HI[n] + 1)) for n in (0, 2, 4, 6))
 
 
 def tile_modelnew_t_kernel(tc, Q, K, V, out):
@@ -70,33 +74,44 @@ def tile_modelnew_t_kernel(tc, Q, K, V, out):
                     in_=Q[0, G * kv + g].rearrange("(b i) d -> i b d", i=NB)[:, b0:b1, :],
                 )
 
-        def load_v(k0, k1):
-            nc.sync.dma_start(out=vn[:, k0:k1], in_=V[0, k0:k1].rearrange("h (p j) d -> p h j d", j=4))
-
-        load_k(0, nc.gpsimd)
-        load_q(0, 0, 4)
-        load_q(0, 9, NPB)
-        load_q(0, 4, 9)
-        load_v(0, 1)
-        load_k(1)
-        load_q(1, 0, NPB)
-        load_v(1, 4)
-        load_v(4, HKV)
-        for kv in range(2, HKV):
+        def load_head(kv):
             load_k(kv)
             load_q(kv, 0, NPB)
 
-        vlo = {}
-        vhi = {}
-        for b in VORDER:
-            vlo[b] = const.tile([P, HKV, P], I32, name="vlo%d" % b, align_bytes=64)
-            vhi[b] = const.tile([P, HKV, P], I32, name="vhi%d" % b, align_bytes=64)
+        def load_v(k0, k1):
+            nc.sync.dma_start(out=vn[:, k0:k1], in_=V[0, k0:k1].rearrange("h (p j) d -> p h j d", j=4))
 
-        def v_zero(eng, t, k0, k1=HKV):
-            eng.memset(t[:, k0:k1], 0)
+        load_k(0, nc.scalar)
+        load_q(0, 0, 4)
+        load_q(0, 9, NPB)
+        load_q(0, 4, 9)
+        load_v(0, 2)
+        load_k(1)
+        load_q(1, 0, NPB)
+        load_k(2)
+        load_q(2, 0, NPB)
+        load_v(2, HKV)
+        load_k(3)
+        load_q(3, 0, NPB)
 
-        for b in (1, 2, 3):
-            v_zero(nc.vector, vlo[b], 0)
+        vg = const.tile([P, HKV, D, 4], BF16, name="vg", align_bytes=64)
+        vc = const.tile([P, HKV, P], I32, name="vc", align_bytes=64)
+        vs = const.tile([P, HKV, P], U8, name="vs", align_bytes=64)
+        vsh = const.tile([P, HKV, P], I32, name="vsh", align_bytes=64)
+        vx = const.tile([P, HKV, P], I32, name="vx", align_bytes=64)
+        var = []
+        for part, nh in enumerate((2, HKV - 2)):
+            slo = const.tile([P, 8, nh, P], U8, name="slo%d" % part, align_bytes=64)
+            shi = const.tile([P, 7, nh, P], U8, name="shi%d" % part, align_bytes=64)
+            ssh = const.tile([P, 1, nh, P], U8, name="ssh%d" % part, align_bytes=64)
+            sx = const.tile([P, 1, nh, P], U8, name="sx%d" % part, align_bytes=64)
+            var.append((slo, shi, ssh, sx))
+
+        def s_zero(eng, t):
+            eng.memset(t[:].rearrange("p n h d -> p (n h d)").bitcast(I32), 0)
+
+        for t in var[0]:
+            s_zero(nc.vector, t)
 
         ident = const.tile([P, P], BF16, name="ident")
         make_identity(nc, ident[:])
@@ -110,12 +125,16 @@ def tile_modelnew_t_kernel(tc, Q, K, V, out):
         nc.gpsimd.tensor_copy(out=identf[:], in_=ident[:])
 
         th = {}
-        for j in range(NGR):
-            th[(False, j)] = const.tile([P, 2, SLOT], F32, name="th%d" % j)
-            th[(True, j)] = const.tile([P, 2, SLOT], F32, name="thl%d" % j) if j > 1 else th[(False, j)]
-            w = 64 * (j + 1)
+        for j, (a, b) in enumerate(TILES):
+            w = 32 * (b + 1)
+            th[(False, j)] = const.tile([P, 2, w + LONG], F32, name="th%d" % j)
+            th[(True, j)] = const.tile([P, 2, w + LONG], F32, name="thl%d" % j) if j > 1 else th[(False, j)]
             for t in (th[(False, j)], th[(True, j)])[0 : 1 + j // 2]:
-                nc.vector.memset(t[:, 0, LONG0 - w : LONG0 - w + 32], FILL)
+                nc.vector.memset(t[:, 0, 0 : 32 * (b - a)], FILL)
+
+        nc.vector.memset(vx[:].rearrange("p h d -> p (h d)"), 0)
+        nc.vector.memset(vsh[0:64].rearrange("p h d -> p (h d)"), 0)
+        s_zero(nc.vector, var[1][0])
 
         mnear = const.tile([P, 32], F32, name="mnear")
         mfar = const.tile([P, 32], F32, name="mfar")
@@ -142,22 +161,11 @@ def tile_modelnew_t_kernel(tc, Q, K, V, out):
             return t[:].rearrange("p u w e -> p (u w e)").bitcast(F32)
 
         def p_zero(ti):
-            b = ti + 10 if ti < 7 else ti + 1
+            b = ti + 10
             for st in range(2):
-                if b < NPB:
+                if ti < 5:
                     nc.vector.memset(pt[st][ti][:, :, 8 * b : P, :].rearrange("p u w e -> p u (w e)").bitcast(I32), 0)
 
-        for ti in range(NT):
-            p_zero(ti)
-        v_zero(nc.vector, vlo[4], 0)
-        for b in (5, 6, 7):
-            v_zero(nc.vector, vlo[b], 0, 2)
-        for b in (1, 2):
-            v_zero(nc.gpsimd, vhi[b], 2)
-
-        vg = const.tile([P, HKV, D, 4], BF16, name="vg", align_bytes=64)
-        vc = const.tile([P, HKV, P], I32, name="vc", align_bytes=64)
-        vs = const.tile([P, HKV, P], U8, name="vs", align_bytes=64)
 
         def v_regroup(k0, k1):
             for k in range(k0, k1):
@@ -173,14 +181,23 @@ def tile_modelnew_t_kernel(tc, Q, K, V, out):
                 in_=vg[:, k0:k1].rearrange("p h d j -> p (h d j)"),
             )
 
-        def v_variant_dve(b):
-            nc.vector.tensor_copy(out=vlo[b][0 : 8 * b, 0:2], in_=vc[0 : 8 * b, 0:2])
-            nc.vector.tensor_copy(out=vhi[b][:, 0:2], in_=vc[:, 0:2])
-            nc.vector.memset(vhi[b][0 : 8 * b, 0:2], 0)
-
-        def v_variant_dma(b):
-            nc.sync.dma_start(out=vlo[b][0 : 8 * b, 2:HKV], in_=vc[0 : 8 * b, 2:HKV])
-            nc.sync.dma_start(out=vhi[b][8 * b : P, 2:HKV], in_=vc[8 * b : P, 2:HKV])
+        def v_variants(part):
+            k0, k1 = ((0, 2), (2, HKV))[part]
+            slo, shi, ssh, sx = var[part]
+            nc.sync.dma_start(out=vsh[64:P, k0:k1], in_=vc[0:64, k0:k1])
+            nc.sync.dma_start(out=vx[120:P, k0:k1], in_=vc[64:72, k0:k1])
+            for t, runs, shift in (
+                (slo, LO_COPY, 0),
+                (shi, HI_COPY, 0),
+                (ssh, ((8, 12, slice(0, 1)), (12, 16, slice(0, 1))), 8),
+                (sx, ((15, 16, slice(0, 1)),), 7),
+            ):
+                for b0, b1, n in runs:
+                    p0 = 32 * (b0 // 4) + b0 % 4
+                    q0 = 32 * ((b0 - shift) // 4) + (b0 - shift) % 4
+                    o = t[p0 : p0 + b1 - b0, n].rearrange("p n h d -> p n (h d)").bitcast(I32)
+                    v = vs[q0 : q0 + b1 - b0, k0:k1].rearrange("p h d -> p (h d)").bitcast(I32)
+                    nc.sync.dma_start(out=o, in_=v.unsqueeze(1).to_broadcast(list(o.shape)))
 
         kts = {}
         qts = {}
@@ -236,75 +253,77 @@ def tile_modelnew_t_kernel(tc, Q, K, V, out):
 
         def group(g):
             kv, n = divmod(g, NGR)
-            return kv, (n + 2) % NGR if kv == HKV - 1 else n
+            return kv, LAST[n] if kv == HKV - 1 else n
 
         def ok(g):
             return 0 <= g < NG
 
-        def short_of(j, s):
-            return 2 * j + s
-
         def place(j, kind, s):
             return s if kind == 0 else (2 + s if j < 3 else 3 - s)
+
+        def long_of(k):
+            return k + 9 if k < 7 else 8
 
         def s_qk(g):
             kv, j = group(g)
             st[g] = {"raw": []}
             kt = kts[kv][:].rearrange("p n w -> p (n w)")
-
-            def mm(dst, pb, nblk):
-                w0 = 32 * (pb + 1 - nblk)
-                nc.tensor.matmul(
-                    out=dst, lhsT=qts[kv][:, QPOS[pb], :], rhs=kt[:, w0 : w0 + 32 * nblk], start=True, stop=True
-                )
-
-            for s in range(2):
-                k = short_of(j, s)
-                w = 32 * (k + 1)
+            a, b = TILES[j]
+            cut = max(0, b + 1 + 9 - 16)
+            banks = [
+                [(a, 0, a + 1), (a + 9, a + 1, a + 10), (b, 0, cut)],
+                [(b, cut, b + 1), (long_of(b), long_of(b) - 8, long_of(b) + 1)],
+            ]
+            c0 = 32 * (b - a)
+            for n, jobs in enumerate(banks):
                 raw = psr.tile([P, 512], F32, name="raw", tag="raw")
-                if s < NFILL:
+                if n < NFILL:
                     nc.tensor.matmul(
                         out=raw[:], lhsT=ident[:], rhs=qn[kv][:, 0:4, :].rearrange("p b d -> p (b d)"), start=True, stop=True
                     )
-                mm(raw[:, 0:w], k, k + 1)
-                if k < 7:
-                    mm(raw[:, w : w + LONG], k + 9, 9)
-                    st[g]["raw"].append((raw, w + LONG, s, LONG0 - w))
-                else:
-                    st[g]["raw"].append((raw, w, s, LONG0 - w))
-                    raw = psr.tile([P, 512], F32, name="raw", tag="raw")
-                    mm(raw[:, 0:LONG], 8, 9)
-                    st[g]["raw"].append((raw, LONG, s, LONG0))
+                w = 0
+                for pb, k0, k1 in jobs:
+                    if k1 > k0:
+                        nc.tensor.matmul(
+                            out=raw[:, w : w + 32 * (k1 - k0)],
+                            lhsT=qts[kv][:, QPOS[pb], :],
+                            rhs=kt[:, 32 * k0 : 32 * k1],
+                            start=True,
+                            stop=True,
+                        )
+                        w += 32 * (k1 - k0)
+                st[g]["raw"].append((raw, w, c0))
+                c0 += w
+
+        def th_of(g):
+            kv, j = group(g)
+            return th[(kv == HKV - 1, j)], 32 * (TILES[j][1] + 1)
 
         def s_tanh(g):
-            kv, j = group(g)
-            for raw, w, s, c0 in st[g]["raw"]:
+            t, ws = th_of(g)
+            flat = t[:].rearrange("p s c -> p (s c)")
+            for raw, w, c0 in st[g]["raw"]:
                 nc.scalar.activation(
-                    out=th[(kv == HKV - 1, j)][:, s, c0 : c0 + w], in_=raw[:, 0:w], func=AF.Tanh, scale=SCALE / SOFTCAP
+                    out=flat[:, c0 : c0 + w], in_=raw[:, 0:w], func=AF.Tanh, scale=SCALE / SOFTCAP
                 )
 
         def s_mask(g):
-            kv, j = group(g)
-            for c0, w in ((NEAR0, 64), (LONG0 + LONG - 32, 32)):
-                v = th[(kv == HKV - 1, j)][:, :, c0 : c0 + w]
+            t, ws = th_of(g)
+            for c0, w in ((ws - 32, 64), (ws + LONG - 32, 32)):
+                v = t[:, :, c0 : c0 + w]
                 (nc.gpsimd if MASK_ENG == "gpsimd" else nc.vector).tensor_tensor(
                     out=v, in0=v, in1=mk[:, 0:w].unsqueeze(1).to_broadcast([P, 2, w]), op=ALU.add
                 )
 
         def s_max_long(g):
-            kv, j = group(g)
+            t, ws = th_of(g)
             mx = small.tile([P, 4], F32, name="mx", tag="mx")
             st[g]["mx"] = mx
-            nc.vector.tensor_reduce(
-                out=mx[:, 2:4], in_=th[(kv == HKV - 1, j)][:, :, LONG0 : LONG0 + LONG], axis=AX.X, op=ALU.max
-            )
+            nc.vector.tensor_reduce(out=mx[:, 2:4], in_=t[:, :, ws : ws + LONG], axis=AX.X, op=ALU.max)
 
         def s_max_short(g):
-            kv, j = group(g)
-            w = 64 * (j + 1)
-            nc.vector.tensor_reduce(
-                out=st[g]["mx"][:, 0:2], in_=th[(kv == HKV - 1, j)][:, :, LONG0 - w : LONG0], axis=AX.X, op=ALU.max
-            )
+            t, ws = th_of(g)
+            nc.vector.tensor_reduce(out=st[g]["mx"][:, 0:2], in_=t[:, :, 0:ws], axis=AX.X, op=ALU.max)
 
         def s_nb(g):
             nb = small.tile([P, 4], F32, name="nb", tag="nb")
@@ -322,35 +341,41 @@ def tile_modelnew_t_kernel(tc, Q, K, V, out):
             kv, j = group(g)
             h = g // 2
             if h not in halves:
-                halves[h] = {"ls": small.tile([P, 8], F32, name="ls", tag="ls")}
+                halves[h] = {"ls": small.tile([P, 9], F32, name="ls", tag="ls")}
             ls = halves[h]["ls"]
             nb = st[g]["nb"]
-            for kind in range(2):
-                for s in range(2):
-                    k = short_of(j, s)
-                    if kind == 0:
-                        c0, nblk, blk0, ti = LONG0 - 32 * (k + 1), k + 1, 0, k
-                    elif k < 7:
-                        c0, nblk, blk0, ti = LONG0, 9, k + 1, k
-                    else:
-                        c0, nblk, blk0, ti = LONG0, 9, 0, 8
-                    u = 2 * kind + s
-                    col = 4 * (g % 2) + place(j, kind, s)
-                    nc.scalar.activation(
-                        out=pt[kv % 2][ti][:, :, 8 * blk0 : 8 * (blk0 + nblk), :].rearrange("p u (b c) e -> p u b (c e)", c=8),
-                        in_=th[(kv == HKV - 1, j)][:, s, c0 : c0 + 32 * nblk].rearrange("p (b u x) -> p u b x", u=2, x=16),
-                        func=AF.Exp,
-                        bias=nb[:, u : u + 1],
-                        scale=SOFTCAP,
-                        accum_out=ls[:, col : col + 1],
-                    )
+            t, ws = th_of(g)
+
+            def piece(s, u, c0, nblk, ti, blk0, col):
+                nc.scalar.activation(
+                    out=pt[kv % 2][ti][:, :, 8 * blk0 : 8 * (blk0 + nblk), :].rearrange("p u (b c) e -> p u b (c e)", c=8),
+                    in_=t[:, s, c0 : c0 + 32 * nblk].rearrange("p (b u x) -> p u b x", u=2, x=16),
+                    func=AF.Exp,
+                    bias=nb[:, u : u + 1],
+                    scale=SOFTCAP,
+                    accum_out=ls[:, col : col + 1],
+                )
+
+            for s, k in enumerate(TILES[j]):
+                piece(s, s, ws - 32 * (k + 1), k + 1, k, 0, 4 * (g % 2) + place(j, 0, s))
+            for s, k in enumerate(TILES[j]):
+                col = 4 * (g % 2) + place(j, 1, s)
+                if k < 7:
+                    piece(s, 2 + s, ws, 9, k, k + 1, col)
+                else:
+                    piece(s, 2 + s, ws, 8, 7, 8, col)
+                    piece(s, 2 + s, ws + 256, 1, 5, 15, 8)
 
         def s_rl_add(g):
             if g % 2 == 0:
                 return
             h = halves[g // 2]
             h["le"] = small.tile([P, 8], F32, name="le", tag="le")
-            nc.gpsimd.tensor_scalar(out=h["le"][:], in0=h["ls"][:], scalar1=EPS, scalar2=1.0, op0=ALU.add, op1=ALU.mult)
+            nc.gpsimd.tensor_scalar(out=h["le"][:], in0=h["ls"][:, 0:8], scalar1=EPS, scalar2=1.0, op0=ALU.add, op1=ALU.mult)
+            if group(g)[1] == 3:
+                nc.gpsimd.tensor_scalar(
+                    out=h["le"][:, 6:7], in0=h["ls"][:, 6:7], scalar1=h["ls"][:, 8:9], scalar2=EPS, op0=ALU.add, op1=ALU.add
+                )
 
         def s_rl(g):
             if g % 2 == 0:
@@ -359,141 +384,129 @@ def tile_modelnew_t_kernel(tc, Q, K, V, out):
             h["rl"] = small.tile([P, 8], F32, name="rl", tag="rl")
             nc.vector.reciprocal(out=h["rl"][:], in_=h["le"][:])
 
-        def tiles_of(g):
-            kv, j = group(g)
-            return ((2 * j, 2 * j + 1),) if j < 3 else ((6, 7), (8,))
-
         def s_tr(g):
-            kv = g // NGR
-            st[g]["tp"] = []
-            for tis in tiles_of(g):
-                tp = pst.tile([P, 2, 2, P], F32, name="tp", tag="tp")
-                for n, ti in enumerate(tis):
-                    for u in range(2):
-                        nc.tensor.transpose(tp[:, n, u, :], words(pt[kv % 2][ti])[:, P * u : P * u + P], identf[:])
-                st[g]["tp"].append((tp, len(tis)))
+            kv, j = group(g)
+            tp = pst.tile([P, 2, 2, P], F32, name="tp", tag="tp")
+            st[g]["tp"] = tp
+            for n, ti in enumerate(TILES[j]):
+                for u in range(2):
+                    nc.tensor.transpose(tp[:, n, u, :], words(pt[kv % 2][ti])[:, P * u : P * u + P], identf[:])
 
         def s_evac(g):
-            st[g]["gt"] = {}
-            for n in range(len(st[g]["tp"])):
-                tp, m = st[g]["tp"][n]
-                gt = gp.tile([P, 2, P, 4], BF16, name="gt", tag="gt", align_bytes=64)
-                (nc.vector.tensor_copy if (g, n) in EVAC_V or (group(g)[1], n) in EVAC_V else nc.scalar.copy)(
-                    out=gt[:, 0:m].rearrange("p n r t -> p (n r t)").bitcast(F32).rearrange("p (n r u) -> p n r u", n=m, u=2),
-                    in_=tp[:, 0:m].rearrange("p n u r -> p n r u"),
-                )
-                st[g]["gt"][n] = (gt, m)
+            kv, j = group(g)
+            gt = gp.tile([P, 2, P, 4], BF16, name="gt", tag="gt", align_bytes=64)
+            (nc.vector.tensor_copy if j in EVAC_V[kv] else nc.scalar.copy)(
+                out=gt[:].rearrange("p n r t -> p (n r t)").bitcast(F32).rearrange("p (n r u) -> p n r u", n=2, u=2),
+                in_=st[g]["tp"][:].rearrange("p n u r -> p n r u"),
+            )
+            st[g]["gt"] = gt
 
         def s_quant(g):
-            st[g]["q"] = []
-            for n in range(len(st[g]["gt"])):
-                gt, m = st[g]["gt"][n]
-                cd = gp.tile([P, 2, P], I32, name="cd", tag="cd", align_bytes=64)
-                sc = gp.tile([P, 2, P], U8, name="sc", tag="sc", align_bytes=64)
-                nc.vector.quantize_mx(
-                    out=cd[:, 0:m].rearrange("p n r -> p (n r)").bitcast(FP8X4),
-                    scales=sc[:, 0:m].rearrange("p n r -> p (n r)"),
-                    in_=gt[:, 0:m].rearrange("p n r t -> p (n r t)"),
-                )
-                st[g]["q"].append((cd, sc))
+            cd = gp.tile([P, 2, P], I32, name="cd", tag="cd", align_bytes=64)
+            sc = gp.tile([P, 2, P], U8, name="sc", tag="sc", align_bytes=64)
+            nc.vector.quantize_mx(
+                out=cd[:].rearrange("p n r -> p (n r)").bitcast(FP8X4),
+                scales=sc[:].rearrange("p n r -> p (n r)"),
+                in_=st[g]["gt"][:].rearrange("p n r t -> p (n r t)"),
+            )
+            st[g]["q"] = (cd, sc)
 
         def s_mx(g):
             kv, j = group(g)
-            acc = psa.tile([P, 4, D], F32, name="acc", tag="acc")
+            if g == NG - 1:
+                acc = psr.tile([P, 4, D], F32, name="raw", tag="raw")
+            else:
+                acc = psa.tile([P, 4, D], F32, name="acc", tag="acc")
             st[g]["acc"] = acc
-            for s in range(2):
-                k = short_of(j, s)
-                cd, sc = st[g]["q"][0]
-                if k < 7:
-                    jobs = ((0, cd, sc, s, vlo[k + 1]), (1, cd, sc, s, vhi[k + 1]))
-                else:
-                    cd8, sc8 = st[g]["q"][1]
-                    jobs = ((0, cd, sc, s, vc), (1, cd8, sc8, 0, vc))
-                for kind, c, e, n, rhs in jobs:
+            cd, sc = st[g]["q"]
+            slo, shi, ssh, sx = var[min(1, kv // 2)]
+
+            def mx(u, passes):
+                for i, (n, rhs, rs) in enumerate(passes):
                     nc.tensor.matmul_mx(
-                        out=acc[:, place(j, kind, s), :],
-                        lhsT=c[:, n, :].bitcast(FP8X4),
-                        lhsT_scale=e[:, n, :],
+                        out=acc[:, u, :],
+                        lhsT=cd[:, n, :].bitcast(FP8X4),
+                        lhsT_scale=sc[:, n, :],
                         rhs=rhs[:, kv, :].bitcast(FP8X4),
-                        rhs_scale=vs[:, kv, :],
-                        start=True,
-                        stop=True,
+                        rhs_scale=rs[:, kv if kv < 2 else kv - 2, :],
+                        start=(i == 0),
+                        stop=(i == len(passes) - 1),
                     )
+
+            for s, k in enumerate(TILES[j]):
+                mx(place(j, 0, s), [(s, vc, slo[:, k])])
+                mx(place(j, 1, s), [(s, vc, shi[:, HI[k]])] if k < 7 else [(1, vsh, ssh[:, 0]), (0, vx, sx[:, 0])])
 
         def store(kv, b0, b1, o):
             for q in range(G):
                 nc.sync.dma_start(
-                    out=out[0, G * kv + q].rearrange("(b i) d -> i b d", i=NB)[:, b0:b1, :], in_=o[q:P:G]
+                    out=out[0, G * kv + q].rearrange("(b i) d -> i b d", i=NB)[:, b0:b1, :], in_=o[q:P:G, b0:b1]
                 )
 
         def s_norm(g):
             kv, j = group(g)
             rl = halves[g // 2]["rl"][:, 4 * (g % 2) : 4 * (g % 2) + 4]
             acc = st[g]["acc"]
-            last = kv == HKV - 1
             ko = (kv, kv >= HKV - 2 and j < 2)
             if ko not in oall:
-                oall[ko] = op.tile([P, 22, D], F32, name="oall", tag="oall")
+                oall[ko] = op.tile([P, 2, 9, D], F32, name="oall", tag="oall")
             o = oall[ko]
-            if j < 3:
-                a = 2 * j
+            flat = o[:].rearrange("p x y d -> p (x y) d")
+            a, b = TILES[j]
+            if g == NG - 2:
+                for u, n in enumerate((a, b, a + 9, b + 9)):
+                    nc.scalar.activation(out=flat[:, n], in_=acc[:, u, :], func=AF.Copy, scale=rl[:, u : u + 1])
+            elif j < 3:
                 nc.vector.tensor_tensor(
-                    out=o[:, a : a + 18, :].rearrange("p (x y) d -> p x y d", x=2)[:, :, 0:2, :],
+                    out=o[:, :, a : b + 1 : b - a, :],
                     in0=acc[:].rearrange("p (x y) d -> p x y d", x=2),
                     in1=rl.rearrange("p (x y) -> p x y", x=2).unsqueeze(3).to_broadcast([P, 2, 2, D]),
                     op=ALU.mult,
                 )
             else:
-                spans = ((6, 9), (15, 16))
-                for (b0, b1), u in zip(spans, (0, 3)):
-                    m = b1 - b0
+                for u, b0, step in ((0, a, b - a), (2, 8, 6)):
                     nc.vector.tensor_tensor(
-                        out=o[:, b0:b1, :],
-                        in0=acc[:, u : u + m, :],
-                        in1=rl[:, u : u + m].unsqueeze(2).to_broadcast([P, m, D]),
+                        out=flat[:, b0 : b0 + step + 1 : step, :],
+                        in0=acc[:, u : u + 2, :],
+                        in1=rl[:, u : u + 2].unsqueeze(2).to_broadcast([P, 2, D]),
                         op=ALU.mult,
                     )
-            if last:
-                if j == 3:
-                    store(kv, 4, 9, o[:, 4:9])
-                    store(kv, 13, NPB, o[:, 13:NPB])
-                elif j == 1:
-                    store(kv, 0, 4, o[:, 0:4])
-                    store(kv, 9, 13, o[:, 9:13])
-            elif kv == HKV - 2:
-                if j == 1:
-                    store(kv, 0, 4, o[:, 0:4])
-                    store(kv, 9, 13, o[:, 9:13])
+            if kv >= HKV - 2:
+                if g % NGR == 3 and j < 2 or kv < HKV - 1 and j == 1:
+                    store(kv, 0, 4, flat)
+                    store(kv, 9, 13, flat)
                 elif j == 3:
-                    store(kv, 4, 9, o[:, 4:9])
-                    store(kv, 13, NPB, o[:, 13:NPB])
+                    store(kv, 4, 9, flat)
+                    store(kv, 13, NPB, flat)
             elif j == 3:
-                store(kv, 0, NPB, o[:, 0:NPB])
+                store(kv, 0, NPB, flat)
 
         prep = {0: [(0, 1)], 1: [(1, 0)], 2: [(1, 1), (1, 2)]}
         for kv in range(2, HKV):
             for part in range(3):
                 prep[NGR * (kv - 1) + part] = [(kv, (1 - part if kv == HKV - 1 and part < 2 else part))]
 
-        ZEROS = ((0, vhi[3]), (1, vhi[4]), (2, vlo[5]), (6, vhi[5]), (6, vlo[6]), (7, vhi[6]), (7, vlo[7]), (8, vhi[7]))
-        VDMA = {1: 6, 2: 6, 3: 6, 4: 6, 5: 7, 6: 8, 7: 9}
         extra = {}
 
         def at(i, f):
             extra.setdefault(i, []).append(f)
 
-        for k0, k1 in ((0, 1), (1, 2), (2, 4), (4, 6), (6, 8)):
-            at(V_AT[k0], lambda k0=k0, k1=k1: v_regroup(k0, k1))
-            at(V_AT[k0] + 1, lambda k0=k0, k1=k1: v_quant(k0, k1))
-        for i, t in ZEROS:
-            at(i, lambda t=t: v_zero(nc.gpsimd, t, 2))
-        for b in VORDER:
-            at((b + 1) // 2 + 2 + DEL0, lambda b=b: v_variant_dve(b))
-            at(VDMA[b], lambda b=b: v_variant_dma(b))
+        for k in range(HKV):
+            at(V_AT[k], lambda k=k: v_regroup(k, k + 1))
+            if k % 2:
+                at(V_AT[k] + 1, lambda k=k: v_quant(k - 1, k + 1))
+        for t in var[1][1:]:
+            at(3, lambda t=t: s_zero(nc.vector, t))
+        at(V_AT[1] + 1, lambda: v_variants(0))
+        for kv in range(4, HKV):
+            at(V_AT[1] + 1, lambda kv=kv: load_head(kv))
+        at(V_AT[7] + 2, lambda: v_variants(1))
         prep_pe(0, 2)
         prep_pe(0, 0)
         prep_copy(0, 2)
         prep_copy(0, 0)
+        for ti in range(NT):
+            p_zero(ti)
         s_qk(0)
         def exps(g):
             if ok(g):
@@ -513,13 +526,14 @@ def tile_modelnew_t_kernel(tc, Q, K, V, out):
                 prep_copy(*a)
             if ok(i + 1):
                 s_qk(i + 1)
+            if ok(i - L_MAX):
+                s_max_long(i - L_MAX)
+                s_max_short(i - L_MAX)
+                s_nb(i - L_MAX)
             if ok(i - L_EVAC):
                 s_evac(i - L_EVAC)
             for g in mx_at.get(i, []):
                 s_quant(g)
-            if ok(i - L_MAX):
-                s_max_long(i - L_MAX)
-                s_max_short(i - L_MAX)
             if ok(i - L_EXP - 1):
                 s_rl(i - L_EXP - 1)
             for a in prep.get(i, []):
@@ -529,25 +543,29 @@ def tile_modelnew_t_kernel(tc, Q, K, V, out):
                 s_mx(g)
             for g in mx_at.get(i - 1, []):
                 s_norm(g)
-            if ok(i - L_MAX):
-                s_nb(i - L_MAX)
             for f in extra.get(i, []):
                 f()
         z = NG - 1
         s_max_long(z)
         s_max_short(z)
         s_nb(z)
-        for n in range(4):
-            q = z - 3 + n
-            if n < 2:
-                exps(z - 1 + n)
-            if n < 3:
-                s_evac(z - 2 + n)
-            if n == 0:
-                s_rl(z - 2)
-            if n == 2:
-                s_rl(z)
-            s_quant(q)
-            s_mx(q)
-            s_norm(q - 1)
+        exps(z - 1)
+        s_evac(z - 2)
+        s_rl(z - 2)
+        s_quant(z - 3)
+        s_mx(z - 3)
+        s_norm(z - 4)
+        s_quant(z - 2)
+        s_mx(z - 2)
+        s_norm(z - 3)
+        exps(z)
+        s_evac(z - 1)
+        s_norm(z - 2)
+        s_evac(z)
+        s_quant(z - 1)
+        s_mx(z - 1)
+        s_rl(z)
+        s_quant(z)
+        s_mx(z)
+        s_norm(z - 1)
         s_norm(z)

@@ -34,16 +34,13 @@ L_MASK, L_MAX, L_EXP, L_EVAC, L_QUANT, L_NORM = 0, 1, 2, 3, 4, 5
 MASK_ENG = "gpsimd"
 NFILL = 1
 V_AT = (0, 1, 2, 3, 4, 5, 6, 7)
-EVAC_V = {0: (0, 1, 2, 3), 1: (2,), 2: (2,), 3: (2,), 4: (2,), 5: (2,), 6: (2,), 7: (2,)}
+EVAC_V = {0: (0, 1, 2, 3,), 1: (2,), 2: (0, 2,), 3: (2,), 4: (2,), 5: (2,), 6: (2,), 7: (2,)}
 NB_POOL = True
 DEL0, DELN = 3, 8
 LAST = (2, 3, 1, 0)
-HI = (0, 1, 2, 3, 5, 6, 4)
-LO_COPY = ((0, 4, slice(3, 8)), (0, 2, slice(1, 3)), (4, 8, slice(7, 8)), (4, 6, slice(5, 7))) + tuple(
-    (n, n + 1, slice(n, n + 1)) for n in (0, 2, 4, 6)
+SCALES = tuple((b, b + 1, 0, b, b + 8) for b in range(8)) + (
+    (8, 12, 0, 8, 15), (12, 14, 0, 8, 15), (14, 15, 0, 8, 15), (15, 16, 0, 14, 15), (8, 12, 8, 15, 16), (12, 16, 8, 15, 16), (15, 16, 7, 16, 17)
 )
-HI_COPY = ((8, 12, slice(0, 7)), (12, 16, slice(0, 6)), (12, 14, slice(6, 7)), (14, 15, slice(6, 7)), (4, 8, slice(0, 4)),
-           (6, 8, slice(5, 7)), (2, 4, slice(0, 2))) + tuple((n + 1, n + 2, slice(HI[n], HI[n] + 1)) for n in (0, 2, 4, 6))
 
 
 def tile_modelnew_t_kernel(tc, Q, K, V, out):
@@ -91,27 +88,21 @@ def tile_modelnew_t_kernel(tc, Q, K, V, out):
         load_k(2)
         load_q(2, 0, NPB)
         load_v(2, HKV)
-        load_k(3)
-        load_q(3, 0, NPB)
 
         vg = const.tile([P, HKV, D, 4], BF16, name="vg", align_bytes=64)
         vc = const.tile([P, HKV, P], I32, name="vc", align_bytes=64)
         vs = const.tile([P, HKV, P], U8, name="vs", align_bytes=64)
         vsh = const.tile([P, HKV, P], I32, name="vsh", align_bytes=64)
         vx = const.tile([P, HKV, P], I32, name="vx", align_bytes=64)
-        var = []
-        for part, nh in enumerate((2, HKV - 2)):
-            slo = const.tile([P, 8, nh, P], U8, name="slo%d" % part, align_bytes=64)
-            shi = const.tile([P, 7, nh, P], U8, name="shi%d" % part, align_bytes=64)
-            ssh = const.tile([P, 1, nh, P], U8, name="ssh%d" % part, align_bytes=64)
-            sx = const.tile([P, 1, nh, P], U8, name="sx%d" % part, align_bytes=64)
-            var.append((slo, shi, ssh, sx))
+        var = [
+            const.tile([P, 17, nh, P], U8, name="sv%d" % part, align_bytes=64)
+            for part, nh in enumerate((2, HKV - 2))
+        ]
 
-        def s_zero(eng, t):
-            eng.memset(t[:].rearrange("p n h d -> p (n h d)").bitcast(I32), 0)
+        def s_zero(part, n0, n1):
+            nc.vector.memset(var[part][:, n0:n1].rearrange("p n h d -> p (n h d)").bitcast(I32), 0)
 
-        for t in var[0]:
-            s_zero(nc.vector, t)
+        s_zero(0, 0, 17)
 
         ident = const.tile([P, P], BF16, name="ident")
         make_identity(nc, ident[:])
@@ -132,9 +123,7 @@ def tile_modelnew_t_kernel(tc, Q, K, V, out):
             for t in (th[(False, j)], th[(True, j)])[0 : 1 + j // 2]:
                 nc.vector.memset(t[:, 0, 0 : 32 * (b - a)], FILL)
 
-        nc.vector.memset(vx[:].rearrange("p h d -> p (h d)"), 0)
-        nc.vector.memset(vsh[0:64].rearrange("p h d -> p (h d)"), 0)
-        s_zero(nc.vector, var[1][0])
+        s_zero(1, 0, 17)
 
         mnear = const.tile([P, 32], F32, name="mnear")
         mfar = const.tile([P, 32], F32, name="mfar")
@@ -154,6 +143,9 @@ def tile_modelnew_t_kernel(tc, Q, K, V, out):
                 out=mk[:, 32 * n : 32 * n + 32].rearrange("p (u c e) -> p u c e", u=2, e=2),
                 in_=m[:].rearrange("p (u e c) -> p u c e", u=2, e=2),
             )
+
+        nc.gpsimd.memset(vx[:].rearrange("p h d -> p (h d)"), 0)
+        nc.gpsimd.memset(vsh[0:64].rearrange("p h d -> p (h d)"), 0)
 
         pt = [[const.tile([P, 2, P, 2], BF16, name="pt%d_%d" % (st, ti)) for ti in range(NT)] for st in range(2)]
 
@@ -183,21 +175,14 @@ def tile_modelnew_t_kernel(tc, Q, K, V, out):
 
         def v_variants(part):
             k0, k1 = ((0, 2), (2, HKV))[part]
-            slo, shi, ssh, sx = var[part]
             nc.sync.dma_start(out=vsh[64:P, k0:k1], in_=vc[0:64, k0:k1])
             nc.sync.dma_start(out=vx[120:P, k0:k1], in_=vc[64:72, k0:k1])
-            for t, runs, shift in (
-                (slo, LO_COPY, 0),
-                (shi, HI_COPY, 0),
-                (ssh, ((8, 12, slice(0, 1)), (12, 16, slice(0, 1))), 8),
-                (sx, ((15, 16, slice(0, 1)),), 7),
-            ):
-                for b0, b1, n in runs:
-                    p0 = 32 * (b0 // 4) + b0 % 4
-                    q0 = 32 * ((b0 - shift) // 4) + (b0 - shift) % 4
-                    o = t[p0 : p0 + b1 - b0, n].rearrange("p n h d -> p n (h d)").bitcast(I32)
-                    v = vs[q0 : q0 + b1 - b0, k0:k1].rearrange("p h d -> p (h d)").bitcast(I32)
-                    nc.sync.dma_start(out=o, in_=v.unsqueeze(1).to_broadcast(list(o.shape)))
+            for b0, b1, shift, n0, n1 in SCALES:
+                p0 = 32 * (b0 // 4) + b0 % 4
+                q0 = 32 * ((b0 - shift) // 4) + (b0 - shift) % 4
+                o = var[part][p0 : p0 + b1 - b0, n0:n1].rearrange("p n h d -> p n (h d)").bitcast(I32)
+                v = vs[q0 : q0 + b1 - b0, k0:k1].rearrange("p h d -> p (h d)").bitcast(I32)
+                nc.sync.dma_start(out=o, in_=v.unsqueeze(1).to_broadcast(list(o.shape)))
 
         kts = {}
         qts = {}
@@ -248,7 +233,7 @@ def tile_modelnew_t_kernel(tc, Q, K, V, out):
 
         NG = HKV * NGR
         st = {}
-        halves = {}
+        sums = {}
         oall = {}
 
         def group(g):
@@ -258,8 +243,8 @@ def tile_modelnew_t_kernel(tc, Q, K, V, out):
         def ok(g):
             return 0 <= g < NG
 
-        def place(j, kind, s):
-            return s if kind == 0 else (2 + s if j < 3 else 3 - s)
+        def place(kv, j, kind, s):
+            return s if kind == 0 else (2 + s if j < 3 or kv < HKV - 2 else 3 - s)
 
         def long_of(k):
             return k + 9 if k < 7 else 8
@@ -339,10 +324,13 @@ def tile_modelnew_t_kernel(tc, Q, K, V, out):
 
         def s_exp(g):
             kv, j = group(g)
-            h = g // 2
-            if h not in halves:
-                halves[h] = {"ls": small.tile([P, 9], F32, name="ls", tag="ls")}
-            ls = halves[h]["ls"]
+            if kv not in sums:
+                sums[kv] = {
+                    "ls": small.tile([P, 17], F32, name="ls", tag="ls"),
+                    "le": small.tile([P, 16], F32, name="le", tag="le"),
+                    "rl": small.tile([P, 16], F32, name="rl", tag="rl"),
+                }
+            ls = sums[kv]["ls"]
             nb = st[g]["nb"]
             t, ws = th_of(g)
 
@@ -357,32 +345,47 @@ def tile_modelnew_t_kernel(tc, Q, K, V, out):
                 )
 
             for s, k in enumerate(TILES[j]):
-                piece(s, s, ws - 32 * (k + 1), k + 1, k, 0, 4 * (g % 2) + place(j, 0, s))
+                piece(s, s, ws - 32 * (k + 1), k + 1, k, 0, 4 * (g % NGR) + place(kv, j, 0, s))
             for s, k in enumerate(TILES[j]):
-                col = 4 * (g % 2) + place(j, 1, s)
+                col = 4 * (g % NGR) + place(kv, j, 1, s)
                 if k < 7:
                     piece(s, 2 + s, ws, 9, k, k + 1, col)
                 else:
                     piece(s, 2 + s, ws, 8, 7, 8, col)
-                    piece(s, 2 + s, ws + 256, 1, 5, 15, 8)
+                    piece(s, 2 + s, ws + 256, 1, 5, 15, 16)
+
+        def ready(g):
+            kv, n = divmod(g, NGR)
+            if n == 3:
+                return (8, 16) if kv == HKV - 1 else (0, 16)
+            return (0, 8) if n == 1 and kv == HKV - 1 else None
 
         def s_rl_add(g):
-            if g % 2 == 0:
+            if ready(g) is None:
                 return
-            h = halves[g // 2]
-            h["le"] = small.tile([P, 8], F32, name="le", tag="le")
-            nc.gpsimd.tensor_scalar(out=h["le"][:], in0=h["ls"][:, 0:8], scalar1=EPS, scalar2=1.0, op0=ALU.add, op1=ALU.mult)
-            if group(g)[1] == 3:
-                nc.gpsimd.tensor_scalar(
-                    out=h["le"][:, 6:7], in0=h["ls"][:, 6:7], scalar1=h["ls"][:, 8:9], scalar2=EPS, op0=ALU.add, op1=ALU.add
-                )
+            c0, c1 = ready(g)
+            h = sums[g // NGR]
+            nc.gpsimd.tensor_scalar(
+                out=h["le"][:, c0:c1], in0=h["ls"][:, c0:c1], scalar1=EPS, scalar2=1.0, op0=ALU.add, op1=ALU.mult
+            )
+            for n in range(c0 // 4, c1 // 4):
+                if group(g - g % NGR + n)[1] == 3:
+                    c = 4 * n + place(g // NGR, 3, 1, 1)
+                    nc.gpsimd.tensor_scalar(
+                        out=h["le"][:, c : c + 1],
+                        in0=h["ls"][:, c : c + 1],
+                        scalar1=h["ls"][:, 16:17],
+                        scalar2=EPS,
+                        op0=ALU.add,
+                        op1=ALU.add,
+                    )
 
         def s_rl(g):
-            if g % 2 == 0:
+            if ready(g) is None:
                 return
-            h = halves[g // 2]
-            h["rl"] = small.tile([P, 8], F32, name="rl", tag="rl")
-            nc.vector.reciprocal(out=h["rl"][:], in_=h["le"][:])
+            c0, c1 = ready(g)
+            h = sums[g // NGR]
+            nc.vector.reciprocal(out=h["rl"][:, c0:c1], in_=h["le"][:, c0:c1])
 
         def s_tr(g):
             kv, j = group(g)
@@ -419,7 +422,7 @@ def tile_modelnew_t_kernel(tc, Q, K, V, out):
                 acc = psa.tile([P, 4, D], F32, name="acc", tag="acc")
             st[g]["acc"] = acc
             cd, sc = st[g]["q"]
-            slo, shi, ssh, sx = var[min(1, kv // 2)]
+            sv = var[min(1, kv // 2)]
 
             def mx(u, passes):
                 for i, (n, rhs, rs) in enumerate(passes):
@@ -428,32 +431,40 @@ def tile_modelnew_t_kernel(tc, Q, K, V, out):
                         lhsT=cd[:, n, :].bitcast(FP8X4),
                         lhsT_scale=sc[:, n, :],
                         rhs=rhs[:, kv, :].bitcast(FP8X4),
-                        rhs_scale=rs[:, kv if kv < 2 else kv - 2, :],
+                        rhs_scale=sv[:, rs, kv if kv < 2 else kv - 2, :],
                         start=(i == 0),
                         stop=(i == len(passes) - 1),
                     )
 
             for s, k in enumerate(TILES[j]):
-                mx(place(j, 0, s), [(s, vc, slo[:, k])])
-                mx(place(j, 1, s), [(s, vc, shi[:, HI[k]])] if k < 7 else [(1, vsh, ssh[:, 0]), (0, vx, sx[:, 0])])
+                mx(place(kv, j, 0, s), [(s, vc, k)])
+                mx(place(kv, j, 1, s), [(s, vc, 8 + k)] if k < 7 else [(1, vsh, 15), (0, vx, 16)])
 
-        def store(kv, b0, b1, o):
+        def store(kv, b0, b1, o, slot=None, eng=nc.sync):
+            slot = b0 if slot is None else slot
             for q in range(G):
-                nc.sync.dma_start(
-                    out=out[0, G * kv + q].rearrange("(b i) d -> i b d", i=NB)[:, b0:b1, :], in_=o[q:P:G, b0:b1]
+                eng.dma_start(
+                    out=out[0, G * kv + q].rearrange("(b i) d -> i b d", i=NB)[:, b0:b1, :], in_=o[q:P:G, slot : slot + b1 - b0]
                 )
 
         def s_norm(g):
             kv, j = group(g)
-            rl = halves[g // 2]["rl"][:, 4 * (g % 2) : 4 * (g % 2) + 4]
+            rl = sums[kv]["rl"][:, 4 * (g % NGR) : 4 * (g % NGR) + 4]
             acc = st[g]["acc"]
-            ko = (kv, kv >= HKV - 2 and j < 2)
+            ko = (kv, kv == HKV - 1 and j < 2)
             if ko not in oall:
                 oall[ko] = op.tile([P, 2, 9, D], F32, name="oall", tag="oall")
             o = oall[ko]
             flat = o[:].rearrange("p x y d -> p (x y) d")
             a, b = TILES[j]
-            if g == NG - 2:
+            if j == 3 and kv < HKV - 2:
+                nc.vector.tensor_tensor(
+                    out=o[:, :, a : b + 1 : b - a, :],
+                    in0=acc[:].rearrange("p (x y) d -> p x y d", x=2),
+                    in1=rl.rearrange("p (x y) -> p x y", x=2).unsqueeze(3).to_broadcast([P, 2, 2, D]),
+                    op=ALU.mult,
+                )
+            elif g == NG - 2:
                 for u, n in enumerate((a, b, a + 9, b + 9)):
                     nc.scalar.activation(out=flat[:, n], in_=acc[:, u, :], func=AF.Copy, scale=rl[:, u : u + 1])
             elif j < 3:
@@ -472,14 +483,21 @@ def tile_modelnew_t_kernel(tc, Q, K, V, out):
                         op=ALU.mult,
                     )
             if kv >= HKV - 2:
-                if g % NGR == 3 and j < 2 or kv < HKV - 1 and j == 1:
+                if kv < HKV - 1:
+                    if j == 1:
+                        store(kv, 0, 4, flat)
+                    elif j == 3:
+                        store(kv, 4, NPB, flat)
+                elif g % NGR == 3:
                     store(kv, 0, 4, flat)
                     store(kv, 9, 13, flat)
                 elif j == 3:
                     store(kv, 4, 9, flat)
-                    store(kv, 13, NPB, flat)
+                    store(kv, 13, NPB, flat, eng=nc.gpsimd if kv == HKV - 1 else nc.sync)
             elif j == 3:
-                store(kv, 0, NPB, flat)
+                store(kv, 0, 8, flat)
+                store(kv, 8, 9, flat, 16)
+                store(kv, 9, NPB, flat)
 
         prep = {0: [(0, 1)], 1: [(1, 0)], 2: [(1, 1), (1, 2)]}
         for kv in range(2, HKV):
@@ -495,12 +513,12 @@ def tile_modelnew_t_kernel(tc, Q, K, V, out):
             at(V_AT[k], lambda k=k: v_regroup(k, k + 1))
             if k % 2:
                 at(V_AT[k] + 1, lambda k=k: v_quant(k - 1, k + 1))
-        for t in var[1][1:]:
-            at(3, lambda t=t: s_zero(nc.vector, t))
         at(V_AT[1] + 1, lambda: v_variants(0))
-        for kv in range(4, HKV):
+        for kv in (3, 4):
             at(V_AT[1] + 1, lambda kv=kv: load_head(kv))
-        at(V_AT[7] + 2, lambda: v_variants(1))
+        at(V_AT[7] + 1, lambda: v_variants(1))
+        for kv in range(5, HKV):
+            at(V_AT[7] + 2 + 3 * (kv - 5), lambda kv=kv: load_head(kv))
         prep_pe(0, 2)
         prep_pe(0, 0)
         prep_copy(0, 2)
@@ -516,7 +534,8 @@ def tile_modelnew_t_kernel(tc, Q, K, V, out):
 
         mx_at = {}
         for g in range(NG):
-            mx_at.setdefault(g + L_QUANT + max(0, DEL0 - g // DELN), []).append(g)
+            lag = 1 if g % NGR == 0 and g < NG - NGR else 0
+            mx_at.setdefault(g + L_QUANT + max(lag, DEL0 - g // DELN), []).append(g)
 
         for i in range(NG):
             s_tanh(i)

@@ -36,7 +36,7 @@ NFILL = 1
 V_AT = (0, 1, 2, 3, 4, 5, 6, 7)
 EVAC_V = {0: (0, 1, 2, 3,), 1: (2,), 2: (0, 2,), 3: (2,), 4: (2,), 5: (2,), 6: (2,), 7: (2,)}
 NB_POOL = True
-DEL0, DELN = 3, 8
+DEL0, DELN = 4, 6
 LAST = (2, 3, 1, 0)
 SCALES = tuple((b, b + 1, 0, b, b + 8) for b in range(8)) + (
     (8, 12, 0, 8, 15), (12, 14, 0, 8, 15), (14, 15, 0, 8, 15), (15, 16, 0, 14, 15), (8, 12, 8, 15, 16), (12, 16, 8, 15, 16), (15, 16, 7, 16, 17)
@@ -49,7 +49,7 @@ def tile_modelnew_t_kernel(tc, Q, K, V, out):
         ctx.enter_context(tc.manual_schedule())
         const = ctx.enter_context(tc.tile_pool(name="const", bufs=1))
         qtp = ctx.enter_context(tc.tile_pool(name="qtp", bufs=2))
-        gp = ctx.enter_context(tc.tile_pool(name="gp", bufs=7))
+        gp = ctx.enter_context(tc.tile_pool(name="gp", bufs=8))
         small = ctx.enter_context(tc.tile_pool(name="small", bufs=6))
         op = ctx.enter_context(tc.tile_pool(name="op", bufs=3))
         psq = ctx.enter_context(tc.psum_pool(name="psq", bufs=1))
@@ -88,6 +88,7 @@ def tile_modelnew_t_kernel(tc, Q, K, V, out):
         load_k(2)
         load_q(2, 0, NPB)
         load_v(2, HKV)
+        load_head(3)
 
         vg = const.tile([P, HKV, D, 4], BF16, name="vg", align_bytes=64)
         vc = const.tile([P, HKV, P], I32, name="vc", align_bytes=64)
@@ -243,8 +244,8 @@ def tile_modelnew_t_kernel(tc, Q, K, V, out):
         def ok(g):
             return 0 <= g < NG
 
-        def place(kv, j, kind, s):
-            return s if kind == 0 else (2 + s if j < 3 or kv < HKV - 2 else 3 - s)
+        def place(j, kind, s):
+            return s if kind == 0 else (2 + s if j < 3 else 3 - s)
 
         def long_of(k):
             return k + 9 if k < 7 else 8
@@ -345,9 +346,9 @@ def tile_modelnew_t_kernel(tc, Q, K, V, out):
                 )
 
             for s, k in enumerate(TILES[j]):
-                piece(s, s, ws - 32 * (k + 1), k + 1, k, 0, 4 * (g % NGR) + place(kv, j, 0, s))
+                piece(s, s, ws - 32 * (k + 1), k + 1, k, 0, 4 * (g % NGR) + place(j, 0, s))
             for s, k in enumerate(TILES[j]):
-                col = 4 * (g % NGR) + place(kv, j, 1, s)
+                col = 4 * (g % NGR) + place(j, 1, s)
                 if k < 7:
                     piece(s, 2 + s, ws, 9, k, k + 1, col)
                 else:
@@ -370,7 +371,7 @@ def tile_modelnew_t_kernel(tc, Q, K, V, out):
             )
             for n in range(c0 // 4, c1 // 4):
                 if group(g - g % NGR + n)[1] == 3:
-                    c = 4 * n + place(g // NGR, 3, 1, 1)
+                    c = 4 * n + place(3, 1, 1)
                     nc.gpsimd.tensor_scalar(
                         out=h["le"][:, c : c + 1],
                         in0=h["ls"][:, c : c + 1],
@@ -437,33 +438,38 @@ def tile_modelnew_t_kernel(tc, Q, K, V, out):
                     )
 
             for s, k in enumerate(TILES[j]):
-                mx(place(kv, j, 0, s), [(s, vc, k)])
-                mx(place(kv, j, 1, s), [(s, vc, 8 + k)] if k < 7 else [(1, vsh, 15), (0, vx, 16)])
+                mx(place(j, 0, s), [(s, vc, k)])
+                mx(place(j, 1, s), [(s, vc, 8 + k)] if k < 7 else [(1, vsh, 15), (0, vx, 16)])
 
-        def store(kv, b0, b1, o, slot=None, eng=nc.sync):
-            slot = b0 if slot is None else slot
+        def store(kv, b0, b1, o):
             for q in range(G):
-                eng.dma_start(
-                    out=out[0, G * kv + q].rearrange("(b i) d -> i b d", i=NB)[:, b0:b1, :], in_=o[q:P:G, slot : slot + b1 - b0]
+                nc.sync.dma_start(
+                    out=out[0, G * kv + q].rearrange("(b i) d -> i b d", i=NB)[:, b0:b1, :], in_=o[q:P:G, b0:b1]
                 )
 
         def s_norm(g):
             kv, j = group(g)
             rl = sums[kv]["rl"][:, 4 * (g % NGR) : 4 * (g % NGR) + 4]
             acc = st[g]["acc"]
-            ko = (kv, kv == HKV - 1 and j < 2)
+            ko = (kv, False)
             if ko not in oall:
                 oall[ko] = op.tile([P, 2, 9, D], F32, name="oall", tag="oall")
+                if kv == HKV - 1:
+                    oall[(kv, True)] = op.tile([P, 2, 9, D], F32, name="oall", tag="oall")
             o = oall[ko]
             flat = o[:].rearrange("p x y d -> p (x y) d")
             a, b = TILES[j]
-            if j == 3 and kv < HKV - 2:
-                nc.vector.tensor_tensor(
-                    out=o[:, :, a : b + 1 : b - a, :],
-                    in0=acc[:].rearrange("p (x y) d -> p x y d", x=2),
-                    in1=rl.rearrange("p (x y) -> p x y", x=2).unsqueeze(3).to_broadcast([P, 2, 2, D]),
-                    op=ALU.mult,
-                )
+            if kv == HKV - 1 and j > 1:
+                mid = oall[(kv, True)][:].rearrange("p x y d -> p (x y) d")
+                for u, n, t, b0, step in ((0, 2, mid, a, 2),) + (((2, 2, flat, a + 9, 2),) if j == 2 else ((2, 1, mid, 8, 1), (3, 1, flat, 14, 1))):
+                    nc.vector.tensor_tensor(
+                        out=t[:, b0 : b0 + step * (n - 1) + 1 : step, :],
+                        in0=acc[:, u : u + n, :],
+                        in1=rl[:, u : u + n].unsqueeze(2).to_broadcast([P, n, D]),
+                        op=ALU.mult,
+                    )
+                if j == 3:
+                    store(kv, 4, 9, mid)
             elif g == NG - 2:
                 for u, n in enumerate((a, b, a + 9, b + 9)):
                     nc.scalar.activation(out=flat[:, n], in_=acc[:, u, :], func=AF.Copy, scale=rl[:, u : u + 1])
@@ -482,22 +488,12 @@ def tile_modelnew_t_kernel(tc, Q, K, V, out):
                         in1=rl[:, u : u + 2].unsqueeze(2).to_broadcast([P, 2, D]),
                         op=ALU.mult,
                     )
-            if kv >= HKV - 2:
-                if kv < HKV - 1:
-                    if j == 1:
-                        store(kv, 0, 4, flat)
-                    elif j == 3:
-                        store(kv, 4, NPB, flat)
-                elif g % NGR == 3:
-                    store(kv, 0, 4, flat)
-                    store(kv, 9, 13, flat)
-                elif j == 3:
-                    store(kv, 4, 9, flat)
-                    store(kv, 13, NPB, flat, eng=nc.gpsimd if kv == HKV - 1 else nc.sync)
-            elif j == 3:
-                store(kv, 0, 8, flat)
-                store(kv, 8, 9, flat, 16)
+            if kv < HKV - 1:
+                if j == 3:
+                    store(kv, 0, NPB, flat)
+            elif g % NGR == 3:
                 store(kv, 9, NPB, flat)
+                store(kv, 0, 4, flat)
 
         prep = {0: [(0, 1)], 1: [(1, 0)], 2: [(1, 1), (1, 2)]}
         for kv in range(2, HKV):
@@ -514,7 +510,7 @@ def tile_modelnew_t_kernel(tc, Q, K, V, out):
             if k % 2:
                 at(V_AT[k] + 1, lambda k=k: v_quant(k - 1, k + 1))
         at(V_AT[1] + 1, lambda: v_variants(0))
-        for kv in (3, 4):
+        for kv in (4,):
             at(V_AT[1] + 1, lambda kv=kv: load_head(kv))
         at(V_AT[7] + 1, lambda: v_variants(1))
         for kv in range(5, HKV):

import math
from contextlib import ExitStack

import concourse.mybir as mybir
from concourse.masks import make_identity

F32 = mybir.dt.float32
BF16 = mybir.dt.bfloat16
I32 = mybir.dt.int32
U8 = mybir.dt.uint8
FP8X4 = mybir.dt.float8_e4m3fn_x4
AF = mybir.ActivationFunctionType
ALU = mybir.AluOpType
AX = mybir.AxisListType

P = 128
HQ, HKV, S, D = 32, 8, 512, 128
G = HQ // HKV
NB = 32
NPB = S // NB
SOFTCAP = 30.0
SCALE = 1.0 / math.sqrt(D)
EPS = 1e-9
FILL = -1.0e4
FLOPS = 2 * 2 * HQ * 98688 * D

NGR = 4
NT = 8
LONG = 288
TILES = ((0, 1), (2, 3), (4, 6), (5, 7))
QORDER = (0, 1, 9, 10, 2, 3, 11, 12, 4, 6, 13, 15, 5, 7, 14, 8)
QPOS = {b: n for n, b in enumerate(QORDER)}
L_MASK, L_MAX, L_EXP, L_EVAC, L_QUANT, L_NORM = 0, 1, 2, 3, 4, 5
MASK_ENG = "gpsimd"
NFILL = 1
V_AT = (0, 1, 2, 3, 4, 5, 6, 7)
EVAC_V = {0: (0, 1, 2, 3,), 1: (2,), 2: (0, 2,), 3: (2,), 4: (2,), 5: (2,), 6: (2,), 7: (2,)}
NB_POOL = True
DEL0, DELN = 4, 6
LAST = (2, 3, 1, 0)
SCALES = tuple((b, b + 1, 0, b, b + 8) for b in range(8)) + (
    (8, 12, 0, 8, 15), (12, 14, 0, 8, 15), (14, 15, 0, 8, 15), (15, 16, 0, 14, 15), (8, 12, 8, 15, 16), (12, 16, 8, 15, 16), (15, 16, 7, 16, 17)
)


def tile_modelnew_t_kernel(tc, Q, K, V, out):
    nc = tc.nc
    with ExitStack() as ctx:
        ctx.enter_context(tc.manual_schedule())
        const = ctx.enter_context(tc.tile_pool(name="const", bufs=1))
        qtp = ctx.enter_context(tc.tile_pool(name="qtp", bufs=2))
        gp = ctx.enter_context(tc.tile_pool(name="gp", bufs=8))
        small = ctx.enter_context(tc.tile_pool(name="small", bufs=6))
        op = ctx.enter_context(tc.tile_pool(name="op", bufs=3))
        psq = ctx.enter_context(tc.psum_pool(name="psq", bufs=1))
        psr = ctx.enter_context(tc.psum_pool(name="psr", bufs=3))
        pst = ctx.enter_context(tc.psum_pool(name="pst", bufs=2))
        psa = ctx.enter_context(tc.psum_pool(name="psa", bufs=2))

        qn = [const.tile([P, NPB, D], BF16, name="qn%d" % kv) for kv in range(HKV)]
        kn = [const.tile([P, 4, D], BF16, name="kn%d" % kv) for kv in range(HKV)]
        vn = const.tile([P, HKV, 4, D], BF16, name="vn")

        def load_k(kv, eng=None):
            (eng or nc.sync).dma_start(out=kn[kv][:], in_=K[0, kv].rearrange("(n p) d -> p n d", n=4))

        def load_q(kv, b0, b1):
            for g in range(G):
                nc.sync.dma_start(
                    out=qn[kv][g:P:G, b0:b1, :],
                    in_=Q[0, G * kv + g].rearrange("(b i) d -> i b d", i=NB)[:, b0:b1, :],
                )

        def load_head(kv):
            load_k(kv)
            load_q(kv, 0, NPB)

        def load_v(k0, k1):
            nc.sync.dma_start(out=vn[:, k0:k1], in_=V[0, k0:k1].rearrange("h (p j) d -> p h j d", j=4))

        load_k(0, nc.scalar)
        load_q(0, 0, 4)
        load_q(0, 9, NPB)
        load_q(0, 4, 9)
        load_v(0, 2)
        load_k(1)
        load_q(1, 0, NPB)
        load_k(2)
        load_q(2, 0, NPB)
        load_v(2, HKV)
        load_head(3)

        vg = const.tile([P, HKV, D, 4], BF16, name="vg", align_bytes=64)
        vc = const.tile([P, HKV, P], I32, name="vc", align_bytes=64)
        vs = const.tile([P, HKV, P], U8, name="vs", align_bytes=64)
        vsh = const.tile([P, HKV, P], I32, name="vsh", align_bytes=64)
        vx = const.tile([P, HKV, P], I32, name="vx", align_bytes=64)
        var = [
            const.tile([P, 17, nh, P], U8, name="sv%d" % part, align_bytes=64)
            for part, nh in enumerate((2, HKV - 2))
        ]

        def s_zero(part, n0, n1):
            nc.vector.memset(var[part][:, n0:n1].rearrange("p n h d -> p (n h d)").bitcast(I32), 0)

        s_zero(0, 0, 17)

        ident = const.tile([P, P], BF16, name="ident")
        make_identity(nc, ident[:])
        perm = const.tile([P, P], BF16, name="perm")
        for u in range(2):
            nc.vector.tensor_copy(
                out=perm[:].rearrange("p (b u c e) -> p b u c e", b=4, u=2, e=2)[:, :, u],
                in_=ident[:].rearrange("p (b c u e) -> p b u c e", b=4, u=2, e=2)[:, :, u],
            )
        identf = const.tile([P, P], F32, name="identf")
        nc.gpsimd.tensor_copy(out=identf[:], in_=ident[:])

        th = {}
        for j, (a, b) in enumerate(TILES):
            w = 32 * (b + 1)
            th[(False, j)] = const.tile([P, 2, w + LONG], F32, name="th%d" % j)
            th[(True, j)] = const.tile([P, 2, w + LONG], F32, name="thl%d" % j) if j > 1 else th[(False, j)]
            for t in (th[(False, j)], th[(True, j)])[0 : 1 + j // 2]:
                nc.vector.memset(t[:, 0, 0 : 32 * (b - a)], FILL)

        s_zero(1, 0, 17)

        mnear = const.tile([P, 32], F32, name="mnear")
        mfar = const.tile([P, 32], F32, name="mfar")
        mk = const.tile([P, 64], F32, name="mk")
        nc.gpsimd.memset(mnear[:], 0.0)
        nc.gpsimd.memset(mfar[:], 0.0)
        nc.gpsimd.affine_select(
            out=mnear[:], in_=mnear[:], pattern=[[-4, 4], [-16, 8]], compare_op=ALU.is_ge,
            fill=FILL, base=0, channel_multiplier=1,
        )
        nc.gpsimd.affine_select(
            out=mfar[:], in_=mfar[:], pattern=[[4, 4], [16, 8]], compare_op=ALU.is_ge,
            fill=FILL, base=3, channel_multiplier=-1,
        )
        for n, m in enumerate((mnear, mfar)):
            nc.gpsimd.tensor_copy(
                out=mk[:, 32 * n : 32 * n + 32].rearrange("p (u c e) -> p u c e", u=2, e=2),
                in_=m[:].rearrange("p (u e c) -> p u c e", u=2, e=2),
            )

        nc.gpsimd.memset(vx[:].rearrange("p h d -> p (h d)"), 0)
        nc.gpsimd.memset(vsh[0:64].rearrange("p h d -> p (h d)"), 0)

        pt = [[const.tile([P, 2, P, 2], BF16, name="pt%d_%d" % (st, ti)) for ti in range(NT)] for st in range(2)]

        def words(t):
            return t[:].rearrange("p u w e -> p (u w e)").bitcast(F32)

        def p_zero(ti):
            b = ti + 10
            for st in range(2):
                if ti < 5:
                    nc.vector.memset(pt[st][ti][:, :, 8 * b : P, :].rearrange("p u w e -> p u (w e)").bitcast(I32), 0)


        def v_regroup(k0, k1):
            for k in range(k0, k1):
                nc.gpsimd.tensor_scalar(
                    out=vg[:, k], in0=vn[:, k].rearrange("p j d -> p d j"),
                    scalar1=1.0, scalar2=0.0, op0=ALU.mult, op1=ALU.add,
                )

        def v_quant(k0, k1):
            nc.vector.quantize_mx(
                out=vc[:, k0:k1].rearrange("p h d -> p (h d)").bitcast(FP8X4),
                scales=vs[:, k0:k1].rearrange("p h d -> p (h d)"),
                in_=vg[:, k0:k1].rearrange("p h d j -> p (h d j)"),
            )

        def v_variants(part):
            k0, k1 = ((0, 2), (2, HKV))[part]
            nc.sync.dma_start(out=vsh[64:P, k0:k1], in_=vc[0:64, k0:k1])
            nc.sync.dma_start(out=vx[120:P, k0:k1], in_=vc[64:72, k0:k1])
            for b0, b1, shift, n0, n1 in SCALES:
                p0 = 32 * (b0 // 4) + b0 % 4
                q0 = 32 * ((b0 - shift) // 4) + (b0 - shift) % 4
                o = var[part][p0 : p0 + b1 - b0, n0:n1].rearrange("p n h d -> p n (h d)").bitcast(I32)
                v = vs[q0 : q0 + b1 - b0, k0:k1].rearrange("p h d -> p (h d)").bitcast(I32)
                nc.sync.dma_start(out=o, in_=v.unsqueeze(1).to_broadcast(list(o.shape)))

        kts = {}
        qts = {}
        pps = {}

        def prep_pe(kv, part):
            if kv < 2 and part == 2:
                ps = psa.tile([P, 8, P], BF16, name="acc", tag="acc")
            elif kv == 0:
                for h in range(2):
                    if part == 1 and h == 0:
                        ps = psq.tile([P, 4, P], BF16, name="qps", tag="qps")
                    elif part == 1:
                        ps = psa.tile([P, 4, P], BF16, name="acc", tag="acc")
                    else:
                        ps = pst.tile([P, 4, P], BF16, name="tp", tag="tp")
                    for n in range(4):
                        nc.tensor.transpose(ps[:, n, :], qn[kv][:, QORDER[8 * part + 4 * h + n], :], ident[:])
                    pps[(kv, part, h)] = ps
                return
            else:
                ps = psq.tile([P, 8, P], BF16, name="qps", tag="qps")
            if part == 2:
                for t in range(4):
                    nc.tensor.transpose(ps[:, t, :], kn[kv][:, t, :], perm[:])
            else:
                for n in range(8):
                    nc.tensor.transpose(ps[:, n, :], qn[kv][:, QORDER[8 * part + n], :], ident[:])
            pps[(kv, part)] = ps

        def prep_copy(kv, part):
            if kv == 0 and part < 2:
                if part == 0:
                    qts[kv] = qtp.tile([P, NPB, P], BF16, name="qt", tag="qt")
                b = 8 * part
                nc.scalar.copy(out=qts[kv][:, b : b + 4, :], in_=pps[(kv, part, 0)][:])
                nc.vector.tensor_copy(out=qts[kv][:, b + 4 : b + 8, :], in_=pps[(kv, part, 1)][:])
                return
            ps = pps[(kv, part)]
            if part == 2:
                kts[kv] = qtp.tile([P, 4, P], BF16, name="kt", tag="kt")
                nc.vector.tensor_copy(out=kts[kv][:], in_=ps[:, 0:4, :])
            else:
                if kv not in qts:
                    qts[kv] = qtp.tile([P, NPB, P], BF16, name="qt", tag="qt")
                o = qts[kv][:, 8 * part : 8 * part + 8, :]
                nc.vector.tensor_copy(out=o, in_=ps[:])

        NG = HKV * NGR
        st = {}
        sums = {}
        oall = {}

        def group(g):
            kv, n = divmod(g, NGR)
            return kv, LAST[n] if kv == HKV - 1 else n

        def ok(g):
            return 0 <= g < NG

        def place(j, kind, s):
            return s if kind == 0 else (2 + s if j < 3 else 3 - s)

        def long_of(k):
            return k + 9 if k < 7 else 8

        def s_qk(g):
            kv, j = group(g)
            st[g] = {"raw": []}
            kt = kts[kv][:].rearrange("p n w -> p (n w)")
            a, b = TILES[j]
            cut = max(0, b + 1 + 9 - 16)
            banks = [
                [(a, 0, a + 1), (a + 9, a + 1, a + 10), (b, 0, cut)],
                [(b, cut, b + 1), (long_of(b), long_of(b) - 8, long_of(b) + 1)],
            ]
            c0 = 32 * (b - a)
            for n, jobs in enumerate(banks):
                raw = psr.tile([P, 512], F32, name="raw", tag="raw")
                if n < NFILL:
                    nc.tensor.matmul(
                        out=raw[:], lhsT=ident[:], rhs=qn[kv][:, 0:4, :].rearrange("p b d -> p (b d)"), start=True, stop=True
                    )
                w = 0
                for pb, k0, k1 in jobs:
                    if k1 > k0:
                        nc.tensor.matmul(
                            out=raw[:, w : w + 32 * (k1 - k0)],
                            lhsT=qts[kv][:, QPOS[pb], :],
                            rhs=kt[:, 32 * k0 : 32 * k1],
                            start=True,
                            stop=True,
                        )
                        w += 32 * (k1 - k0)
                st[g]["raw"].append((raw, w, c0))
                c0 += w

        def th_of(g):
            kv, j = group(g)
            return th[(kv == HKV - 1, j)], 32 * (TILES[j][1] + 1)

        def s_tanh(g):
            t, ws = th_of(g)
            flat = t[:].rearrange("p s c -> p (s c)")
            for raw, w, c0 in st[g]["raw"]:
                nc.scalar.activation(
                    out=flat[:, c0 : c0 + w], in_=raw[:, 0:w], func=AF.Tanh, scale=SCALE / SOFTCAP
                )

        def s_mask(g):
            t, ws = th_of(g)
            for c0, w in ((ws - 32, 64), (ws + LONG - 32, 32)):
                v = t[:, :, c0 : c0 + w]
                (nc.gpsimd if MASK_ENG == "gpsimd" else nc.vector).tensor_tensor(
                    out=v, in0=v, in1=mk[:, 0:w].unsqueeze(1).to_broadcast([P, 2, w]), op=ALU.add
                )

        def s_max_long(g):
            t, ws = th_of(g)
            mx = small.tile([P, 4], F32, name="mx", tag="mx")
            st[g]["mx"] = mx
            nc.vector.tensor_reduce(out=mx[:, 2:4], in_=t[:, :, ws : ws + LONG], axis=AX.X, op=ALU.max)

        def s_max_short(g):
            t, ws = th_of(g)
            nc.vector.tensor_reduce(out=st[g]["mx"][:, 0:2], in_=t[:, :, 0:ws], axis=AX.X, op=ALU.max)

        def s_nb(g):
            nb = small.tile([P, 4], F32, name="nb", tag="nb")
            if NB_POOL:
                nc.gpsimd.tensor_scalar(
                    out=nb[:], in0=st[g]["mx"][:], scalar1=-SOFTCAP, scalar2=0.0, op0=ALU.mult, op1=ALU.add
                )
            else:
                nc.vector.tensor_scalar(
                    out=nb[:], in0=st[g]["mx"][:], scalar1=-SOFTCAP, scalar2=None, op0=ALU.mult
                )
            st[g]["nb"] = nb

        def s_exp(g):
            kv, j = group(g)
            if kv not in sums:
                sums[kv] = {
                    "ls": small.tile([P, 17], F32, name="ls", tag="ls"),
                    "le": small.tile([P, 16], F32, name="le", tag="le"),
                    "rl": small.tile([P, 16], F32, name="rl", tag="rl"),
                }
            ls = sums[kv]["ls"]
            nb = st[g]["nb"]
            t, ws = th_of(g)

            def piece(s, u, c0, nblk, ti, blk0, col):
                nc.scalar.activation(
                    out=pt[kv % 2][ti][:, :, 8 * blk0 : 8 * (blk0 + nblk), :].rearrange("p u (b c) e -> p u b (c e)", c=8),
                    in_=t[:, s, c0 : c0 + 32 * nblk].rearrange("p (b u x) -> p u b x", u=2, x=16),
                    func=AF.Exp,
                    bias=nb[:, u : u + 1],
                    scale=SOFTCAP,
                    accum_out=ls[:, col : col + 1],
                )

            for s, k in enumerate(TILES[j]):
                piece(s, s, ws - 32 * (k + 1), k + 1, k, 0, 4 * (g % NGR) + place(j, 0, s))
            for s, k in enumerate(TILES[j]):
                col = 4 * (g % NGR) + place(j, 1, s)
                if k < 7:
                    piece(s, 2 + s, ws, 9, k, k + 1, col)
                else:
                    piece(s, 2 + s, ws, 8, 7, 8, col)
                    piece(s, 2 + s, ws + 256, 1, 5, 15, 16)

        def ready(g):
            kv, n = divmod(g, NGR)
            if n == 3:
                return (8, 16) if kv == HKV - 1 else (0, 16)
            return (0, 8) if n == 1 and kv == HKV - 1 else None

        def s_rl_add(g):
            if ready(g) is None:
                return
            c0, c1 = ready(g)
            h = sums[g // NGR]
            nc.gpsimd.tensor_scalar(
                out=h["le"][:, c0:c1], in0=h["ls"][:, c0:c1], scalar1=EPS, scalar2=1.0, op0=ALU.add, op1=ALU.mult
            )
            for n in range(c0 // 4, c1 // 4):
                if group(g - g % NGR + n)[1] == 3:
                    c = 4 * n + place(3, 1, 1)
                    nc.gpsimd.tensor_scalar(
                        out=h["le"][:, c : c + 1],
                        in0=h["ls"][:, c : c + 1],
                        scalar1=h["ls"][:, 16:17],
                        scalar2=EPS,
                        op0=ALU.add,
                        op1=ALU.add,
                    )

        def s_rl(g):
            if ready(g) is None:
                return
            c0, c1 = ready(g)
            h = sums[g // NGR]
            nc.vector.reciprocal(out=h["rl"][:, c0:c1], in_=h["le"][:, c0:c1])

        def s_tr(g):
            kv, j = group(g)
            tp = pst.tile([P, 2, 2, P], F32, name="tp", tag="tp")
            st[g]["tp"] = tp
            for n, ti in enumerate(TILES[j]):
                for u in range(2):
                    nc.tensor.transpose(tp[:, n, u, :], words(pt[kv % 2][ti])[:, P * u : P * u + P], identf[:])

        def s_evac(g):
            kv, j = group(g)
            gt = gp.tile([P, 2, P, 4], BF16, name="gt", tag="gt", align_bytes=64)
            (nc.vector.tensor_copy if j in EVAC_V[kv] else nc.scalar.copy)(
                out=gt[:].rearrange("p n r t -> p (n r t)").bitcast(F32).rearrange("p (n r u) -> p n r u", n=2, u=2),
                in_=st[g]["tp"][:].rearrange("p n u r -> p n r u"),
            )
            st[g]["gt"] = gt

        def s_quant(g):
            cd = gp.tile([P, 2, P], I32, name="cd", tag="cd", align_bytes=64)
            sc = gp.tile([P, 2, P], U8, name="sc", tag="sc", align_bytes=64)
            nc.vector.quantize_mx(
                out=cd[:].rearrange("p n r -> p (n r)").bitcast(FP8X4),
                scales=sc[:].rearrange("p n r -> p (n r)"),
                in_=st[g]["gt"][:].rearrange("p n r t -> p (n r t)"),
            )
            st[g]["q"] = (cd, sc)

        def s_mx(g):
            kv, j = group(g)
            if g == NG - 1:
                acc = psr.tile([P, 4, D], F32, name="raw", tag="raw")
            else:
                acc = psa.tile([P, 4, D], F32, name="acc", tag="acc")
            st[g]["acc"] = acc
            cd, sc = st[g]["q"]
            sv = var[min(1, kv // 2)]

            def mx(u, passes):
                for i, (n, rhs, rs) in enumerate(passes):
                    nc.tensor.matmul_mx(
                        out=acc[:, u, :],
                        lhsT=cd[:, n, :].bitcast(FP8X4),
                        lhsT_scale=sc[:, n, :],
                        rhs=rhs[:, kv, :].bitcast(FP8X4),
                        rhs_scale=sv[:, rs, kv if kv < 2 else kv - 2, :],
                        start=(i == 0),
                        stop=(i == len(passes) - 1),
                    )

            for s, k in enumerate(TILES[j]):
                mx(place(j, 0, s), [(s, vc, k)])
                mx(place(j, 1, s), [(s, vc, 8 + k)] if k < 7 else [(1, vsh, 15), (0, vx, 16)])

        def store(kv, b0, b1, o):
            for q in range(G):
                nc.sync.dma_start(
                    out=out[0, G * kv + q].rearrange("(b i) d -> i b d", i=NB)[:, b0:b1, :], in_=o[q:P:G, b0:b1]
                )

        def s_norm(g):
            kv, j = group(g)
            rl = sums[kv]["rl"][:, 4 * (g % NGR) : 4 * (g % NGR) + 4]
            acc = st[g]["acc"]
            ko = (kv, False)
            if ko not in oall:
                oall[ko] = op.tile([P, 2, 9, D], F32, name="oall", tag="oall")
                if kv == HKV - 1:
                    oall[(kv, True)] = op.tile([P, 2, 9, D], F32, name="oall", tag="oall")
            o = oall[ko]
            flat = o[:].rearrange("p x y d -> p (x y) d")
            a, b = TILES[j]
            if kv == HKV - 1 and j > 1:
                mid = oall[(kv, True)][:].rearrange("p x y d -> p (x y) d")
                for u, n, t, b0, step in ((0, 2, mid, a, 2),) + (((2, 2, flat, a + 9, 2),) if j == 2 else ((2, 1, mid, 8, 1), (3, 1, flat, 14, 1))):
                    nc.vector.tensor_tensor(
                        out=t[:, b0 : b0 + step * (n - 1) + 1 : step, :],
                        in0=acc[:, u : u + n, :],
                        in1=rl[:, u : u + n].unsqueeze(2).to_broadcast([P, n, D]),
                        op=ALU.mult,
                    )
                if j == 3:
                    store(kv, 4, 9, mid)
            elif g == NG - 2:
                for u, n in enumerate((a, b, a + 9, b + 9)):
                    nc.scalar.activation(out=flat[:, n], in_=acc[:, u, :], func=AF.Copy, scale=rl[:, u : u + 1])
            elif j < 3:
                nc.vector.tensor_tensor(
                    out=o[:, :, a : b + 1 : b - a, :],
                    in0=acc[:].rearrange("p (x y) d -> p x y d", x=2),
                    in1=rl.rearrange("p (x y) -> p x y", x=2).unsqueeze(3).to_broadcast([P, 2, 2, D]),
                    op=ALU.mult,
                )
            else:
                for u, b0, step in ((0, a, b - a), (2, 8, 6)):
                    nc.vector.tensor_tensor(
                        out=flat[:, b0 : b0 + step + 1 : step, :],
                        in0=acc[:, u : u + 2, :],
                        in1=rl[:, u : u + 2].unsqueeze(2).to_broadcast([P, 2, D]),
                        op=ALU.mult,
                    )
            if kv < HKV - 1:
                if j == 3:
                    store(kv, 0, NPB, flat)
            elif g % NGR == 3:
                store(kv, 9, NPB, flat)
                store(kv, 0, 4, flat)

        prep = {0: [(0, 1)], 1: [(1, 0)], 2: [(1, 1), (1, 2)]}
        for kv in range(2, HKV):
            for part in range(3):
                prep[NGR * (kv - 1) + part] = [(kv, (1 - part if kv == HKV - 1 and part < 2 else part))]

        extra = {}

        def at(i, f):
            extra.setdefault(i, []).append(f)

        for k in range(HKV):
            at(V_AT[k], lambda k=k: v_regroup(k, k + 1))
            if k % 2:
                at(V_AT[k] + 1, lambda k=k: v_quant(k - 1, k + 1))
        at(V_AT[1] + 1, lambda: v_variants(0))
        for kv in (4,):
            at(V_AT[1] + 1, lambda kv=kv: load_head(kv))
        at(V_AT[7] + 1, lambda: v_variants(1))
        for kv in range(5, HKV):
            at(V_AT[7] + 2 + 3 * (kv - 5), lambda kv=kv: load_head(kv))
        prep_pe(0, 2)
        prep_pe(0, 0)
        prep_copy(0, 2)
        prep_copy(0, 0)
        for ti in range(NT):
            p_zero(ti)
        s_qk(0)
        def exps(g):
            if ok(g):
                s_exp(g)
                s_rl_add(g)
                s_tr(g)

        mx_at = {}
        for g in range(NG):
            lag = 1 if g % NGR == 0 and g < NG - NGR else 0
            mx_at.setdefault(g + L_QUANT + max(lag, DEL0 - g // DELN), []).append(g)

        for i in range(NG):
            s_tanh(i)
            if ok(i - L_MASK):
                s_mask(i - L_MASK)
            for a in prep.get(i - 1, []):
                prep_copy(*a)
            if ok(i + 1):
                s_qk(i + 1)
            if ok(i - L_MAX):
                s_max_long(i - L_MAX)
                s_max_short(i - L_MAX)
                s_nb(i - L_MAX)
            if ok(i - L_EVAC):
                s_evac(i - L_EVAC)
            for g in mx_at.get(i, []):
                s_quant(g)
            if ok(i - L_EXP - 1):
                s_rl(i - L_EXP - 1)
            for a in prep.get(i, []):
                prep_pe(*a)
            exps(i - L_EXP)
            for g in mx_at.get(i, []):
                s_mx(g)
            for g in mx_at.get(i - 1, []):
                s_norm(g)
            for f in extra.get(i, []):
                f()
        z = NG - 1
        s_max_long(z)
        s_max_short(z)
        s_nb(z)
        exps(z - 1)
        s_evac(z - 2)
        s_rl(z - 2)
        s_quant(z - 3)
        s_mx(z - 3)
        s_norm(z - 4)
        s_quant(z - 2)
        s_mx(z - 2)
        s_norm(z - 3)
        exps(z)
        s_evac(z - 1)
        s_norm(z - 2)
        s_evac(z)
        s_quant(z - 1)
        s_mx(z - 1)
        s_rl(z)
        s_quant(z)
        s_mx(z)
        s_norm(z - 1)
        s_norm(z)
